import numpy as np
import ml_dtypes


def mxq(x, axis, fmt="e4m3"):
    dtype, down = {"e4m3": (ml_dtypes.float8_e4m3fn, 7), "e5m2": (ml_dtypes.float8_e5m2, 14)}[fmt]
    v = np.moveaxis(np.asarray(x, np.float32).astype(ml_dtypes.bfloat16).astype(np.float64), axis, -1)
    blocks = v.reshape(v.shape[:-1] + (-1, 32))
    amax = np.abs(blocks).max(-1, keepdims=True)
    byte = np.maximum(np.where(amax > 0, np.frexp(amax)[1] - 1 + 127, 0) - down, 1)
    scale = np.exp2(byte - 127.0)
    codes = (blocks / scale).astype(np.float32).astype(dtype).astype(np.float64)
    return np.moveaxis((codes * scale).reshape(v.shape), -1, axis)


WIDE = False


def mx_kscale(k):
    if not WIDE:
        return np.ones(k)
    levels = np.array([20, -20, 10, -10, 0])
    a = np.random.permutation(np.resize(levels, k // 512 * 4)).reshape(k // 512, 4)
    idx = np.arange(k)
    return np.exp2(a[idx // 512, idx % 128 // 32])


BF16 = ml_dtypes.bfloat16


def bf(x):
    return np.asarray(x, np.float32).astype(BF16)


def f64(x):
    return np.asarray(x).astype(np.float64)


B, N, C, F = 2, 32, 1024, 1024
EPS_STD = 1e-5


def messages(x, e_enc, W_pre, b_pre):
    w = f64(W_pre)
    tgt = f64(x) @ w[:C]
    src = f64(x) @ w[C:2 * C]
    edg = f64(e_enc) @ w[2 * C:]
    return tgt[:, :, None, :] + src[:, None, :, :] + edg + f64(b_pre)


def setup_inputs():
    u = mx_kscale(F)
    x = bf(np.random.standard_normal((B, N, C)))
    e_enc = bf(np.random.standard_normal((B, N, N, C)))
    w0 = bf(np.random.standard_normal((3 * C, F)) / np.sqrt(3 * C))
    b_pre = bf(np.random.standard_normal(F) * 0.3)
    g = bf(np.random.standard_normal((B, N, 4 * F)) * np.exp2(np.random.randint(-12, 1, (B, N, 1))) * 64.0 * np.tile(u, 4))
    m = messages(x, e_enc, w0, b_pre)
    return {"x": x, "e_enc": e_enc, "W_pre": bf(f64(w0) / u[None, :]), "b_pre": b_pre,
            "m": np.asarray(m, np.float32), "grad_out": g}


def reference(x, e_enc, W_pre, b_pre, m, grad_out):
    mf = f64(m)
    g = f64(grad_out)
    g_mean = g[:, :, None, 0:F]
    g_mn = g[:, :, None, F:2 * F]
    g_mx = g[:, :, None, 2 * F:3 * F]
    g_std = g[:, :, None, 3 * F:4 * F]
    mean = mf.mean(axis=2, keepdims=True)
    mn = mf.min(axis=2, keepdims=True)
    mx = mf.max(axis=2, keepdims=True)
    var = (mf * mf).mean(axis=2, keepdims=True) - mean * mean
    std = np.sqrt(np.maximum(var, 0.0) + EPS_STD)
    at_mn = (mf == mn) * 1.0
    at_mx = (mf == mx) * 1.0
    dm = (g_mean / N
          + g_mn * at_mn / at_mn.sum(axis=2, keepdims=True)
          + g_mx * at_mx / at_mx.sum(axis=2, keepdims=True)
          + g_std * (var > 0.0) * (mf - mean) / (N * std))
    de = mxq(dm.reshape(B * N * N, F), 1, "e5m2") @ mxq(f64(W_pre)[2 * C:], 1, "e4m3").T
    return de.reshape(B, N, N, C)

@@ -1,0 +1,276 @@
+from contextlib import ExitStack
+
+import concourse.mybir as mybir
+from concourse.masks import make_identity
+
+F32 = mybir.dt.float32
+BF16 = mybir.dt.bfloat16
+U32 = mybir.dt.uint32
+U8 = mybir.dt.uint8
+E4M3_X4 = mybir.dt.float8_e4m3fn_x4
+E5M2_X4 = mybir.dt.float8_e5m2_x4
+ALU = mybir.AluOpType
+FUNC = mybir.ActivationFunctionType
+INNERMOST = mybir.AxisListType.X
+
+GRAPHS = 2
+NODES = 32
+FEATURES = 1024
+CHANNELS = 1024
+EPS_STD = 1e-5
+
+P = 128
+PACK = 4
+K_PASS = P * PACK
+PASSES = FEATURES // K_PASS
+PLANES = FEATURES // P
+N_TILE = 512
+ROWS = GRAPHS * NODES * NODES
+TARGETS = GRAPHS * NODES
+TILE_TARGETS = P // NODES
+BATCH_TILES = 2
+BATCH_ROWS = BATCH_TILES * P
+BATCH_TARGETS = BATCH_TILES * TILE_TARGETS
+BATCHES = ROWS // BATCH_ROWS
+CELLS = PLANES * BATCH_TARGETS
+
+KIND_MEAN, KIND_MIN, KIND_MAX, KIND_STD = 0, 1, 2, 3
+KINDS = 4
+LOW, HIGH = 0, 1
+
+FLOPS = 2 * ROWS * FEATURES * CHANNELS
+BYTES = 4 * ROWS * FEATURES + 2 * TARGETS * KINDS * FEATURES + 2 * CHANNELS * FEATURES + 4 * ROWS * CHANNELS
+
+
+def over_sources(cell_values):
+    return cell_values.unsqueeze(2).to_broadcast([P, CELLS, NODES])
+
+
+def tile_gnnlayer_pa_v_kernel(tc, x, e_enc, W_pre, b_pre, m, grad_out, out):
+    nc = tc.nc
+    m_rows = m.rearrange("b i j f -> (b i j) f")
+    out_rows = out.rearrange("b i j c -> (b i j) c")
+    grad_rows = grad_out.rearrange("b i k -> (b i) k")
+    w_edge = W_pre[2 * FEATURES : 3 * FEATURES, :]
+
+    with ExitStack() as stack:
+        keep = stack.enter_context(tc.tile_pool(name="keep", bufs=1))
+        stream = stack.enter_context(tc.tile_pool(name="stream", bufs=4))
+        planes = stack.enter_context(tc.tile_pool(name="planes", bufs=3))
+        work = stack.enter_context(tc.tile_pool(name="work", bufs=2))
+        scratch = stack.enter_context(tc.tile_pool(name="scratch", bufs=1))
+        psum_turn = stack.enter_context(tc.psum_pool(name="psum_turn", bufs=2))
+        psum_prep = stack.enter_context(tc.psum_pool(name="psum_prep", bufs=2))
+        psum_sums = stack.enter_context(tc.psum_pool(name="psum_sums", bufs=2))
+        psum_out = stack.enter_context(tc.psum_pool(name="psum_out", bufs=2))
+
+        ident_f32 = keep.tile([P, P], F32)
+        make_identity(nc, ident_f32[:])
+        ident_bf16 = keep.tile([P, P], BF16)
+        make_identity(nc, ident_bf16[:])
+        target_of_row = keep.tile([P, TILE_TARGETS], F32)
+        nc.vector.tensor_reduce(
+            out=target_of_row[:],
+            in_=ident_f32[:].rearrange("p (q j) -> p q j", j=NODES),
+            axis=INNERMOST,
+            op=ALU.add,
+        )
+
+        grad_t = keep.tile([P, KINDS, PLANES, TARGETS], F32)
+        w_codes = keep.tile([P, PASSES, CHANNELS], U32, align_bytes=64)
+        w_scales = keep.tile([P, PASSES, CHANNELS], U8, align_bytes=64)
+
+        def prepare_grad():
+            half = KINDS * FEATURES // 2
+            grad_nat = keep.tile([P, half], BF16)
+            for side in range(2):
+                nc.sync.dma_start(
+                    out=grad_nat[side * TARGETS : (side + 1) * TARGETS, :],
+                    in_=grad_rows[:, side * half : (side + 1) * half],
+                )
+            for first in range(2):
+                turned = psum_prep.tile([P, PLANES, P], BF16, name="turned")
+                for plane in range(PLANES):
+                    col0 = (first * PLANES + plane) * P
+                    nc.tensor.transpose(turned[:, plane, :], grad_nat[:, col0 : col0 + P], ident_bf16[:])
+                for side in range(2):
+                    kind = 2 * side + first
+                    nc.scalar.activation(
+                        out=grad_t[:, kind],
+                        in_=turned[:, :, side * TARGETS : (side + 1) * TARGETS],
+                        func=FUNC.Copy,
+                        scale=1.0 / NODES if kind in (KIND_MEAN, KIND_STD) else 1.0,
+                    )
+
+        def prepare_weight():
+            w_nat = keep.tile([P, CHANNELS // P, FEATURES], BF16)
+            nc.sync.dma_start(out=w_nat[:], in_=w_edge.rearrange("(a p) f -> p a f", p=P))
+            w_grouped = keep.tile([P, PASSES, CHANNELS, PACK], BF16, align_bytes=64)
+            for h in range(PASSES):
+                for a in range(CHANNELS // P):
+                    turned = psum_prep.tile([P, PACK, P], BF16, name="turned")
+                    for t in range(PACK):
+                        col0 = (h * PACK + t) * P
+                        nc.tensor.transpose(turned[:, t, :], w_nat[:, a, col0 : col0 + P], ident_bf16[:])
+                    nc.scalar.copy(
+                        out=w_grouped[:, h, a * P : (a + 1) * P, :],
+                        in_=turned[:].rearrange("p t c -> p c t"),
+                    )
+            for h in range(PASSES):
+                nc.vector.quantize_mx(
+                    out=w_codes[:, h, :].bitcast(E4M3_X4),
+                    scales=w_scales[:, h, :],
+                    in_=w_grouped[:, h].rearrange("p c t -> p (c t)"),
+                )
+
+        def load_and_turn(batch):
+            m_t = planes.tile([P, PLANES, BATCH_ROWS], F32, name="m_t")
+            sums = psum_sums.tile([P, 2, PLANES, BATCH_TARGETS], F32, name="sums")
+            for a in range(BATCH_TILES):
+                row0 = (batch * BATCH_TILES + a) * P
+                m_nat = stream.tile([P, FEATURES], F32, name="m_nat")
+                nc.sync.dma_start(out=m_nat[:], in_=m_rows[row0 : row0 + P, :])
+                m_sq = stream.tile([P, FEATURES], F32, name="m_sq")
+                nc.scalar.activation(out=m_sq[:], in_=m_nat[:], func=FUNC.Square)
+                for h in range(PASSES):
+                    turned = psum_turn.tile([P, PACK, P], F32, name="turned_m")
+                    for t in range(PACK):
+                        col0 = (h * PACK + t) * P
+                        nc.tensor.transpose(turned[:, t, :], m_nat[:, col0 : col0 + P], ident_f32[:])
+                    nc.scalar.copy(out=m_t[:, h * PACK : (h + 1) * PACK, a * P : (a + 1) * P], in_=turned[:])
+                targets = slice(a * TILE_TARGETS, (a + 1) * TILE_TARGETS)
+                for power, operand in enumerate((m_nat, m_sq)):
+                    for plane in range(PLANES):
+                        nc.tensor.matmul(
+                            out=sums[:, power, plane, targets],
+                            lhsT=operand[:, plane * P : (plane + 1) * P],
+                            rhs=target_of_row[:],
+                            start=True,
+                            stop=True,
+                        )
+            return m_t, sums
+
+        def statistics(batch, m_t, sums):
+            targets = slice(batch * BATCH_TARGETS, (batch + 1) * BATCH_TARGETS)
+            m_cells = m_t[:].rearrange("p c (g j) -> p (c g) j", j=NODES)
+
+            extreme = work.tile([P, 2, CELLS], F32, name="extreme")
+            nc.vector.tensor_reduce(out=extreme[:, LOW, :], in_=m_cells, axis=INNERMOST, op=ALU.min)
+            nc.vector.tensor_reduce(out=extreme[:, HIGH, :], in_=m_cells, axis=INNERMOST, op=ALU.max)
+            at_extreme = work.tile([P, 2, CELLS, NODES], BF16, name="at_extreme")
+            for side in (LOW, HIGH):
+                nc.vector.tensor_tensor(
+                    out=at_extreme[:, side], in0=m_cells, in1=over_sources(extreme[:, side, :]), op=ALU.is_equal
+                )
+
+            level = at_extreme[:].rearrange("p s x j -> p (s x) j")
+            for halving in range(1, 6):
+                width = NODES >> halving
+                shorter = scratch.tile([P, 2 * CELLS, width], F32 if width == 1 else BF16, name="count%d" % width)
+                nc.vector.tensor_tensor(
+                    out=shorter[:], in0=level[:, :, 0:width], in1=level[:, :, width : 2 * width], op=ALU.add
+                )
+                level = shorter[:]
+            share = work.tile([P, 2, PLANES, BATCH_TARGETS], F32, name="share")
+            nc.vector.reciprocal(
+                out=share[:].rearrange("p s c g -> p (s c g)"), in_=level.rearrange("p x o -> p (x o)")
+            )
+            amplitude = work.tile([P, 2, PLANES, BATCH_TARGETS], F32, name="amplitude")
+            nc.gpsimd.tensor_tensor(
+                out=amplitude[:], in0=grad_t[:, KIND_MIN : KIND_MAX + 1, :, targets], in1=share[:], op=ALU.mult
+            )
+
+            cell_shape = [P, PLANES, BATCH_TARGETS]
+            moments = work.tile([P, 2, PLANES, BATCH_TARGETS], F32, name="moments")
+            nc.scalar.mul(out=moments[:], in_=sums[:], mul=1.0 / NODES)
+            mean = moments[:, 0]
+            var = work.tile(cell_shape, F32, name="var")
+            nc.gpsimd.tensor_tensor(out=var[:], in0=mean, in1=mean, op=ALU.mult)
+            nc.gpsimd.tensor_tensor(out=var[:], in0=moments[:, 1], in1=var[:], op=ALU.subtract)
+            std = work.tile(cell_shape, F32, name="std")
+            nc.gpsimd.tensor_scalar(
+                out=std[:], in0=var[:], scalar1=0.0, scalar2=EPS_STD, op0=ALU.max, op1=ALU.add
+            )
+            nc.scalar.activation(out=std[:], in_=std[:], func=FUNC.Sqrt)
+            slope = work.tile(cell_shape, F32, name="slope")
+            nc.gpsimd.tensor_scalar(
+                out=slope[:], in0=var[:], scalar1=0.0, scalar2=1.0, op0=ALU.is_gt, op1=ALU.mult
+            )
+            nc.gpsimd.tensor_tensor(out=slope[:], in0=slope[:], in1=grad_t[:, KIND_STD, :, targets], op=ALU.mult)
+            nc.vector.reciprocal(out=std[:], in_=std[:])
+            nc.gpsimd.tensor_tensor(out=slope[:], in0=slope[:], in1=std[:], op=ALU.mult)
+            offset = work.tile(cell_shape, F32, name="offset")
+            nc.gpsimd.tensor_tensor(out=offset[:], in0=slope[:], in1=mean, op=ALU.mult)
+            nc.gpsimd.tensor_tensor(out=offset[:], in0=grad_t[:, KIND_MEAN, :, targets], in1=offset[:], op=ALU.subtract)
+            return at_extreme, amplitude, slope, offset
+
+        def finish(batch, m_t, at_extreme, amplitude, slope, offset):
+            linear = work.tile([P, PLANES, BATCH_ROWS], F32, name="linear")
+            for plane in range(PLANES):
+                for g in range(BATCH_TARGETS):
+                    sources = slice(g * NODES, (g + 1) * NODES)
+                    nc.scalar.activation(
+                        out=linear[:, plane, sources],
+                        in_=m_t[:, plane, sources],
+                        func=FUNC.Identity,
+                        scale=slope[:, plane, g : g + 1],
+                        bias=offset[:, plane, g : g + 1],
+                    )
+            spikes = []
+            for side in (LOW, HIGH):
+                spike = scratch.tile([P, PLANES, BATCH_ROWS], F32, name="spike%d" % side)
+                nc.vector.tensor_tensor(
+                    out=spike[:].rearrange("p c (g j) -> p (c g) j", j=NODES),
+                    in0=at_extreme[:, side],
+                    in1=over_sources(amplitude[:, side].rearrange("p c g -> p (c g)")),
+                    op=ALU.mult,
+                )
+                spikes.append(spike)
+            nc.vector.tensor_tensor(out=spikes[LOW][:], in0=spikes[LOW][:], in1=linear[:], op=ALU.add)
+            dm_grouped = work.tile([P, PASSES, BATCH_ROWS, PACK], BF16, name="dm_grouped", align_bytes=64)
+            dm_codes = work.tile([P, PASSES, BATCH_ROWS], U32, name="dm_codes", align_bytes=64)
+            dm_scales = work.tile([P, PASSES, BATCH_ROWS], U8, name="dm_scales", align_bytes=64)
+            for h in range(PASSES):
+                pass_planes = slice(h * PACK, (h + 1) * PACK)
+                nc.vector.tensor_tensor(
+                    out=dm_grouped[:, h],
+                    in0=spikes[LOW][:, pass_planes, :].rearrange("p t r -> p r t"),
+                    in1=spikes[HIGH][:, pass_planes, :].rearrange("p t r -> p r t"),
+                    op=ALU.add,
+                )
+            for h in range(PASSES):
+                nc.vector.quantize_mx(
+                    out=dm_codes[:, h, :].bitcast(E5M2_X4),
+                    scales=dm_scales[:, h, :],
+                    in_=dm_grouped[:, h].rearrange("p r t -> p (r t)"),
+                )
+            for a in range(BATCH_TILES):
+                rows = slice(a * P, (a + 1) * P)
+                row0 = (batch * BATCH_TILES + a) * P
+                result = stream.tile([P, CHANNELS], F32, name="result")
+                for n in range(CHANNELS // N_TILE):
+                    cols = slice(n * N_TILE, (n + 1) * N_TILE)
+                    acc = psum_out.tile([P, N_TILE], F32, name="acc")
+                    for h in range(PASSES):
+                        nc.tensor.matmul_mx(
+                            out=acc[:],
+                            lhsT=dm_codes[:, h, rows].bitcast(E5M2_X4),
+                            lhsT_scale=dm_scales[:, h, rows],
+                            rhs=w_codes[:, h, cols].bitcast(E4M3_X4),
+                            rhs_scale=w_scales[:, h, cols],
+                            start=(h == 0),
+                            stop=(h == PASSES - 1),
+                        )
+                    nc.scalar.copy(out=result[:, cols], in_=acc[:])
+                nc.scalar.dma_start(out=out_rows[row0 : row0 + P, :], in_=result[:])
+
+        prepare_grad()
+        m_t, sums = load_and_turn(0)
+        prepare_weight()
+        ready = (m_t,) + statistics(0, m_t, sums)
+        for batch in range(BATCHES):
+            current = ready
+            if batch + 1 < BATCHES:
+                m_t, sums = load_and_turn(batch + 1)
+                ready = (m_t,) + statistics(batch + 1, m_t, sums)
+            finish(batch, *current)

@@ -52,10 +52,11 @@ def tile_gnnlayer_pa_v_kernel(tc, x, e_enc, W_pre, b_pre, m, grad_out, out):
     out_rows = out.rearrange("b i j c -> (b i j) c")
     grad_rows = grad_out.rearrange("b i k -> (b i) k")
     w_edge = W_pre[2 * FEATURES : 3 * FEATURES, :]
+    cell_shape = [P, PLANES, BATCH_TARGETS]
 
     with ExitStack() as stack:
         keep = stack.enter_context(tc.tile_pool(name="keep", bufs=1))
-        stream = stack.enter_context(tc.tile_pool(name="stream", bufs=4))
+        stream = stack.enter_context(tc.tile_pool(name="stream", bufs=3))
         planes = stack.enter_context(tc.tile_pool(name="planes", bufs=3))
         work = stack.enter_context(tc.tile_pool(name="work", bufs=2))
         scratch = stack.enter_context(tc.tile_pool(name="scratch", bufs=1))
@@ -63,6 +64,7 @@ def tile_gnnlayer_pa_v_kernel(tc, x, e_enc, W_pre, b_pre, m, grad_out, out):
         psum_prep = stack.enter_context(tc.psum_pool(name="psum_prep", bufs=2))
         psum_sums = stack.enter_context(tc.psum_pool(name="psum_sums", bufs=2))
         psum_out = stack.enter_context(tc.psum_pool(name="psum_out", bufs=2))
+        stack.enter_context(tc.manual_schedule())
 
         ident_f32 = keep.tile([P, P], F32)
         make_identity(nc, ident_f32[:])
@@ -77,8 +79,14 @@ def tile_gnnlayer_pa_v_kernel(tc, x, e_enc, W_pre, b_pre, m, grad_out, out):
         )
 
         grad_t = keep.tile([P, KINDS, PLANES, TARGETS], F32)
+        w_nat = keep.tile([P, CHANNELS // P, FEATURES], BF16)
+        w_grouped = keep.tile([P, PASSES, CHANNELS, PACK], BF16, align_bytes=64)
         w_codes = keep.tile([P, PASSES, CHANNELS], U32, align_bytes=64)
         w_scales = keep.tile([P, PASSES, CHANNELS], U8, align_bytes=64)
+        live = {}
+
+        def targets_of(batch):
+            return slice(batch * BATCH_TARGETS, (batch + 1) * BATCH_TARGETS)
 
         def prepare_grad():
             half = KINDS * FEATURES // 2
@@ -102,10 +110,8 @@ def tile_gnnlayer_pa_v_kernel(tc, x, e_enc, W_pre, b_pre, m, grad_out, out):
                         scale=1.0 / NODES if kind in (KIND_MEAN, KIND_STD) else 1.0,
                     )
 
-        def prepare_weight():
-            w_nat = keep.tile([P, CHANNELS // P, FEATURES], BF16)
+        def turn_weight():
             nc.sync.dma_start(out=w_nat[:], in_=w_edge.rearrange("(a p) f -> p a f", p=P))
-            w_grouped = keep.tile([P, PASSES, CHANNELS, PACK], BF16, align_bytes=64)
             for h in range(PASSES):
                 for a in range(CHANNELS // P):
                     turned = psum_prep.tile([P, PACK, P], BF16, name="turned")
@@ -116,6 +122,8 @@ def tile_gnnlayer_pa_v_kernel(tc, x, e_enc, W_pre, b_pre, m, grad_out, out):
                         out=w_grouped[:, h, a * P : (a + 1) * P, :],
                         in_=turned[:].rearrange("p t c -> p c t"),
                     )
+
+        def quantise_weight():
             for h in range(PASSES):
                 nc.vector.quantize_mx(
                     out=w_codes[:, h, :].bitcast(E4M3_X4),
@@ -148,12 +156,53 @@ def tile_gnnlayer_pa_v_kernel(tc, x, e_enc, W_pre, b_pre, m, grad_out, out):
                             start=True,
                             stop=True,
                         )
-            return m_t, sums
+            moments = planes.tile([P, 2, PLANES, BATCH_TARGETS], F32, name="moments")
+            nc.scalar.mul(out=moments[:], in_=sums[:], mul=1.0 / NODES)
+            mean_sq = work.tile(cell_shape, F32, name="mean_sq")
+            nc.scalar.activation(out=mean_sq[:], in_=moments[:, 0], func=FUNC.Square)
+            live[batch] = {"m_t": m_t, "moments": moments, "mean_sq": mean_sq}
 
-        def statistics(batch, m_t, sums):
-            targets = slice(batch * BATCH_TARGETS, (batch + 1) * BATCH_TARGETS)
-            m_cells = m_t[:].rearrange("p c (g j) -> p (c g) j", j=NODES)
+        def deviation(batch):
+            tiles = live[batch]
+            var = work.tile(cell_shape, F32, name="var")
+            nc.vector.tensor_tensor(out=var[:], in0=tiles["moments"][:, 1], in1=tiles["mean_sq"][:], op=ALU.subtract)
+            std = work.tile(cell_shape, F32, name="std")
+            nc.vector.tensor_scalar(
+                out=std[:], in0=var[:], scalar1=0.0, scalar2=EPS_STD, op0=ALU.max, op1=ALU.add
+            )
+            nc.scalar.activation(out=std[:], in_=std[:], func=FUNC.Sqrt)
+            tiles["var"] = var
+            tiles["std"] = std
 
+        def linear_part(batch):
+            tiles = live[batch]
+            targets = targets_of(batch)
+            slope = work.tile(cell_shape, F32, name="slope")
+            offset = work.tile(cell_shape, F32, name="offset")
+            nc.vector.reciprocal(out=tiles["std"][:], in_=tiles["std"][:])
+            nc.vector.scalar_tensor_tensor(
+                out=slope[:], in0=tiles["var"][:], scalar=0.0, in1=grad_t[:, KIND_STD, :, targets],
+                op0=ALU.is_gt, op1=ALU.mult,
+            )
+            nc.vector.tensor_tensor(out=slope[:], in0=slope[:], in1=tiles["std"][:], op=ALU.mult)
+            nc.vector.tensor_tensor(out=offset[:], in0=slope[:], in1=tiles["moments"][:, 0], op=ALU.mult)
+            nc.vector.tensor_tensor(out=offset[:], in0=grad_t[:, KIND_MEAN, :, targets], in1=offset[:], op=ALU.subtract)
+            linear = work.tile([P, PLANES, BATCH_ROWS], F32, name="linear")
+            for plane in range(PLANES):
+                for g in range(BATCH_TARGETS):
+                    sources = slice(g * NODES, (g + 1) * NODES)
+                    nc.scalar.activation(
+                        out=linear[:, plane, sources],
+                        in_=tiles["m_t"][:, plane, sources],
+                        func=FUNC.Identity,
+                        scale=slope[:, plane, g : g + 1],
+                        bias=offset[:, plane, g : g + 1],
+                    )
+            tiles["linear"] = linear
+
+        def extremes(batch):
+            tiles = live[batch]
+            m_cells = tiles["m_t"][:].rearrange("p c (g j) -> p (c g) j", j=NODES)
             extreme = work.tile([P, 2, CELLS], F32, name="extreme")
             nc.vector.tensor_reduce(out=extreme[:, LOW, :], in_=m_cells, axis=INNERMOST, op=ALU.min)
             nc.vector.tensor_reduce(out=extreme[:, HIGH, :], in_=m_cells, axis=INNERMOST, op=ALU.max)
@@ -162,7 +211,6 @@ def tile_gnnlayer_pa_v_kernel(tc, x, e_enc, W_pre, b_pre, m, grad_out, out):
                 nc.vector.tensor_tensor(
                     out=at_extreme[:, side], in0=m_cells, in1=over_sources(extreme[:, side, :]), op=ALU.is_equal
                 )
-
             level = at_extreme[:].rearrange("p s x j -> p (s x) j")
             for halving in range(1, 6):
                 width = NODES >> halving
@@ -171,62 +219,37 @@ def tile_gnnlayer_pa_v_kernel(tc, x, e_enc, W_pre, b_pre, m, grad_out, out):
                     out=shorter[:], in0=level[:, :, 0:width], in1=level[:, :, width : 2 * width], op=ALU.add
                 )
                 level = shorter[:]
-            share = work.tile([P, 2, PLANES, BATCH_TARGETS], F32, name="share")
-            nc.vector.reciprocal(
-                out=share[:].rearrange("p s c g -> p (s c g)"), in_=level.rearrange("p x o -> p (x o)")
-            )
             amplitude = work.tile([P, 2, PLANES, BATCH_TARGETS], F32, name="amplitude")
-            nc.gpsimd.tensor_tensor(
-                out=amplitude[:], in0=grad_t[:, KIND_MIN : KIND_MAX + 1, :, targets], in1=share[:], op=ALU.mult
+            nc.vector.reciprocal(
+                out=amplitude[:].rearrange("p s c g -> p (s c g)"), in_=level.rearrange("p x o -> p (x o)")
             )
+            nc.vector.tensor_tensor(
+                out=amplitude[:],
+                in0=grad_t[:, KIND_MIN : KIND_MAX + 1, :, targets_of(batch)],
+                in1=amplitude[:],
+                op=ALU.mult,
+            )
+            tiles["at_extreme"] = at_extreme
+            tiles["amplitude"] = amplitude
 
-            cell_shape = [P, PLANES, BATCH_TARGETS]
-            moments = work.tile([P, 2, PLANES, BATCH_TARGETS], F32, name="moments")
-            nc.scalar.mul(out=moments[:], in_=sums[:], mul=1.0 / NODES)
-            mean = moments[:, 0]
-            var = work.tile(cell_shape, F32, name="var")
-            nc.gpsimd.tensor_tensor(out=var[:], in0=mean, in1=mean, op=ALU.mult)
-            nc.gpsimd.tensor_tensor(out=var[:], in0=moments[:, 1], in1=var[:], op=ALU.subtract)
-            std = work.tile(cell_shape, F32, name="std")
-            nc.gpsimd.tensor_scalar(
-                out=std[:], in0=var[:], scalar1=0.0, scalar2=EPS_STD, op0=ALU.max, op1=ALU.add
-            )
-            nc.scalar.activation(out=std[:], in_=std[:], func=FUNC.Sqrt)
-            slope = work.tile(cell_shape, F32, name="slope")
-            nc.gpsimd.tensor_scalar(
-                out=slope[:], in0=var[:], scalar1=0.0, scalar2=1.0, op0=ALU.is_gt, op1=ALU.mult
-            )
-            nc.gpsimd.tensor_tensor(out=slope[:], in0=slope[:], in1=grad_t[:, KIND_STD, :, targets], op=ALU.mult)
-            nc.vector.reciprocal(out=std[:], in_=std[:])
-            nc.gpsimd.tensor_tensor(out=slope[:], in0=slope[:], in1=std[:], op=ALU.mult)
-            offset = work.tile(cell_shape, F32, name="offset")
-            nc.gpsimd.tensor_tensor(out=offset[:], in0=slope[:], in1=mean, op=ALU.mult)
-            nc.gpsimd.tensor_tensor(out=offset[:], in0=grad_t[:, KIND_MEAN, :, targets], in1=offset[:], op=ALU.subtract)
-            return at_extreme, amplitude, slope, offset
-
-        def finish(batch, m_t, at_extreme, amplitude, slope, offset):
-            linear = work.tile([P, PLANES, BATCH_ROWS], F32, name="linear")
-            for plane in range(PLANES):
-                for g in range(BATCH_TARGETS):
-                    sources = slice(g * NODES, (g + 1) * NODES)
-                    nc.scalar.activation(
-                        out=linear[:, plane, sources],
-                        in_=m_t[:, plane, sources],
-                        func=FUNC.Identity,
-                        scale=slope[:, plane, g : g + 1],
-                        bias=offset[:, plane, g : g + 1],
-                    )
-            spikes = []
+        def spikes(batch):
+            tiles = live[batch]
             for side in (LOW, HIGH):
-                spike = scratch.tile([P, PLANES, BATCH_ROWS], F32, name="spike%d" % side)
-                nc.vector.tensor_tensor(
-                    out=spike[:].rearrange("p c (g j) -> p (c g) j", j=NODES),
-                    in0=at_extreme[:, side],
-                    in1=over_sources(amplitude[:, side].rearrange("p c g -> p (c g)")),
-                    op=ALU.mult,
-                )
-                spikes.append(spike)
-            nc.vector.tensor_tensor(out=spikes[LOW][:], in0=spikes[LOW][:], in1=linear[:], op=ALU.add)
+                spike = work.tile([P, PLANES, BATCH_ROWS], F32, name="spike%d" % side)
+                for plane in range(PLANES):
+                    for g in range(BATCH_TARGETS):
+                        nc.scalar.activation(
+                            out=spike[:, plane, g * NODES : (g + 1) * NODES],
+                            in_=tiles["at_extreme"][:, side, plane * BATCH_TARGETS + g, :],
+                            func=FUNC.Copy,
+                            scale=tiles["amplitude"][:, side, plane, g : g + 1],
+                        )
+                tiles["spike%d" % side] = spike
+
+        def assemble(batch):
+            tiles = live[batch]
+            low, high = tiles["spike%d" % LOW], tiles["spike%d" % HIGH]
+            nc.vector.tensor_tensor(out=low[:], in0=low[:], in1=tiles["linear"][:], op=ALU.add)
             dm_grouped = work.tile([P, PASSES, BATCH_ROWS, PACK], BF16, name="dm_grouped", align_bytes=64)
             dm_codes = work.tile([P, PASSES, BATCH_ROWS], U32, name="dm_codes", align_bytes=64)
             dm_scales = work.tile([P, PASSES, BATCH_ROWS], U8, name="dm_scales", align_bytes=64)
@@ -234,8 +257,8 @@ def tile_gnnlayer_pa_v_kernel(tc, x, e_enc, W_pre, b_pre, m, grad_out, out):
                 pass_planes = slice(h * PACK, (h + 1) * PACK)
                 nc.vector.tensor_tensor(
                     out=dm_grouped[:, h],
-                    in0=spikes[LOW][:, pass_planes, :].rearrange("p t r -> p r t"),
-                    in1=spikes[HIGH][:, pass_planes, :].rearrange("p t r -> p r t"),
+                    in0=low[:, pass_planes, :].rearrange("p t r -> p r t"),
+                    in1=high[:, pass_planes, :].rearrange("p t r -> p r t"),
                     op=ALU.add,
                 )
             for h in range(PASSES):
@@ -244,6 +267,10 @@ def tile_gnnlayer_pa_v_kernel(tc, x, e_enc, W_pre, b_pre, m, grad_out, out):
                     scales=dm_scales[:, h, :],
                     in_=dm_grouped[:, h].rearrange("p r t -> p (r t)"),
                 )
+            live[batch] = {"dm_codes": dm_codes, "dm_scales": dm_scales}
+
+        def product(batch):
+            dm_codes, dm_scales = live[batch]["dm_codes"], live[batch]["dm_scales"]
             for a in range(BATCH_TILES):
                 rows = slice(a * P, (a + 1) * P)
                 row0 = (batch * BATCH_TILES + a) * P
@@ -264,13 +291,25 @@ def tile_gnnlayer_pa_v_kernel(tc, x, e_enc, W_pre, b_pre, m, grad_out, out):
                     nc.scalar.copy(out=result[:, cols], in_=acc[:])
                 nc.scalar.dma_start(out=out_rows[row0 : row0 + P, :], in_=result[:])
 
+        def exists(batch):
+            return 0 <= batch < BATCHES
+
         prepare_grad()
-        m_t, sums = load_and_turn(0)
-        prepare_weight()
-        ready = (m_t,) + statistics(0, m_t, sums)
-        for batch in range(BATCHES):
-            current = ready
-            if batch + 1 < BATCHES:
-                m_t, sums = load_and_turn(batch + 1)
-                ready = (m_t,) + statistics(batch + 1, m_t, sums)
-            finish(batch, *current)
+        for step in range(-2, BATCHES + 1):
+            if exists(step - 1):
+                product(step - 1)
+            if exists(step + 2):
+                load_and_turn(step + 2)
+            if exists(step + 1):
+                linear_part(step + 1)
+                extremes(step + 1)
+            if exists(step + 2):
+                deviation(step + 2)
+            if exists(step + 1):
+                spikes(step + 1)
+            if step == -1:
+                turn_weight()
+            if exists(step):
+                assemble(step)
+            if step == 0:
+                quantise_weight()

@@ -57,13 +57,16 @@ def tile_gnnlayer_pa_v_kernel(tc, x, e_enc, W_pre, b_pre, m, grad_out, out):
     with ExitStack() as stack:
         keep = stack.enter_context(tc.tile_pool(name="keep", bufs=1))
         stream = stack.enter_context(tc.tile_pool(name="stream", bufs=3))
-        planes = stack.enter_context(tc.tile_pool(name="planes", bufs=3))
+        planes = stack.enter_context(tc.tile_pool(name="planes", bufs=4))
         work = stack.enter_context(tc.tile_pool(name="work", bufs=2))
         scratch = stack.enter_context(tc.tile_pool(name="scratch", bufs=1))
         psum_turn = stack.enter_context(tc.psum_pool(name="psum_turn", bufs=2))
-        psum_prep = stack.enter_context(tc.psum_pool(name="psum_prep", bufs=2))
-        psum_sums = stack.enter_context(tc.psum_pool(name="psum_sums", bufs=2))
-        psum_out = stack.enter_context(tc.psum_pool(name="psum_out", bufs=2))
+        psum_prep = stack.enter_context(tc.psum_pool(name="psum_prep", bufs=1))
+        psum_sums = stack.enter_context(tc.psum_pool(name="psum_sums", bufs=1))
+        psum_counts = stack.enter_context(tc.psum_pool(name="psum_counts", bufs=1))
+        psum_extreme = stack.enter_context(tc.psum_pool(name="psum_extreme", bufs=1))
+        psum_affine = stack.enter_context(tc.psum_pool(name="psum_affine", bufs=1))
+        psum_out = stack.enter_context(tc.psum_pool(name="psum_out", bufs=1))
         stack.enter_context(tc.manual_schedule())
 
         ident_f32 = keep.tile([P, P], F32)
@@ -77,6 +80,8 @@ def tile_gnnlayer_pa_v_kernel(tc, x, e_enc, W_pre, b_pre, m, grad_out, out):
             axis=INNERMOST,
             op=ALU.add,
         )
+        target_of_row_bf16 = keep.tile([P, TILE_TARGETS], BF16)
+        nc.vector.tensor_copy(out=target_of_row_bf16[:], in_=target_of_row[:])
 
         grad_t = keep.tile([P, KINDS, PLANES, TARGETS], F32)
         w_nat = keep.tile([P, CHANNELS // P, FEATURES], BF16)
@@ -164,9 +169,9 @@ def tile_gnnlayer_pa_v_kernel(tc, x, e_enc, W_pre, b_pre, m, grad_out, out):
 
         def deviation(batch):
             tiles = live[batch]
-            var = work.tile(cell_shape, F32, name="var")
+            var = planes.tile(cell_shape, F32, name="var")
             nc.vector.tensor_tensor(out=var[:], in0=tiles["moments"][:, 1], in1=tiles["mean_sq"][:], op=ALU.subtract)
-            std = work.tile(cell_shape, F32, name="std")
+            std = planes.tile(cell_shape, F32, name="std")
             nc.vector.tensor_scalar(
                 out=std[:], in0=var[:], scalar1=0.0, scalar2=EPS_STD, op0=ALU.max, op1=ALU.add
             )
@@ -174,54 +179,71 @@ def tile_gnnlayer_pa_v_kernel(tc, x, e_enc, W_pre, b_pre, m, grad_out, out):
             tiles["var"] = var
             tiles["std"] = std
 
-        def linear_part(batch):
-            tiles = live[batch]
-            targets = targets_of(batch)
-            slope = work.tile(cell_shape, F32, name="slope")
-            offset = work.tile(cell_shape, F32, name="offset")
-            nc.vector.reciprocal(out=tiles["std"][:], in_=tiles["std"][:])
-            nc.vector.scalar_tensor_tensor(
-                out=slope[:], in0=tiles["var"][:], scalar=0.0, in1=grad_t[:, KIND_STD, :, targets],
-                op0=ALU.is_gt, op1=ALU.mult,
-            )
-            nc.vector.tensor_tensor(out=slope[:], in0=slope[:], in1=tiles["std"][:], op=ALU.mult)
-            nc.vector.tensor_tensor(out=offset[:], in0=slope[:], in1=tiles["moments"][:, 0], op=ALU.mult)
-            nc.vector.tensor_tensor(out=offset[:], in0=grad_t[:, KIND_MEAN, :, targets], in1=offset[:], op=ALU.subtract)
-            linear = work.tile([P, PLANES, BATCH_ROWS], F32, name="linear")
-            for plane in range(PLANES):
-                for g in range(BATCH_TARGETS):
-                    sources = slice(g * NODES, (g + 1) * NODES)
-                    nc.scalar.activation(
-                        out=linear[:, plane, sources],
-                        in_=tiles["m_t"][:, plane, sources],
-                        func=FUNC.Identity,
-                        scale=slope[:, plane, g : g + 1],
-                        bias=offset[:, plane, g : g + 1],
-                    )
-            tiles["linear"] = linear
 
-        def extremes(batch):
+        def into_psum(values, pool, name):
+            turned = psum_turn.tile([P, PACK, P], F32, name="turned_m")
+            nc.tensor.transpose(turned[:, 0, :], values, ident_f32[:])
+            rows = work.tile([P, P], F32, name=name + "_rows")
+            nc.scalar.copy(out=rows[:], in_=turned[:, 0, :])
+            back = pool.tile([P, 2, CELLS], F32, name=name)
+            nc.tensor.transpose(back[:].rearrange("p s x -> p (s x)"), rows[:], ident_f32[:])
+            return back
+
+        def lowest_and_highest(batch):
             tiles = live[batch]
             m_cells = tiles["m_t"][:].rearrange("p c (g j) -> p (c g) j", j=NODES)
             extreme = work.tile([P, 2, CELLS], F32, name="extreme")
             nc.vector.tensor_reduce(out=extreme[:, LOW, :], in_=m_cells, axis=INNERMOST, op=ALU.min)
             nc.vector.tensor_reduce(out=extreme[:, HIGH, :], in_=m_cells, axis=INNERMOST, op=ALU.max)
+            tiles["extreme"] = into_psum(extreme[:].rearrange("p s x -> p (s x)"), psum_extreme, "extreme_ps")
+
+        def masks(batch):
+            tiles = live[batch]
+            m_cells = tiles["m_t"][:].rearrange("p c (g j) -> p (c g) j", j=NODES)
             at_extreme = work.tile([P, 2, CELLS, NODES], BF16, name="at_extreme")
             for side in (LOW, HIGH):
                 nc.vector.tensor_tensor(
-                    out=at_extreme[:, side], in0=m_cells, in1=over_sources(extreme[:, side, :]), op=ALU.is_equal
+                    out=at_extreme[:, side], in0=m_cells, in1=over_sources(tiles["extreme"][:, side, :]), op=ALU.is_equal
                 )
-            level = at_extreme[:].rearrange("p s x j -> p (s x) j")
-            for halving in range(1, 6):
-                width = NODES >> halving
-                shorter = scratch.tile([P, 2 * CELLS, width], F32 if width == 1 else BF16, name="count%d" % width)
-                nc.vector.tensor_tensor(
-                    out=shorter[:], in0=level[:, :, 0:width], in1=level[:, :, width : 2 * width], op=ALU.add
+            mask_blocks = at_extreme[:].rearrange("p s (k x) j -> p (s k) (x j)", x=TILE_TARGETS)
+            blocks = 2 * CELLS // TILE_TARGETS
+            mask_rows = scratch.tile([P, blocks, P], BF16, name="mask_rows")
+            for first in range(0, blocks, PLANES):
+                turned = psum_prep.tile([P, PLANES, P], BF16, name="turned")
+                for k in range(PLANES):
+                    nc.tensor.transpose(turned[:, k, :], mask_blocks[:, first + k, :], ident_bf16[:])
+                nc.scalar.copy(out=mask_rows[:, first : first + PLANES, :], in_=turned[:])
+            counts = psum_counts.tile([P, blocks, TILE_TARGETS], F32, name="counts")
+            for k in range(blocks):
+                nc.tensor.matmul(
+                    out=counts[:, k, :], lhsT=mask_rows[:, k, :], rhs=target_of_row_bf16[:], start=True, stop=True
                 )
-                level = shorter[:]
+            tiles["at_extreme"] = at_extreme
+            tiles["counts"] = counts
+
+        def slope_and_offset(batch):
+            tiles = live[batch]
+            targets = targets_of(batch)
+            affine = work.tile([P, 2, PLANES, BATCH_TARGETS], F32, name="affine")
+            slope, offset = affine[:, 0], affine[:, 1]
+            nc.vector.reciprocal(out=tiles["std"][:], in_=tiles["std"][:])
+            nc.vector.scalar_tensor_tensor(
+                out=slope, in0=tiles["var"][:], scalar=0.0, in1=grad_t[:, KIND_STD, :, targets],
+                op0=ALU.is_gt, op1=ALU.mult,
+            )
+            nc.vector.tensor_tensor(out=slope, in0=slope, in1=tiles["std"][:], op=ALU.mult)
+            nc.vector.tensor_tensor(out=offset, in0=slope, in1=tiles["moments"][:, 0], op=ALU.mult)
+            nc.vector.tensor_tensor(out=offset, in0=grad_t[:, KIND_MEAN, :, targets], in1=offset, op=ALU.subtract)
+            tiles["affine"] = into_psum(affine[:].rearrange("p s c g -> p (s c g)"), psum_affine, "affine_ps")
+
+        def cells(tile_of_planes):
+            return tile_of_planes[:].rearrange("p c (g j) -> p (c g) j", j=NODES)
+
+        def spikes(batch):
+            tiles = live[batch]
             amplitude = work.tile([P, 2, PLANES, BATCH_TARGETS], F32, name="amplitude")
             nc.vector.reciprocal(
-                out=amplitude[:].rearrange("p s c g -> p (s c g)"), in_=level.rearrange("p x o -> p (x o)")
+                out=amplitude[:].rearrange("p s c g -> p (s c g)"), in_=tiles["counts"][:].rearrange("p k x -> p (k x)")
             )
             nc.vector.tensor_tensor(
                 out=amplitude[:],
@@ -229,27 +251,31 @@ def tile_gnnlayer_pa_v_kernel(tc, x, e_enc, W_pre, b_pre, m, grad_out, out):
                 in1=amplitude[:],
                 op=ALU.mult,
             )
-            tiles["at_extreme"] = at_extreme
-            tiles["amplitude"] = amplitude
+            spike = work.tile([P, PLANES, BATCH_ROWS], F32, name="spike")
+            other = scratch.tile([P, PLANES, BATCH_ROWS], F32, name="other")
+            for side, product_tile in ((LOW, spike), (HIGH, other)):
+                nc.gpsimd.tensor_tensor(
+                    out=cells(product_tile),
+                    in0=tiles["at_extreme"][:, side],
+                    in1=over_sources(amplitude[:, side].rearrange("p c g -> p (c g)")),
+                    op=ALU.mult,
+                )
+            nc.gpsimd.tensor_tensor(out=spike[:], in0=spike[:], in1=other[:], op=ALU.add)
+            tiles["spike"] = spike
 
-        def spikes(batch):
+        def linear_part(batch):
             tiles = live[batch]
-            for side in (LOW, HIGH):
-                spike = work.tile([P, PLANES, BATCH_ROWS], F32, name="spike%d" % side)
-                for plane in range(PLANES):
-                    for g in range(BATCH_TARGETS):
-                        nc.scalar.activation(
-                            out=spike[:, plane, g * NODES : (g + 1) * NODES],
-                            in_=tiles["at_extreme"][:, side, plane * BATCH_TARGETS + g, :],
-                            func=FUNC.Copy,
-                            scale=tiles["amplitude"][:, side, plane, g : g + 1],
-                        )
-                tiles["spike%d" % side] = spike
+            linear = work.tile([P, PLANES, BATCH_ROWS], F32, name="linear")
+            nc.vector.tensor_tensor(
+                out=cells(linear), in0=cells(tiles["m_t"]), in1=over_sources(tiles["affine"][:, 0, :]), op=ALU.mult
+            )
+            nc.vector.tensor_tensor(
+                out=cells(linear), in0=cells(linear), in1=over_sources(tiles["affine"][:, 1, :]), op=ALU.add
+            )
+            tiles["linear"] = linear
 
-        def assemble(batch):
+        def quantise(batch):
             tiles = live[batch]
-            low, high = tiles["spike%d" % LOW], tiles["spike%d" % HIGH]
-            nc.vector.tensor_tensor(out=low[:], in0=low[:], in1=tiles["linear"][:], op=ALU.add)
             dm_grouped = work.tile([P, PASSES, BATCH_ROWS, PACK], BF16, name="dm_grouped", align_bytes=64)
             dm_codes = work.tile([P, PASSES, BATCH_ROWS], U32, name="dm_codes", align_bytes=64)
             dm_scales = work.tile([P, PASSES, BATCH_ROWS], U8, name="dm_scales", align_bytes=64)
@@ -257,8 +283,8 @@ def tile_gnnlayer_pa_v_kernel(tc, x, e_enc, W_pre, b_pre, m, grad_out, out):
                 pass_planes = slice(h * PACK, (h + 1) * PACK)
                 nc.vector.tensor_tensor(
                     out=dm_grouped[:, h],
-                    in0=low[:, pass_planes, :].rearrange("p t r -> p r t"),
-                    in1=high[:, pass_planes, :].rearrange("p t r -> p r t"),
+                    in0=tiles["linear"][:, pass_planes, :].rearrange("p t r -> p r t"),
+                    in1=tiles["spike"][:, pass_planes, :].rearrange("p t r -> p r t"),
                     op=ALU.add,
                 )
             for h in range(PASSES):
@@ -295,21 +321,26 @@ def tile_gnnlayer_pa_v_kernel(tc, x, e_enc, W_pre, b_pre, m, grad_out, out):
             return 0 <= batch < BATCHES
 
         prepare_grad()
-        for step in range(-2, BATCHES + 1):
-            if exists(step - 1):
-                product(step - 1)
-            if exists(step + 2):
-                load_and_turn(step + 2)
-            if exists(step + 1):
-                linear_part(step + 1)
-                extremes(step + 1)
-            if exists(step + 2):
-                deviation(step + 2)
-            if exists(step + 1):
-                spikes(step + 1)
-            if step == -1:
-                turn_weight()
+        for step in range(-4, BATCHES + 2):
+            if exists(step - 2):
+                product(step - 2)
             if exists(step):
-                assemble(step)
-            if step == 0:
+                spikes(step)
+            if exists(step + 2):
+                lowest_and_highest(step + 2)
+            if exists(step + 1):
+                masks(step + 1)
+            if exists(step + 3):
+                deviation(step + 3)
+            if exists(step + 1):
+                slope_and_offset(step + 1)
+            if exists(step):
+                linear_part(step)
+            if exists(step - 1):
+                quantise(step - 1)
+            if step == 1:
                 quantise_weight()
+            if exists(step + 4):
+                load_and_turn(step + 4)
+            if step == -2:
+                turn_weight()

@@ -60,13 +60,11 @@ def tile_gnnlayer_pa_v_kernel(tc, x, e_enc, W_pre, b_pre, m, grad_out, out):
         planes = stack.enter_context(tc.tile_pool(name="planes", bufs=4))
         work = stack.enter_context(tc.tile_pool(name="work", bufs=2))
         scratch = stack.enter_context(tc.tile_pool(name="scratch", bufs=1))
-        psum_turn = stack.enter_context(tc.psum_pool(name="psum_turn", bufs=2))
-        psum_prep = stack.enter_context(tc.psum_pool(name="psum_prep", bufs=1))
+        psum_turn = stack.enter_context(tc.psum_pool(name="psum_turn", bufs=3))
         psum_sums = stack.enter_context(tc.psum_pool(name="psum_sums", bufs=1))
-        psum_counts = stack.enter_context(tc.psum_pool(name="psum_counts", bufs=1))
         psum_extreme = stack.enter_context(tc.psum_pool(name="psum_extreme", bufs=1))
         psum_affine = stack.enter_context(tc.psum_pool(name="psum_affine", bufs=1))
-        psum_out = stack.enter_context(tc.psum_pool(name="psum_out", bufs=1))
+        psum_out = stack.enter_context(tc.psum_pool(name="psum_out", bufs=2))
         stack.enter_context(tc.manual_schedule())
 
         ident_f32 = keep.tile([P, P], F32)
@@ -80,8 +78,6 @@ def tile_gnnlayer_pa_v_kernel(tc, x, e_enc, W_pre, b_pre, m, grad_out, out):
             axis=INNERMOST,
             op=ALU.add,
         )
-        target_of_row_bf16 = keep.tile([P, TILE_TARGETS], BF16)
-        nc.vector.tensor_copy(out=target_of_row_bf16[:], in_=target_of_row[:])
 
         grad_t = keep.tile([P, KINDS, PLANES, TARGETS], F32)
         w_nat = keep.tile([P, CHANNELS // P, FEATURES], BF16)
@@ -102,7 +98,7 @@ def tile_gnnlayer_pa_v_kernel(tc, x, e_enc, W_pre, b_pre, m, grad_out, out):
                     in_=grad_rows[:, side * half : (side + 1) * half],
                 )
             for first in range(2):
-                turned = psum_prep.tile([P, PLANES, P], BF16, name="turned")
+                turned = psum_turn.tile([P, PLANES, P], BF16, name="turned", tag="turned_m")
                 for plane in range(PLANES):
                     col0 = (first * PLANES + plane) * P
                     nc.tensor.transpose(turned[:, plane, :], grad_nat[:, col0 : col0 + P], ident_bf16[:])
@@ -119,7 +115,7 @@ def tile_gnnlayer_pa_v_kernel(tc, x, e_enc, W_pre, b_pre, m, grad_out, out):
             nc.sync.dma_start(out=w_nat[:], in_=w_edge.rearrange("(a p) f -> p a f", p=P))
             for h in range(PASSES):
                 for a in range(CHANNELS // P):
-                    turned = psum_prep.tile([P, PACK, P], BF16, name="turned")
+                    turned = psum_turn.tile([P, PACK, P], BF16, name="turned", tag="turned_m")
                     for t in range(PACK):
                         col0 = (h * PACK + t) * P
                         nc.tensor.transpose(turned[:, t, :], w_nat[:, a, col0 : col0 + P], ident_bf16[:])
@@ -138,7 +134,7 @@ def tile_gnnlayer_pa_v_kernel(tc, x, e_enc, W_pre, b_pre, m, grad_out, out):
 
         def load_and_turn(batch):
             m_t = planes.tile([P, PLANES, BATCH_ROWS], F32, name="m_t")
-            sums = psum_sums.tile([P, 2, PLANES, BATCH_TARGETS], F32, name="sums")
+            sums = psum_sums.tile(cell_shape, F32, name="sums")
             for a in range(BATCH_TILES):
                 row0 = (batch * BATCH_TILES + a) * P
                 m_nat = stream.tile([P, FEATURES], F32, name="m_nat")
@@ -151,34 +147,17 @@ def tile_gnnlayer_pa_v_kernel(tc, x, e_enc, W_pre, b_pre, m, grad_out, out):
                         col0 = (h * PACK + t) * P
                         nc.tensor.transpose(turned[:, t, :], m_nat[:, col0 : col0 + P], ident_f32[:])
                     nc.scalar.copy(out=m_t[:, h * PACK : (h + 1) * PACK, a * P : (a + 1) * P], in_=turned[:])
-                targets = slice(a * TILE_TARGETS, (a + 1) * TILE_TARGETS)
-                for power, operand in enumerate((m_nat, m_sq)):
-                    for plane in range(PLANES):
-                        nc.tensor.matmul(
-                            out=sums[:, power, plane, targets],
-                            lhsT=operand[:, plane * P : (plane + 1) * P],
-                            rhs=target_of_row[:],
-                            start=True,
-                            stop=True,
-                        )
-            moments = planes.tile([P, 2, PLANES, BATCH_TARGETS], F32, name="moments")
-            nc.scalar.mul(out=moments[:], in_=sums[:], mul=1.0 / NODES)
-            mean_sq = work.tile(cell_shape, F32, name="mean_sq")
-            nc.scalar.activation(out=mean_sq[:], in_=moments[:, 0], func=FUNC.Square)
-            live[batch] = {"m_t": m_t, "moments": moments, "mean_sq": mean_sq}
-
-        def deviation(batch):
-            tiles = live[batch]
-            var = planes.tile(cell_shape, F32, name="var")
-            nc.vector.tensor_tensor(out=var[:], in0=tiles["moments"][:, 1], in1=tiles["mean_sq"][:], op=ALU.subtract)
-            std = planes.tile(cell_shape, F32, name="std")
-            nc.vector.tensor_scalar(
-                out=std[:], in0=var[:], scalar1=0.0, scalar2=EPS_STD, op0=ALU.max, op1=ALU.add
-            )
-            nc.scalar.activation(out=std[:], in_=std[:], func=FUNC.Sqrt)
-            tiles["var"] = var
-            tiles["std"] = std
-
+                for plane in range(PLANES):
+                    nc.tensor.matmul(
+                        out=sums[:, plane, a * TILE_TARGETS : (a + 1) * TILE_TARGETS],
+                        lhsT=m_sq[:, plane * P : (plane + 1) * P],
+                        rhs=target_of_row[:],
+                        start=True,
+                        stop=True,
+                    )
+            square_mean = planes.tile(cell_shape, F32, name="square_mean")
+            nc.scalar.mul(out=square_mean[:], in_=sums[:], mul=1.0 / NODES)
+            live[batch] = {"m_t": m_t, "square_mean": square_mean}
 
         def into_psum(values, pool, name):
             turned = psum_turn.tile([P, PACK, P], F32, name="turned_m")
@@ -189,13 +168,27 @@ def tile_gnnlayer_pa_v_kernel(tc, x, e_enc, W_pre, b_pre, m, grad_out, out):
             nc.tensor.transpose(back[:].rearrange("p s x -> p (s x)"), rows[:], ident_f32[:])
             return back
 
-        def lowest_and_highest(batch):
+        def reductions(batch):
             tiles = live[batch]
             m_cells = tiles["m_t"][:].rearrange("p c (g j) -> p (c g) j", j=NODES)
             extreme = work.tile([P, 2, CELLS], F32, name="extreme")
             nc.vector.tensor_reduce(out=extreme[:, LOW, :], in_=m_cells, axis=INNERMOST, op=ALU.min)
             nc.vector.tensor_reduce(out=extreme[:, HIGH, :], in_=m_cells, axis=INNERMOST, op=ALU.max)
             tiles["extreme"] = into_psum(extreme[:].rearrange("p s x -> p (s x)"), psum_extreme, "extreme_ps")
+            mean = planes.tile(cell_shape, F32, name="mean")
+            nc.vector.tensor_reduce(out=mean[:].rearrange("p c g -> p (c g)"), in_=m_cells, axis=INNERMOST, op=ALU.add)
+            nc.vector.tensor_scalar_mul(out=mean[:], in0=mean[:], scalar1=1.0 / NODES)
+            var = planes.tile(cell_shape, F32, name="var")
+            nc.vector.tensor_tensor(out=var[:], in0=mean[:], in1=mean[:], op=ALU.mult)
+            nc.vector.tensor_tensor(out=var[:], in0=tiles["square_mean"][:], in1=var[:], op=ALU.subtract)
+            std = planes.tile(cell_shape, F32, name="std")
+            nc.vector.tensor_scalar(
+                out=std[:], in0=var[:], scalar1=0.0, scalar2=EPS_STD, op0=ALU.max, op1=ALU.add
+            )
+            nc.scalar.activation(out=std[:], in_=std[:], func=FUNC.Sqrt)
+            tiles["mean"] = mean
+            tiles["var"] = var
+            tiles["std"] = std
 
         def masks(batch):
             tiles = live[batch]
@@ -205,21 +198,26 @@ def tile_gnnlayer_pa_v_kernel(tc, x, e_enc, W_pre, b_pre, m, grad_out, out):
                 nc.vector.tensor_tensor(
                     out=at_extreme[:, side], in0=m_cells, in1=over_sources(tiles["extreme"][:, side, :]), op=ALU.is_equal
                 )
-            mask_blocks = at_extreme[:].rearrange("p s (k x) j -> p (s k) (x j)", x=TILE_TARGETS)
-            blocks = 2 * CELLS // TILE_TARGETS
-            mask_rows = scratch.tile([P, blocks, P], BF16, name="mask_rows")
-            for first in range(0, blocks, PLANES):
-                turned = psum_prep.tile([P, PLANES, P], BF16, name="turned")
-                for k in range(PLANES):
-                    nc.tensor.transpose(turned[:, k, :], mask_blocks[:, first + k, :], ident_bf16[:])
-                nc.scalar.copy(out=mask_rows[:, first : first + PLANES, :], in_=turned[:])
-            counts = psum_counts.tile([P, blocks, TILE_TARGETS], F32, name="counts")
-            for k in range(blocks):
-                nc.tensor.matmul(
-                    out=counts[:, k, :], lhsT=mask_rows[:, k, :], rhs=target_of_row_bf16[:], start=True, stop=True
+            level = at_extreme[:].rearrange("p s x j -> p (s x) j")
+            for halving in range(1, 6):
+                width = NODES >> halving
+                shorter = scratch.tile([P, 2 * CELLS, width], F32 if width == 1 else BF16, name="count%d" % width)
+                nc.vector.tensor_tensor(
+                    out=shorter[:], in0=level[:, :, 0:width], in1=level[:, :, width : 2 * width], op=ALU.add
                 )
+                level = shorter[:]
+            amplitude = work.tile([P, 2, PLANES, BATCH_TARGETS], F32, name="amplitude")
+            nc.vector.reciprocal(
+                out=amplitude[:].rearrange("p s c g -> p (s c g)"), in_=level.rearrange("p x o -> p (x o)")
+            )
+            nc.vector.tensor_tensor(
+                out=amplitude[:],
+                in0=grad_t[:, KIND_MIN : KIND_MAX + 1, :, targets_of(batch)],
+                in1=amplitude[:],
+                op=ALU.mult,
+            )
             tiles["at_extreme"] = at_extreme
-            tiles["counts"] = counts
+            tiles["amplitude"] = amplitude
 
         def slope_and_offset(batch):
             tiles = live[batch]
@@ -232,7 +230,7 @@ def tile_gnnlayer_pa_v_kernel(tc, x, e_enc, W_pre, b_pre, m, grad_out, out):
                 op0=ALU.is_gt, op1=ALU.mult,
             )
             nc.vector.tensor_tensor(out=slope, in0=slope, in1=tiles["std"][:], op=ALU.mult)
-            nc.vector.tensor_tensor(out=offset, in0=slope, in1=tiles["moments"][:, 0], op=ALU.mult)
+            nc.vector.tensor_tensor(out=offset, in0=slope, in1=tiles["mean"][:], op=ALU.mult)
             nc.vector.tensor_tensor(out=offset, in0=grad_t[:, KIND_MEAN, :, targets], in1=offset, op=ALU.subtract)
             tiles["affine"] = into_psum(affine[:].rearrange("p s c g -> p (s c g)"), psum_affine, "affine_ps")
 
@@ -241,16 +239,7 @@ def tile_gnnlayer_pa_v_kernel(tc, x, e_enc, W_pre, b_pre, m, grad_out, out):
 
         def spikes(batch):
             tiles = live[batch]
-            amplitude = work.tile([P, 2, PLANES, BATCH_TARGETS], F32, name="amplitude")
-            nc.vector.reciprocal(
-                out=amplitude[:].rearrange("p s c g -> p (s c g)"), in_=tiles["counts"][:].rearrange("p k x -> p (k x)")
-            )
-            nc.vector.tensor_tensor(
-                out=amplitude[:],
-                in0=grad_t[:, KIND_MIN : KIND_MAX + 1, :, targets_of(batch)],
-                in1=amplitude[:],
-                op=ALU.mult,
-            )
+            amplitude = tiles["amplitude"]
             spike = work.tile([P, PLANES, BATCH_ROWS], F32, name="spike")
             other = scratch.tile([P, PLANES, BATCH_ROWS], F32, name="other")
             for side, product_tile in ((LOW, spike), (HIGH, other)):
@@ -265,7 +254,7 @@ def tile_gnnlayer_pa_v_kernel(tc, x, e_enc, W_pre, b_pre, m, grad_out, out):
 
         def linear_part(batch):
             tiles = live[batch]
-            linear = work.tile([P, PLANES, BATCH_ROWS], F32, name="linear")
+            linear = scratch.tile([P, PLANES, BATCH_ROWS], F32, name="linear")
             nc.vector.tensor_tensor(
                 out=cells(linear), in0=cells(tiles["m_t"]), in1=over_sources(tiles["affine"][:, 0, :]), op=ALU.mult
             )
@@ -321,26 +310,21 @@ def tile_gnnlayer_pa_v_kernel(tc, x, e_enc, W_pre, b_pre, m, grad_out, out):
             return 0 <= batch < BATCHES
 
         prepare_grad()
-        for step in range(-4, BATCHES + 2):
-            if exists(step - 2):
-                product(step - 2)
-            if exists(step):
-                spikes(step)
+        for step in range(-3, BATCHES + 1):
+            if exists(step - 1):
+                product(step - 1)
+            if exists(step + 3):
+                load_and_turn(step + 3)
             if exists(step + 2):
-                lowest_and_highest(step + 2)
+                reductions(step + 2)
             if exists(step + 1):
                 masks(step + 1)
-            if exists(step + 3):
-                deviation(step + 3)
-            if exists(step + 1):
+                spikes(step + 1)
                 slope_and_offset(step + 1)
+            if step == -1:
+                turn_weight()
             if exists(step):
                 linear_part(step)
-            if exists(step - 1):
-                quantise(step - 1)
-            if step == 1:
+                quantise(step)
+            if step == 0:
                 quantise_weight()
-            if exists(step + 4):
-                load_and_turn(step + 4)
-            if step == -2:
-                turn_weight()

@@ -60,10 +60,8 @@ def tile_gnnlayer_pa_v_kernel(tc, x, e_enc, W_pre, b_pre, m, grad_out, out):
         planes = stack.enter_context(tc.tile_pool(name="planes", bufs=4))
         work = stack.enter_context(tc.tile_pool(name="work", bufs=2))
         scratch = stack.enter_context(tc.tile_pool(name="scratch", bufs=1))
-        psum_turn = stack.enter_context(tc.psum_pool(name="psum_turn", bufs=3))
-        psum_sums = stack.enter_context(tc.psum_pool(name="psum_sums", bufs=1))
-        psum_extreme = stack.enter_context(tc.psum_pool(name="psum_extreme", bufs=1))
-        psum_affine = stack.enter_context(tc.psum_pool(name="psum_affine", bufs=1))
+        psum_turn = stack.enter_context(tc.psum_pool(name="psum_turn", bufs=4))
+        psum_sums = stack.enter_context(tc.psum_pool(name="psum_sums", bufs=2))
         psum_out = stack.enter_context(tc.psum_pool(name="psum_out", bufs=2))
         stack.enter_context(tc.manual_schedule())
 
@@ -111,18 +109,18 @@ def tile_gnnlayer_pa_v_kernel(tc, x, e_enc, W_pre, b_pre, m, grad_out, out):
                         scale=1.0 / NODES if kind in (KIND_MEAN, KIND_STD) else 1.0,
                     )
 
-        def turn_weight():
-            nc.sync.dma_start(out=w_nat[:], in_=w_edge.rearrange("(a p) f -> p a f", p=P))
-            for h in range(PASSES):
-                for a in range(CHANNELS // P):
-                    turned = psum_turn.tile([P, PACK, P], BF16, name="turned", tag="turned_m")
-                    for t in range(PACK):
-                        col0 = (h * PACK + t) * P
-                        nc.tensor.transpose(turned[:, t, :], w_nat[:, a, col0 : col0 + P], ident_bf16[:])
-                    nc.scalar.copy(
-                        out=w_grouped[:, h, a * P : (a + 1) * P, :],
-                        in_=turned[:].rearrange("p t c -> p c t"),
-                    )
+        def turn_weight(h):
+            features = slice(h * K_PASS, (h + 1) * K_PASS)
+            nc.sync.dma_start(out=w_nat[:, :, features], in_=w_edge[:, features].rearrange("(a p) f -> p a f", p=P))
+            for a in range(CHANNELS // P):
+                turned = psum_turn.tile([P, PACK, P], BF16, name="turned", tag="turned_m")
+                for t in range(PACK):
+                    col0 = (h * PACK + t) * P
+                    nc.tensor.transpose(turned[:, t, :], w_nat[:, a, col0 : col0 + P], ident_bf16[:])
+                nc.scalar.copy(
+                    out=w_grouped[:, h, a * P : (a + 1) * P, :],
+                    in_=turned[:].rearrange("p t c -> p c t"),
+                )
 
         def quantise_weight():
             for h in range(PASSES):
@@ -159,45 +157,24 @@ def tile_gnnlayer_pa_v_kernel(tc, x, e_enc, W_pre, b_pre, m, grad_out, out):
             nc.scalar.mul(out=square_mean[:], in_=sums[:], mul=1.0 / NODES)
             live[batch] = {"m_t": m_t, "square_mean": square_mean}
 
-        def into_psum(values, pool, name):
-            turned = psum_turn.tile([P, PACK, P], F32, name="turned_m")
-            nc.tensor.transpose(turned[:, 0, :], values, ident_f32[:])
-            rows = work.tile([P, P], F32, name=name + "_rows")
-            nc.scalar.copy(out=rows[:], in_=turned[:, 0, :])
-            back = pool.tile([P, 2, CELLS], F32, name=name)
-            nc.tensor.transpose(back[:].rearrange("p s x -> p (s x)"), rows[:], ident_f32[:])
-            return back
-
-        def reductions(batch):
+        def statistics(batch):
             tiles = live[batch]
             m_cells = tiles["m_t"][:].rearrange("p c (g j) -> p (c g) j", j=NODES)
+            both_shape = [P, 2, CELLS, NODES]
             extreme = work.tile([P, 2, CELLS], F32, name="extreme")
             nc.vector.tensor_reduce(out=extreme[:, LOW, :], in_=m_cells, axis=INNERMOST, op=ALU.min)
             nc.vector.tensor_reduce(out=extreme[:, HIGH, :], in_=m_cells, axis=INNERMOST, op=ALU.max)
-            tiles["extreme"] = into_psum(extreme[:].rearrange("p s x -> p (s x)"), psum_extreme, "extreme_ps")
-            mean = planes.tile(cell_shape, F32, name="mean")
-            nc.vector.tensor_reduce(out=mean[:].rearrange("p c g -> p (c g)"), in_=m_cells, axis=INNERMOST, op=ALU.add)
-            nc.vector.tensor_scalar_mul(out=mean[:], in0=mean[:], scalar1=1.0 / NODES)
-            var = planes.tile(cell_shape, F32, name="var")
-            nc.vector.tensor_tensor(out=var[:], in0=mean[:], in1=mean[:], op=ALU.mult)
-            nc.vector.tensor_tensor(out=var[:], in0=tiles["square_mean"][:], in1=var[:], op=ALU.subtract)
-            std = planes.tile(cell_shape, F32, name="std")
-            nc.vector.tensor_scalar(
-                out=std[:], in0=var[:], scalar1=0.0, scalar2=EPS_STD, op0=ALU.max, op1=ALU.add
+            total = work.tile(cell_shape, F32, name="total")
+            nc.vector.tensor_reduce(out=total[:].rearrange("p c g -> p (c g)"), in_=m_cells, axis=INNERMOST, op=ALU.add)
+            mean_sq = work.tile(cell_shape, F32, name="mean_sq")
+            nc.scalar.activation(out=mean_sq[:], in_=total[:], func=FUNC.Square, scale=1.0 / NODES)
+            at_extreme = work.tile(both_shape, BF16, name="at_extreme")
+            nc.vector.tensor_tensor(
+                out=at_extreme[:],
+                in0=m_cells.unsqueeze(1).to_broadcast(both_shape),
+                in1=extreme[:].unsqueeze(3).to_broadcast(both_shape),
+                op=ALU.is_equal,
             )
-            nc.scalar.activation(out=std[:], in_=std[:], func=FUNC.Sqrt)
-            tiles["mean"] = mean
-            tiles["var"] = var
-            tiles["std"] = std
-
-        def masks(batch):
-            tiles = live[batch]
-            m_cells = tiles["m_t"][:].rearrange("p c (g j) -> p (c g) j", j=NODES)
-            at_extreme = work.tile([P, 2, CELLS, NODES], BF16, name="at_extreme")
-            for side in (LOW, HIGH):
-                nc.vector.tensor_tensor(
-                    out=at_extreme[:, side], in0=m_cells, in1=over_sources(tiles["extreme"][:, side, :]), op=ALU.is_equal
-                )
             level = at_extreme[:].rearrange("p s x j -> p (s x) j")
             for halving in range(1, 6):
                 width = NODES >> halving
@@ -216,72 +193,79 @@ def tile_gnnlayer_pa_v_kernel(tc, x, e_enc, W_pre, b_pre, m, grad_out, out):
                 in1=amplitude[:],
                 op=ALU.mult,
             )
+            var = work.tile(cell_shape, F32, name="var")
+            nc.vector.tensor_tensor(out=var[:], in0=tiles["square_mean"][:], in1=mean_sq[:], op=ALU.subtract)
+            std = work.tile(cell_shape, F32, name="std")
+            nc.vector.tensor_scalar(
+                out=std[:], in0=var[:], scalar1=0.0, scalar2=EPS_STD, op0=ALU.max, op1=ALU.add
+            )
+            nc.scalar.activation(out=std[:], in_=std[:], func=FUNC.Sqrt)
+            tiles["total"] = total
             tiles["at_extreme"] = at_extreme
             tiles["amplitude"] = amplitude
+            tiles["var"] = var
+            tiles["std"] = std
 
         def slope_and_offset(batch):
             tiles = live[batch]
             targets = targets_of(batch)
-            affine = work.tile([P, 2, PLANES, BATCH_TARGETS], F32, name="affine")
-            slope, offset = affine[:, 0], affine[:, 1]
+            slope = work.tile(cell_shape, F32, name="slope")
+            offset = work.tile(cell_shape, F32, name="offset")
             nc.vector.reciprocal(out=tiles["std"][:], in_=tiles["std"][:])
             nc.vector.scalar_tensor_tensor(
-                out=slope, in0=tiles["var"][:], scalar=0.0, in1=grad_t[:, KIND_STD, :, targets],
+                out=slope[:], in0=tiles["var"][:], scalar=0.0, in1=grad_t[:, KIND_STD, :, targets],
                 op0=ALU.is_gt, op1=ALU.mult,
             )
-            nc.vector.tensor_tensor(out=slope, in0=slope, in1=tiles["std"][:], op=ALU.mult)
-            nc.vector.tensor_tensor(out=offset, in0=slope, in1=tiles["mean"][:], op=ALU.mult)
-            nc.vector.tensor_tensor(out=offset, in0=grad_t[:, KIND_MEAN, :, targets], in1=offset, op=ALU.subtract)
-            tiles["affine"] = into_psum(affine[:].rearrange("p s c g -> p (s c g)"), psum_affine, "affine_ps")
-
-        def cells(tile_of_planes):
-            return tile_of_planes[:].rearrange("p c (g j) -> p (c g) j", j=NODES)
-
-        def spikes(batch):
-            tiles = live[batch]
-            amplitude = tiles["amplitude"]
-            spike = work.tile([P, PLANES, BATCH_ROWS], F32, name="spike")
-            other = scratch.tile([P, PLANES, BATCH_ROWS], F32, name="other")
-            for side, product_tile in ((LOW, spike), (HIGH, other)):
-                nc.gpsimd.tensor_tensor(
-                    out=cells(product_tile),
-                    in0=tiles["at_extreme"][:, side],
-                    in1=over_sources(amplitude[:, side].rearrange("p c g -> p (c g)")),
-                    op=ALU.mult,
-                )
-            nc.gpsimd.tensor_tensor(out=spike[:], in0=spike[:], in1=other[:], op=ALU.add)
-            tiles["spike"] = spike
+            nc.vector.tensor_tensor(out=slope[:], in0=slope[:], in1=tiles["std"][:], op=ALU.mult)
+            nc.vector.scalar_tensor_tensor(
+                out=offset[:], in0=tiles["total"][:], scalar=1.0 / NODES, in1=slope[:], op0=ALU.mult, op1=ALU.mult
+            )
+            nc.vector.tensor_tensor(out=offset[:], in0=grad_t[:, KIND_MEAN, :, targets], in1=offset[:], op=ALU.subtract)
+            tiles["slope"] = slope
+            tiles["offset"] = offset
 
         def linear_part(batch):
             tiles = live[batch]
-            linear = scratch.tile([P, PLANES, BATCH_ROWS], F32, name="linear")
-            nc.vector.tensor_tensor(
-                out=cells(linear), in0=cells(tiles["m_t"]), in1=over_sources(tiles["affine"][:, 0, :]), op=ALU.mult
-            )
-            nc.vector.tensor_tensor(
-                out=cells(linear), in0=cells(linear), in1=over_sources(tiles["affine"][:, 1, :]), op=ALU.add
-            )
+            linear = work.tile([P, PLANES, BATCH_ROWS], F32, name="linear")
+            for plane in range(PLANES):
+                for g in range(BATCH_TARGETS):
+                    sources = slice(g * NODES, (g + 1) * NODES)
+                    nc.scalar.activation(
+                        out=linear[:, plane, sources],
+                        in_=tiles["m_t"][:, plane, sources],
+                        func=FUNC.Identity,
+                        scale=tiles["slope"][:, plane, g : g + 1],
+                        bias=tiles["offset"][:, plane, g : g + 1],
+                    )
             tiles["linear"] = linear
 
-        def quantise(batch):
+        def assemble(batch):
             tiles = live[batch]
+            both_shape = [P, 2, CELLS, NODES]
+            spikes = scratch.tile(both_shape, F32, name="spikes")
+            nc.vector.tensor_tensor(
+                out=spikes[:],
+                in0=tiles["at_extreme"][:],
+                in1=tiles["amplitude"][:].rearrange("p s c g -> p s (c g)").unsqueeze(3).to_broadcast(both_shape),
+                op=ALU.mult,
+            )
+            low = spikes[:, LOW].rearrange("p (c g) j -> p c (g j)", c=PLANES)
+            high = spikes[:, HIGH].rearrange("p (c g) j -> p c (g j)", c=PLANES)
+            nc.vector.tensor_tensor(out=low, in0=low, in1=tiles["linear"][:], op=ALU.add)
             dm_grouped = work.tile([P, PASSES, BATCH_ROWS, PACK], BF16, name="dm_grouped", align_bytes=64)
             dm_codes = work.tile([P, PASSES, BATCH_ROWS], U32, name="dm_codes", align_bytes=64)
             dm_scales = work.tile([P, PASSES, BATCH_ROWS], U8, name="dm_scales", align_bytes=64)
-            for h in range(PASSES):
-                pass_planes = slice(h * PACK, (h + 1) * PACK)
-                nc.vector.tensor_tensor(
-                    out=dm_grouped[:, h],
-                    in0=tiles["linear"][:, pass_planes, :].rearrange("p t r -> p r t"),
-                    in1=tiles["spike"][:, pass_planes, :].rearrange("p t r -> p r t"),
-                    op=ALU.add,
-                )
-            for h in range(PASSES):
-                nc.vector.quantize_mx(
-                    out=dm_codes[:, h, :].bitcast(E5M2_X4),
-                    scales=dm_scales[:, h, :],
-                    in_=dm_grouped[:, h].rearrange("p r t -> p (r t)"),
-                )
+            nc.vector.tensor_tensor(
+                out=dm_grouped[:],
+                in0=low.rearrange("p (h t) r -> p h r t", t=PACK),
+                in1=high.rearrange("p (h t) r -> p h r t", t=PACK),
+                op=ALU.add,
+            )
+            nc.vector.quantize_mx(
+                out=dm_codes[:].rearrange("p h r -> p (h r)").bitcast(E5M2_X4),
+                scales=dm_scales[:].rearrange("p h r -> p (h r)"),
+                in_=dm_grouped[:].rearrange("p h r t -> p (h r t)"),
+            )
             live[batch] = {"dm_codes": dm_codes, "dm_scales": dm_scales}
 
         def product(batch):
@@ -309,22 +293,22 @@ def tile_gnnlayer_pa_v_kernel(tc, x, e_enc, W_pre, b_pre, m, grad_out, out):
         def exists(batch):
             return 0 <= batch < BATCHES
 
-        prepare_grad()
         for step in range(-3, BATCHES + 1):
-            if exists(step - 1):
-                product(step - 1)
-            if exists(step + 3):
-                load_and_turn(step + 3)
-            if exists(step + 2):
-                reductions(step + 2)
-            if exists(step + 1):
-                masks(step + 1)
-                spikes(step + 1)
-                slope_and_offset(step + 1)
-            if step == -1:
-                turn_weight()
             if exists(step):
                 linear_part(step)
-                quantise(step)
+            if exists(step - 1):
+                product(step - 1)
+            if exists(step + 1):
+                statistics(step + 1)
+            if exists(step):
+                assemble(step)
             if step == 0:
                 quantise_weight()
+            if exists(step + 1):
+                slope_and_offset(step + 1)
+            if exists(step + 3):
+                load_and_turn(step + 3)
+            if step == -3:
+                prepare_grad()
+            if step in (-2, -1):
+                turn_weight(step + PASSES)

@@ -37,6 +37,7 @@ CELLS = PLANES * BATCH_TARGETS
 KIND_MEAN, KIND_MIN, KIND_MAX, KIND_STD = 0, 1, 2, 3
 KINDS = 4
 LOW, HIGH = 0, 1
+FIRST, SECOND = 0, 1
 
 FLOPS = 2 * ROWS * FEATURES * CHANNELS
 BYTES = 4 * ROWS * FEATURES + 2 * TARGETS * KINDS * FEATURES + 2 * CHANNELS * FEATURES + 4 * ROWS * CHANNELS
@@ -56,8 +57,10 @@ def tile_gnnlayer_pa_v_kernel(tc, x, e_enc, W_pre, b_pre, m, grad_out, out):
 
     with ExitStack() as stack:
         keep = stack.enter_context(tc.tile_pool(name="keep", bufs=1))
+        loads = stack.enter_context(tc.tile_pool(name="loads", bufs=2 * BATCH_TILES))
         stream = stack.enter_context(tc.tile_pool(name="stream", bufs=3))
         planes = stack.enter_context(tc.tile_pool(name="planes", bufs=4))
+        three = stack.enter_context(tc.tile_pool(name="three", bufs=3))
         work = stack.enter_context(tc.tile_pool(name="work", bufs=2))
         scratch = stack.enter_context(tc.tile_pool(name="scratch", bufs=1))
         psum_turn = stack.enter_context(tc.psum_pool(name="psum_turn", bufs=4))
@@ -77,6 +80,8 @@ def tile_gnnlayer_pa_v_kernel(tc, x, e_enc, W_pre, b_pre, m, grad_out, out):
             op=ALU.add,
         )
 
+        grad_half = KINDS * FEATURES // 2
+        grad_nat = keep.tile([P, grad_half], BF16)
         grad_t = keep.tile([P, KINDS, PLANES, TARGETS], F32)
         w_nat = keep.tile([P, CHANNELS // P, FEATURES], BF16)
         w_grouped = keep.tile([P, PASSES, CHANNELS, PACK], BF16, align_bytes=64)
@@ -87,14 +92,14 @@ def tile_gnnlayer_pa_v_kernel(tc, x, e_enc, W_pre, b_pre, m, grad_out, out):
         def targets_of(batch):
             return slice(batch * BATCH_TARGETS, (batch + 1) * BATCH_TARGETS)
 
-        def prepare_grad():
-            half = KINDS * FEATURES // 2
-            grad_nat = keep.tile([P, half], BF16)
+        def load_grad():
             for side in range(2):
                 nc.sync.dma_start(
                     out=grad_nat[side * TARGETS : (side + 1) * TARGETS, :],
-                    in_=grad_rows[:, side * half : (side + 1) * half],
+                    in_=grad_rows[:, side * grad_half : (side + 1) * grad_half],
                 )
+
+        def prepare_grad():
             for first in range(2):
                 turned = psum_turn.tile([P, PLANES, P], BF16, name="turned", tag="turned_m")
                 for plane in range(PLANES):
@@ -109,9 +114,11 @@ def tile_gnnlayer_pa_v_kernel(tc, x, e_enc, W_pre, b_pre, m, grad_out, out):
                         scale=1.0 / NODES if kind in (KIND_MEAN, KIND_STD) else 1.0,
                     )
 
-        def turn_weight(h):
+        def load_weight(h):
             features = slice(h * K_PASS, (h + 1) * K_PASS)
             nc.sync.dma_start(out=w_nat[:, :, features], in_=w_edge[:, features].rearrange("(a p) f -> p a f", p=P))
+
+        def turn_weight(h):
             for a in range(CHANNELS // P):
                 turned = psum_turn.tile([P, PACK, P], BF16, name="turned", tag="turned_m")
                 for t in range(PACK):
@@ -130,99 +137,137 @@ def tile_gnnlayer_pa_v_kernel(tc, x, e_enc, W_pre, b_pre, m, grad_out, out):
                     in_=w_grouped[:, h].rearrange("p c t -> p (c t)"),
                 )
 
-        def load_and_turn(batch):
-            m_t = planes.tile([P, PLANES, BATCH_ROWS], F32, name="m_t")
-            sums = psum_sums.tile(cell_shape, F32, name="sums")
+        def load(batch):
+            m_nat = []
             for a in range(BATCH_TILES):
                 row0 = (batch * BATCH_TILES + a) * P
-                m_nat = stream.tile([P, FEATURES], F32, name="m_nat")
-                nc.sync.dma_start(out=m_nat[:], in_=m_rows[row0 : row0 + P, :])
-                m_sq = stream.tile([P, FEATURES], F32, name="m_sq")
-                nc.scalar.activation(out=m_sq[:], in_=m_nat[:], func=FUNC.Square)
+                rows = loads.tile([P, FEATURES], F32, name="m_nat")
+                nc.sync.dma_start(out=rows[:], in_=m_rows[row0 : row0 + P, :])
+                m_nat.append(rows)
+            live[batch] = {"m_nat": m_nat}
+
+        def turn(batch):
+            tiles = live[batch]
+            m_t = planes.tile([P, PLANES, BATCH_ROWS], F32, name="m_t")
+            sums = psum_sums.tile([P, 2, PLANES, BATCH_TARGETS], F32, name="sums")
+            m_sq = []
+            for a in range(BATCH_TILES):
+                squares = work.tile([P, FEATURES], F32, name="m_sq")
+                nc.scalar.activation(out=squares[:], in_=tiles["m_nat"][a][:], func=FUNC.Square)
+                m_sq.append(squares)
+            for a in range(BATCH_TILES):
+                m_nat = tiles["m_nat"][a]
                 for h in range(PASSES):
                     turned = psum_turn.tile([P, PACK, P], F32, name="turned_m")
                     for t in range(PACK):
                         col0 = (h * PACK + t) * P
                         nc.tensor.transpose(turned[:, t, :], m_nat[:, col0 : col0 + P], ident_f32[:])
                     nc.scalar.copy(out=m_t[:, h * PACK : (h + 1) * PACK, a * P : (a + 1) * P], in_=turned[:])
-                for plane in range(PLANES):
-                    nc.tensor.matmul(
-                        out=sums[:, plane, a * TILE_TARGETS : (a + 1) * TILE_TARGETS],
-                        lhsT=m_sq[:, plane * P : (plane + 1) * P],
-                        rhs=target_of_row[:],
-                        start=True,
-                        stop=True,
-                    )
-            square_mean = planes.tile(cell_shape, F32, name="square_mean")
-            nc.scalar.mul(out=square_mean[:], in_=sums[:], mul=1.0 / NODES)
-            live[batch] = {"m_t": m_t, "square_mean": square_mean}
-
-        def statistics(batch):
-            tiles = live[batch]
-            m_cells = tiles["m_t"][:].rearrange("p c (g j) -> p (c g) j", j=NODES)
-            both_shape = [P, 2, CELLS, NODES]
-            extreme = work.tile([P, 2, CELLS], F32, name="extreme")
-            nc.vector.tensor_reduce(out=extreme[:, LOW, :], in_=m_cells, axis=INNERMOST, op=ALU.min)
-            nc.vector.tensor_reduce(out=extreme[:, HIGH, :], in_=m_cells, axis=INNERMOST, op=ALU.max)
-            total = work.tile(cell_shape, F32, name="total")
-            nc.vector.tensor_reduce(out=total[:].rearrange("p c g -> p (c g)"), in_=m_cells, axis=INNERMOST, op=ALU.add)
+            for moment, rows in ((FIRST, tiles["m_nat"]), (SECOND, m_sq)):
+                for a in range(BATCH_TILES):
+                    for plane in range(PLANES):
+                        nc.tensor.matmul(
+                            out=sums[:, moment, plane, a * TILE_TARGETS : (a + 1) * TILE_TARGETS],
+                            lhsT=rows[a][:, plane * P : (plane + 1) * P],
+                            rhs=target_of_row[:],
+                            start=True,
+                            stop=True,
+                        )
+            moments = three.tile([P, 2, PLANES, BATCH_TARGETS], F32, name="moments")
+            nc.scalar.mul(out=moments[:], in_=sums[:], mul=1.0 / NODES)
             mean_sq = work.tile(cell_shape, F32, name="mean_sq")
-            nc.scalar.activation(out=mean_sq[:], in_=total[:], func=FUNC.Square, scale=1.0 / NODES)
-            at_extreme = work.tile(both_shape, BF16, name="at_extreme")
+            nc.scalar.activation(out=mean_sq[:], in_=sums[:, FIRST], func=FUNC.Square, scale=1.0 / NODES)
+            live[batch] = {"m_t": m_t, "moments": moments, "mean_sq": mean_sq}
+
+        def m_cells(batch):
+            return live[batch]["m_t"][:].rearrange("p c (g j) -> p (c g) j", j=NODES)
+
+        def extreme(batch, end):
+            tiles = live[batch]
+            if end == LOW:
+                tiles["extreme"] = work.tile([P, 2, CELLS], F32, name="extreme")
+            nc.vector.tensor_reduce(
+                out=tiles["extreme"][:, end, :], in_=m_cells(batch), axis=INNERMOST, op=ALU.min if end == LOW else ALU.max
+            )
+
+        def variance(batch):
+            tiles = live[batch]
+            tiles["var"] = work.tile(cell_shape, F32, name="var")
             nc.vector.tensor_tensor(
-                out=at_extreme[:],
-                in0=m_cells.unsqueeze(1).to_broadcast(both_shape),
-                in1=extreme[:].unsqueeze(3).to_broadcast(both_shape),
+                out=tiles["var"][:], in0=tiles["moments"][:, SECOND], in1=tiles["mean_sq"][:], op=ALU.subtract
+            )
+
+        def std_squared(batch):
+            tiles = live[batch]
+            tiles["divisors"] = work.tile([P, 3, PLANES, BATCH_TARGETS], F32, name="divisors")
+            nc.vector.tensor_scalar(
+                out=tiles["divisors"][:, 2], in0=tiles["var"][:], scalar1=0.0, scalar2=EPS_STD, op0=ALU.max, op1=ALU.add
+            )
+
+        def std_root(batch):
+            std = live[batch]["divisors"][:, 2]
+            nc.scalar.activation(out=std, in_=std, func=FUNC.Sqrt)
+
+        def compare(batch, end):
+            tiles = live[batch]
+            if end == LOW:
+                tiles["at_extreme"] = three.tile([P, 2, CELLS, NODES], BF16, name="at_extreme")
+            nc.vector.tensor_tensor(
+                out=tiles["at_extreme"][:, end],
+                in0=m_cells(batch),
+                in1=over_sources(tiles["extreme"][:, end, :]),
                 op=ALU.is_equal,
             )
-            level = at_extreme[:].rearrange("p s x j -> p (s x) j")
-            for halving in range(1, 6):
-                width = NODES >> halving
-                shorter = scratch.tile([P, 2 * CELLS, width], F32 if width == 1 else BF16, name="count%d" % width)
-                nc.vector.tensor_tensor(
-                    out=shorter[:], in0=level[:, :, 0:width], in1=level[:, :, width : 2 * width], op=ALU.add
-                )
-                level = shorter[:]
-            amplitude = work.tile([P, 2, PLANES, BATCH_TARGETS], F32, name="amplitude")
-            nc.vector.reciprocal(
-                out=amplitude[:].rearrange("p s c g -> p (s c g)"), in_=level.rearrange("p x o -> p (x o)")
-            )
+
+        def count(batch, halving):
+            tiles = live[batch]
+            width = NODES >> halving
+            if halving == 1:
+                tiles["level"] = tiles["at_extreme"][:].rearrange("p s x j -> p (s x) j")
+            level = tiles["level"]
+            if width == 1:
+                shorter = tiles["divisors"][:, 0:2].rearrange("p s c g -> p (s c g)").unsqueeze(2)
+            else:
+                counts = scratch.tile([P, 2 * CELLS, width], BF16, name="count%d" % width)
+                shorter = counts[:]
+            nc.vector.tensor_tensor(out=shorter, in0=level[:, :, 0:width], in1=level[:, :, width : 2 * width], op=ALU.add)
+            tiles["level"] = shorter
+
+        def invert(batch):
+            divisors = live[batch]["divisors"][:].rearrange("p s c g -> p (s c g)")
+            nc.vector.reciprocal(out=divisors, in_=divisors)
+
+        def divide(batch):
+            tiles = live[batch]
+            tiles["quotients"] = work.tile([P, 3, PLANES, BATCH_TARGETS], F32, name="quotients")
             nc.vector.tensor_tensor(
-                out=amplitude[:],
-                in0=grad_t[:, KIND_MIN : KIND_MAX + 1, :, targets_of(batch)],
-                in1=amplitude[:],
+                out=tiles["quotients"][:],
+                in0=grad_t[:, KIND_MIN : KIND_STD + 1, :, targets_of(batch)],
+                in1=tiles["divisors"][:],
                 op=ALU.mult,
             )
-            var = work.tile(cell_shape, F32, name="var")
-            nc.vector.tensor_tensor(out=var[:], in0=tiles["square_mean"][:], in1=mean_sq[:], op=ALU.subtract)
-            std = work.tile(cell_shape, F32, name="std")
-            nc.vector.tensor_scalar(
-                out=std[:], in0=var[:], scalar1=0.0, scalar2=EPS_STD, op0=ALU.max, op1=ALU.add
-            )
-            nc.scalar.activation(out=std[:], in_=std[:], func=FUNC.Sqrt)
-            tiles["total"] = total
-            tiles["at_extreme"] = at_extreme
-            tiles["amplitude"] = amplitude
-            tiles["var"] = var
-            tiles["std"] = std
 
-        def slope_and_offset(batch):
+        def slope(batch):
             tiles = live[batch]
-            targets = targets_of(batch)
-            slope = work.tile(cell_shape, F32, name="slope")
-            offset = work.tile(cell_shape, F32, name="offset")
-            nc.vector.reciprocal(out=tiles["std"][:], in_=tiles["std"][:])
+            tiles["slope"] = work.tile(cell_shape, F32, name="slope")
             nc.vector.scalar_tensor_tensor(
-                out=slope[:], in0=tiles["var"][:], scalar=0.0, in1=grad_t[:, KIND_STD, :, targets],
+                out=tiles["slope"][:], in0=tiles["var"][:], scalar=0.0, in1=tiles["quotients"][:, 2],
                 op0=ALU.is_gt, op1=ALU.mult,
             )
-            nc.vector.tensor_tensor(out=slope[:], in0=slope[:], in1=tiles["std"][:], op=ALU.mult)
-            nc.vector.scalar_tensor_tensor(
-                out=offset[:], in0=tiles["total"][:], scalar=1.0 / NODES, in1=slope[:], op0=ALU.mult, op1=ALU.mult
+
+        def slope_mean(batch):
+            tiles = live[batch]
+            tiles["offset"] = work.tile(cell_shape, F32, name="offset")
+            nc.vector.tensor_tensor(
+                out=tiles["offset"][:], in0=tiles["moments"][:, FIRST], in1=tiles["slope"][:], op=ALU.mult
             )
-            nc.vector.tensor_tensor(out=offset[:], in0=grad_t[:, KIND_MEAN, :, targets], in1=offset[:], op=ALU.subtract)
-            tiles["slope"] = slope
-            tiles["offset"] = offset
+
+        def offset(batch):
+            tiles = live[batch]
+            nc.vector.tensor_tensor(
+                out=tiles["offset"][:], in0=grad_t[:, KIND_MEAN, :, targets_of(batch)], in1=tiles["offset"][:],
+                op=ALU.subtract,
+            )
 
         def linear_part(batch):
             tiles = live[batch]
@@ -239,32 +284,42 @@ def tile_gnnlayer_pa_v_kernel(tc, x, e_enc, W_pre, b_pre, m, grad_out, out):
                     )
             tiles["linear"] = linear
 
-        def assemble(batch):
+        def spike(batch, end):
             tiles = live[batch]
-            both_shape = [P, 2, CELLS, NODES]
-            spikes = scratch.tile(both_shape, F32, name="spikes")
+            if end == LOW:
+                tiles["spikes"] = scratch.tile([P, 2, CELLS, NODES], F32, name="spikes")
             nc.vector.tensor_tensor(
-                out=spikes[:],
-                in0=tiles["at_extreme"][:],
-                in1=tiles["amplitude"][:].rearrange("p s c g -> p s (c g)").unsqueeze(3).to_broadcast(both_shape),
+                out=tiles["spikes"][:, end],
+                in0=tiles["at_extreme"][:, end],
+                in1=over_sources(tiles["quotients"][:, end].rearrange("p c g -> p (c g)")),
                 op=ALU.mult,
             )
-            low = spikes[:, LOW].rearrange("p (c g) j -> p c (g j)", c=PLANES)
-            high = spikes[:, HIGH].rearrange("p (c g) j -> p c (g j)", c=PLANES)
+
+        def by_plane(spikes, end):
+            return spikes[:, end].rearrange("p (c g) j -> p c (g j)", c=PLANES)
+
+        def add_linear(batch):
+            tiles = live[batch]
+            low = by_plane(tiles["spikes"], LOW)
             nc.vector.tensor_tensor(out=low, in0=low, in1=tiles["linear"][:], op=ALU.add)
-            dm_grouped = work.tile([P, PASSES, BATCH_ROWS, PACK], BF16, name="dm_grouped", align_bytes=64)
-            dm_codes = work.tile([P, PASSES, BATCH_ROWS], U32, name="dm_codes", align_bytes=64)
-            dm_scales = work.tile([P, PASSES, BATCH_ROWS], U8, name="dm_scales", align_bytes=64)
+
+        def add_high(batch):
+            tiles = live[batch]
+            tiles["dm_grouped"] = work.tile([P, PASSES, BATCH_ROWS, PACK], BF16, name="dm_grouped", align_bytes=64)
             nc.vector.tensor_tensor(
-                out=dm_grouped[:],
-                in0=low.rearrange("p (h t) r -> p h r t", t=PACK),
-                in1=high.rearrange("p (h t) r -> p h r t", t=PACK),
+                out=tiles["dm_grouped"][:],
+                in0=by_plane(tiles["spikes"], LOW).rearrange("p (h t) r -> p h r t", t=PACK),
+                in1=by_plane(tiles["spikes"], HIGH).rearrange("p (h t) r -> p h r t", t=PACK),
                 op=ALU.add,
             )
+
+        def quantise(batch):
+            dm_codes = work.tile([P, PASSES, BATCH_ROWS], U32, name="dm_codes", align_bytes=64)
+            dm_scales = work.tile([P, PASSES, BATCH_ROWS], U8, name="dm_scales", align_bytes=64)
             nc.vector.quantize_mx(
                 out=dm_codes[:].rearrange("p h r -> p (h r)").bitcast(E5M2_X4),
                 scales=dm_scales[:].rearrange("p h r -> p (h r)"),
-                in_=dm_grouped[:].rearrange("p h r t -> p (h r t)"),
+                in_=live[batch]["dm_grouped"][:].rearrange("p h r t -> p (h r t)"),
             )
             live[batch] = {"dm_codes": dm_codes, "dm_scales": dm_scales}
 
@@ -293,22 +348,41 @@ def tile_gnnlayer_pa_v_kernel(tc, x, e_enc, W_pre, b_pre, m, grad_out, out):
         def exists(batch):
             return 0 <= batch < BATCHES
 
+        load(0)
+        load_grad()
+        load(1)
+        for h in range(PASSES):
+            load_weight(h)
+
         for step in range(-3, BATCHES + 1):
-            if exists(step):
-                linear_part(step)
-            if exists(step - 1):
-                product(step - 1)
-            if exists(step + 1):
-                statistics(step + 1)
-            if exists(step):
-                assemble(step)
+            last, mid, first, new = step, step + 1, step + 2, step + 3
+            if exists(last):
+                linear_part(last)
+            if exists(last - 1):
+                product(last - 1)
+            vector_list = (
+                (mid, count, 1), (first, extreme, LOW), (mid, count, 2), (first, variance, None),
+                (first, extreme, HIGH), (mid, count, 3), (first, std_squared, None), (last, spike, LOW),
+                (mid, count, 4), (last, spike, HIGH), (mid, count, 5), (last, add_linear, None),
+                (mid, invert, None), (first, compare, LOW), (mid, divide, None), (last, add_high, None),
+                (mid, slope, None), (first, compare, HIGH), (mid, slope_mean, None), (last, quantise, None),
+                (mid, offset, None),
+            )
+            for batch, stage, argument in vector_list:
+                if exists(batch):
+                    if argument is None:
+                        stage(batch)
+                    else:
+                        stage(batch, argument)
             if step == 0:
                 quantise_weight()
-            if exists(step + 1):
-                slope_and_offset(step + 1)
-            if exists(step + 3):
-                load_and_turn(step + 3)
+            if exists(new):
+                turn(new)
+            if exists(new + 2):
+                load(new + 2)
             if step == -3:
                 prepare_grad()
             if step in (-2, -1):
                 turn_weight(step + PASSES)
+            if exists(first):
+                std_root(first)

@@ -37,6 +37,7 @@ CELLS = PLANES * BATCH_TARGETS
 KIND_MEAN, KIND_MIN, KIND_MAX, KIND_STD = 0, 1, 2, 3
 KINDS = 4
 LOW, HIGH = 0, 1
+RUN = 4
 FIRST, SECOND = 0, 1
 
 FLOPS = 2 * ROWS * FEATURES * CHANNELS
@@ -306,12 +307,14 @@ def tile_gnnlayer_pa_v_kernel(tc, x, e_enc, W_pre, b_pre, m, grad_out, out):
         def add_high(batch):
             tiles = live[batch]
             tiles["dm_grouped"] = work.tile([P, PASSES, BATCH_ROWS, PACK], BF16, name="dm_grouped", align_bytes=64)
-            nc.vector.tensor_tensor(
-                out=tiles["dm_grouped"][:],
-                in0=by_plane(tiles["spikes"], LOW).rearrange("p (h t) r -> p h r t", t=PACK),
-                in1=by_plane(tiles["spikes"], HIGH).rearrange("p (h t) r -> p h r t", t=PACK),
-                op=ALU.add,
-            )
+            for h in range(PASSES):
+                of_pass = slice(h * PACK, (h + 1) * PACK)
+                nc.vector.tensor_tensor(
+                    out=tiles["dm_grouped"][:, h].rearrange("p (c i) t -> p c t i", i=RUN),
+                    in0=by_plane(tiles["spikes"], LOW)[:, of_pass, :].rearrange("p t (c i) -> p c t i", i=RUN),
+                    in1=by_plane(tiles["spikes"], HIGH)[:, of_pass, :].rearrange("p t (c i) -> p c t i", i=RUN),
+                    op=ALU.add,
+                )
 
         def quantise(batch):
             dm_codes = work.tile([P, PASSES, BATCH_ROWS], U32, name="dm_codes", align_bytes=64)

@@ -191,24 +191,6 @@ def tile_gnnlayer_pa_v_kernel(tc, x, e_enc, W_pre, b_pre, m, grad_out, out):
                 out=tiles["extreme"][:, end, :], in_=m_cells(batch), axis=INNERMOST, op=ALU.min if end == LOW else ALU.max
             )
 
-        def variance(batch):
-            tiles = live[batch]
-            tiles["var"] = work.tile(cell_shape, F32, name="var")
-            nc.vector.tensor_tensor(
-                out=tiles["var"][:], in0=tiles["moments"][:, SECOND], in1=tiles["mean_sq"][:], op=ALU.subtract
-            )
-
-        def std_squared(batch):
-            tiles = live[batch]
-            tiles["divisors"] = work.tile([P, 3, PLANES, BATCH_TARGETS], F32, name="divisors")
-            nc.vector.tensor_scalar(
-                out=tiles["divisors"][:, 2], in0=tiles["var"][:], scalar1=0.0, scalar2=EPS_STD, op0=ALU.max, op1=ALU.add
-            )
-
-        def std_root(batch):
-            std = live[batch]["divisors"][:, 2]
-            nc.scalar.activation(out=std, in_=std, func=FUNC.Sqrt)
-
         def compare(batch, end):
             tiles = live[batch]
             if end == LOW:
@@ -220,41 +202,39 @@ def tile_gnnlayer_pa_v_kernel(tc, x, e_enc, W_pre, b_pre, m, grad_out, out):
                 op=ALU.is_equal,
             )
 
-        def count(batch, halving):
+        def variance(batch):
             tiles = live[batch]
-            width = NODES >> halving
-            if halving == 1:
-                tiles["level"] = tiles["at_extreme"][:].rearrange("p s x j -> p (s x) j")
-            level = tiles["level"]
-            if width == 1:
-                shorter = tiles["divisors"][:, 0:2].rearrange("p s c g -> p (s c g)").unsqueeze(2)
-            else:
-                counts = scratch.tile([P, 2 * CELLS, width], BF16, name="count%d" % width)
-                shorter = counts[:]
-            nc.vector.tensor_tensor(out=shorter, in0=level[:, :, 0:width], in1=level[:, :, width : 2 * width], op=ALU.add)
-            tiles["level"] = shorter
-
-        def invert(batch):
-            divisors = live[batch]["divisors"][:].rearrange("p s c g -> p (s c g)")
-            nc.vector.reciprocal(out=divisors, in_=divisors)
-
-        def divide(batch):
-            tiles = live[batch]
-            tiles["quotients"] = work.tile([P, 3, PLANES, BATCH_TARGETS], F32, name="quotients")
+            tiles["var"] = work.tile(cell_shape, F32, name="var")
             nc.vector.tensor_tensor(
-                out=tiles["quotients"][:],
-                in0=grad_t[:, KIND_MIN : KIND_STD + 1, :, targets_of(batch)],
-                in1=tiles["divisors"][:],
-                op=ALU.mult,
+                out=tiles["var"][:], in0=tiles["moments"][:, SECOND], in1=tiles["mean_sq"][:], op=ALU.subtract
             )
+
+        def std_squared(batch):
+            tiles = live[batch]
+            tiles["std"] = work.tile(cell_shape, F32, name="std")
+            nc.vector.tensor_scalar(
+                out=tiles["std"][:], in0=tiles["var"][:], scalar1=0.0, scalar2=EPS_STD, op0=ALU.max, op1=ALU.add
+            )
+
+        def std_root(batch):
+            std = live[batch]["std"]
+            nc.scalar.activation(out=std[:], in_=std[:], func=FUNC.Sqrt)
+
+        def masked_grad(batch):
+            tiles = live[batch]
+            tiles["slope"] = three.tile(cell_shape, F32, name="slope")
+            nc.vector.scalar_tensor_tensor(
+                out=tiles["slope"][:], in0=tiles["var"][:], scalar=0.0, in1=grad_t[:, KIND_STD, :, targets_of(batch)],
+                op0=ALU.is_gt, op1=ALU.mult,
+            )
+
+        def invert_std(batch):
+            std = live[batch]["std"]
+            nc.vector.reciprocal(out=std[:], in_=std[:])
 
         def slope(batch):
             tiles = live[batch]
-            tiles["slope"] = work.tile(cell_shape, F32, name="slope")
-            nc.vector.scalar_tensor_tensor(
-                out=tiles["slope"][:], in0=tiles["var"][:], scalar=0.0, in1=tiles["quotients"][:, 2],
-                op0=ALU.is_gt, op1=ALU.mult,
-            )
+            nc.vector.tensor_tensor(out=tiles["slope"][:], in0=tiles["slope"][:], in1=tiles["std"][:], op=ALU.mult)
 
         def slope_mean(batch):
             tiles = live[batch]
@@ -268,6 +248,32 @@ def tile_gnnlayer_pa_v_kernel(tc, x, e_enc, W_pre, b_pre, m, grad_out, out):
             nc.vector.tensor_tensor(
                 out=tiles["offset"][:], in0=grad_t[:, KIND_MEAN, :, targets_of(batch)], in1=tiles["offset"][:],
                 op=ALU.subtract,
+            )
+
+        def count(batch, halving):
+            tiles = live[batch]
+            width = NODES >> halving
+            if halving == 1:
+                tiles["level"] = tiles["at_extreme"][:].rearrange("p s x j -> p (s x) j")
+            level = tiles["level"]
+            counts = scratch.tile([P, 2 * CELLS, width], F32 if width == 1 else BF16, name="count%d" % width)
+            nc.vector.tensor_tensor(out=counts[:], in0=level[:, :, 0:width], in1=level[:, :, width : 2 * width], op=ALU.add)
+            tiles["level"] = counts[:]
+
+        def invert_counts(batch):
+            tiles = live[batch]
+            tiles["amplitude"] = work.tile([P, 2, PLANES, BATCH_TARGETS], F32, name="amplitude")
+            nc.vector.reciprocal(
+                out=tiles["amplitude"][:].rearrange("p s c g -> p (s c g)"), in_=tiles["level"].rearrange("p x o -> p (x o)")
+            )
+
+        def divide(batch):
+            tiles = live[batch]
+            nc.vector.tensor_tensor(
+                out=tiles["amplitude"][:],
+                in0=grad_t[:, KIND_MIN : KIND_MAX + 1, :, targets_of(batch)],
+                in1=tiles["amplitude"][:],
+                op=ALU.mult,
             )
 
         def linear_part(batch):
@@ -292,7 +298,7 @@ def tile_gnnlayer_pa_v_kernel(tc, x, e_enc, W_pre, b_pre, m, grad_out, out):
             nc.vector.tensor_tensor(
                 out=tiles["spikes"][:, end],
                 in0=tiles["at_extreme"][:, end],
-                in1=over_sources(tiles["quotients"][:, end].rearrange("p c g -> p (c g)")),
+                in1=over_sources(tiles["amplitude"][:, end].rearrange("p c g -> p (c g)")),
                 op=ALU.mult,
             )
 
@@ -302,7 +308,7 @@ def tile_gnnlayer_pa_v_kernel(tc, x, e_enc, W_pre, b_pre, m, grad_out, out):
         def add_linear(batch):
             tiles = live[batch]
             low = by_plane(tiles["spikes"], LOW)
-            nc.vector.tensor_tensor(out=low, in0=low, in1=tiles["linear"][:], op=ALU.add)
+            nc.gpsimd.tensor_tensor(out=low, in0=low, in1=tiles["linear"][:], op=ALU.add)
 
         def add_high(batch):
             tiles = live[batch]
@@ -359,17 +365,15 @@ def tile_gnnlayer_pa_v_kernel(tc, x, e_enc, W_pre, b_pre, m, grad_out, out):
 
         for step in range(-3, BATCHES + 1):
             last, mid, first, new = step, step + 1, step + 2, step + 3
-            if exists(last):
-                linear_part(last)
             if exists(last - 1):
                 product(last - 1)
             vector_list = (
-                (mid, count, 1), (first, extreme, LOW), (mid, count, 2), (first, variance, None),
-                (first, extreme, HIGH), (mid, count, 3), (first, std_squared, None), (last, spike, LOW),
-                (mid, count, 4), (last, spike, HIGH), (mid, count, 5), (last, add_linear, None),
-                (mid, invert, None), (first, compare, LOW), (mid, divide, None), (last, add_high, None),
-                (mid, slope, None), (first, compare, HIGH), (mid, slope_mean, None), (last, quantise, None),
-                (mid, offset, None),
+                (last, spike, LOW), (last, add_linear, None), (first, extreme, LOW), (first, extreme, HIGH),
+                (mid, count, 2), (mid, invert_std, None), (last, spike, HIGH), (mid, count, 3), (mid, slope, None),
+                (first, compare, LOW), (mid, count, 4), (mid, slope_mean, None), (last, add_high, None),
+                (mid, count, 5), (mid, offset, None), (first, compare, HIGH), (mid, invert_counts, None),
+                (first, variance, None), (last, quantise, None), (mid, divide, None), (first, std_squared, None),
+                (first, count, 1), (first, masked_grad, None),
             )
             for batch, stage, argument in vector_list:
                 if exists(batch):
@@ -389,3 +393,5 @@ def tile_gnnlayer_pa_v_kernel(tc, x, e_enc, W_pre, b_pre, m, grad_out, out):
                 turn_weight(step + PASSES)
             if exists(first):
                 std_root(first)
+            if exists(mid):
+                linear_part(mid)

@@ -367,15 +367,14 @@ def tile_gnnlayer_pa_v_kernel(tc, x, e_enc, W_pre, b_pre, m, grad_out, out):
             last, mid, first, new = step, step + 1, step + 2, step + 3
             if exists(last - 1):
                 product(last - 1)
-            vector_list = (
+            for batch, stage, argument in (
                 (last, spike, LOW), (last, add_linear, None), (first, extreme, LOW), (first, extreme, HIGH),
-                (mid, count, 2), (mid, invert_std, None), (last, spike, HIGH), (mid, count, 3), (mid, slope, None),
-                (first, compare, LOW), (mid, count, 4), (mid, slope_mean, None), (last, add_high, None),
-                (mid, count, 5), (mid, offset, None), (first, compare, HIGH), (mid, invert_counts, None),
-                (first, variance, None), (last, quantise, None), (mid, divide, None), (first, std_squared, None),
-                (first, count, 1), (first, masked_grad, None),
-            )
-            for batch, stage, argument in vector_list:
+                (first, variance, None), (mid, count, 2), (last, spike, HIGH), (first, std_squared, None),
+                (first, std_root, None), (mid, count, 3), (first, compare, LOW), (first, masked_grad, None),
+                (mid, count, 4), (last, add_high, None), (mid, count, 5), (first, invert_std, None),
+                (first, compare, HIGH), (mid, invert_counts, None), (first, slope, None), (last, quantise, None),
+                (mid, divide, None), (first, slope_mean, None), (first, count, 1), (first, offset, None),
+            ):
                 if exists(batch):
                     if argument is None:
                         stage(batch)
@@ -383,6 +382,8 @@ def tile_gnnlayer_pa_v_kernel(tc, x, e_enc, W_pre, b_pre, m, grad_out, out):
                         stage(batch, argument)
             if step == 0:
                 quantise_weight()
+            if exists(mid):
+                linear_part(mid)
             if exists(new):
                 turn(new)
             if exists(new + 2):
@@ -391,7 +392,3 @@ def tile_gnnlayer_pa_v_kernel(tc, x, e_enc, W_pre, b_pre, m, grad_out, out):
                 prepare_grad()
             if step in (-2, -1):
                 turn_weight(step + PASSES)
-            if exists(first):
-                std_root(first)
-            if exists(mid):
-                linear_part(mid)

@@ -37,7 +37,7 @@ CELLS = PLANES * BATCH_TARGETS
 KIND_MEAN, KIND_MIN, KIND_MAX, KIND_STD = 0, 1, 2, 3
 KINDS = 4
 LOW, HIGH = 0, 1
-RUN = 4
+SCALAR_CELLS = 5 * BATCH_TARGETS
 FIRST, SECOND = 0, 1
 
 FLOPS = 2 * ROWS * FEATURES * CHANNELS
@@ -174,11 +174,15 @@ def tile_gnnlayer_pa_v_kernel(tc, x, e_enc, W_pre, b_pre, m, grad_out, out):
                             start=True,
                             stop=True,
                         )
-            moments = three.tile([P, 2, PLANES, BATCH_TARGETS], F32, name="moments")
-            nc.scalar.mul(out=moments[:], in_=sums[:], mul=1.0 / NODES)
-            mean_sq = work.tile(cell_shape, F32, name="mean_sq")
-            nc.scalar.activation(out=mean_sq[:], in_=sums[:, FIRST], func=FUNC.Square, scale=1.0 / NODES)
-            live[batch] = {"m_t": m_t, "moments": moments, "mean_sq": mean_sq}
+            live[batch] = {"m_t": m_t, "sums": sums}
+
+        def means(batch):
+            tiles = live[batch]
+            sums = tiles["sums"]
+            tiles["moments"] = three.tile([P, 2, PLANES, BATCH_TARGETS], F32, name="moments")
+            nc.scalar.mul(out=tiles["moments"][:], in_=sums[:], mul=1.0 / NODES)
+            tiles["mean_sq"] = work.tile(cell_shape, F32, name="mean_sq")
+            nc.scalar.activation(out=tiles["mean_sq"][:], in_=sums[:, FIRST], func=FUNC.Square, scale=1.0 / NODES)
 
         def m_cells(batch):
             return live[batch]["m_t"][:].rearrange("p c (g j) -> p (c g) j", j=NODES)
@@ -209,16 +213,11 @@ def tile_gnnlayer_pa_v_kernel(tc, x, e_enc, W_pre, b_pre, m, grad_out, out):
                 out=tiles["var"][:], in0=tiles["moments"][:, SECOND], in1=tiles["mean_sq"][:], op=ALU.subtract
             )
 
-        def std_squared(batch):
+        def inverse_std(batch):
             tiles = live[batch]
             tiles["std"] = work.tile(cell_shape, F32, name="std")
-            nc.vector.tensor_scalar(
-                out=tiles["std"][:], in0=tiles["var"][:], scalar1=0.0, scalar2=EPS_STD, op0=ALU.max, op1=ALU.add
-            )
-
-        def std_root(batch):
-            std = live[batch]["std"]
-            nc.scalar.activation(out=std[:], in_=std[:], func=FUNC.Sqrt)
+            nc.scalar.activation(out=tiles["std"][:], in_=tiles["var"][:], func=FUNC.Relu)
+            nc.scalar.activation(out=tiles["std"][:], in_=tiles["std"][:], func=FUNC.Abs_reciprocal_sqrt, bias=EPS_STD)
 
         def masked_grad(batch):
             tiles = live[batch]
@@ -227,10 +226,6 @@ def tile_gnnlayer_pa_v_kernel(tc, x, e_enc, W_pre, b_pre, m, grad_out, out):
                 out=tiles["slope"][:], in0=tiles["var"][:], scalar=0.0, in1=grad_t[:, KIND_STD, :, targets_of(batch)],
                 op0=ALU.is_gt, op1=ALU.mult,
             )
-
-        def invert_std(batch):
-            std = live[batch]["std"]
-            nc.vector.reciprocal(out=std[:], in_=std[:])
 
         def slope(batch):
             tiles = live[batch]
@@ -291,14 +286,26 @@ def tile_gnnlayer_pa_v_kernel(tc, x, e_enc, W_pre, b_pre, m, grad_out, out):
                     )
             tiles["linear"] = linear
 
+        def scalar_spikes(batch):
+            tiles = live[batch]
+            tiles["spikes"] = scratch.tile([P, 2, CELLS, NODES], F32, name="spikes")
+            for cell in range(SCALAR_CELLS):
+                nc.scalar.activation(
+                    out=tiles["spikes"][:, HIGH, cell, :],
+                    in_=tiles["at_extreme"][:, HIGH, cell, :],
+                    func=FUNC.Copy,
+                    scale=tiles["amplitude"][:, HIGH].rearrange("p c g -> p (c g)")[:, cell : cell + 1],
+                )
+
         def spike(batch, end):
             tiles = live[batch]
-            if end == LOW:
-                tiles["spikes"] = scratch.tile([P, 2, CELLS, NODES], F32, name="spikes")
+            cells = slice(SCALAR_CELLS if end == HIGH else 0, CELLS)
             nc.vector.tensor_tensor(
-                out=tiles["spikes"][:, end],
-                in0=tiles["at_extreme"][:, end],
-                in1=over_sources(tiles["amplitude"][:, end].rearrange("p c g -> p (c g)")),
+                out=tiles["spikes"][:, end, cells, :],
+                in0=tiles["at_extreme"][:, end, cells, :],
+                in1=tiles["amplitude"][:, end].rearrange("p c g -> p (c g)")[:, cells].unsqueeze(2).to_broadcast(
+                    [P, CELLS - cells.start, NODES]
+                ),
                 op=ALU.mult,
             )
 
@@ -313,14 +320,12 @@ def tile_gnnlayer_pa_v_kernel(tc, x, e_enc, W_pre, b_pre, m, grad_out, out):
         def add_high(batch):
             tiles = live[batch]
             tiles["dm_grouped"] = work.tile([P, PASSES, BATCH_ROWS, PACK], BF16, name="dm_grouped", align_bytes=64)
-            for h in range(PASSES):
-                of_pass = slice(h * PACK, (h + 1) * PACK)
-                nc.vector.tensor_tensor(
-                    out=tiles["dm_grouped"][:, h].rearrange("p (c i) t -> p c t i", i=RUN),
-                    in0=by_plane(tiles["spikes"], LOW)[:, of_pass, :].rearrange("p t (c i) -> p c t i", i=RUN),
-                    in1=by_plane(tiles["spikes"], HIGH)[:, of_pass, :].rearrange("p t (c i) -> p c t i", i=RUN),
-                    op=ALU.add,
-                )
+            nc.vector.tensor_tensor(
+                out=tiles["dm_grouped"][:],
+                in0=by_plane(tiles["spikes"], LOW).rearrange("p (h t) r -> p h r t", t=PACK),
+                in1=by_plane(tiles["spikes"], HIGH).rearrange("p (h t) r -> p h r t", t=PACK),
+                op=ALU.add,
+            )
 
         def quantise(batch):
             dm_codes = work.tile([P, PASSES, BATCH_ROWS], U32, name="dm_codes", align_bytes=64)
@@ -365,15 +370,21 @@ def tile_gnnlayer_pa_v_kernel(tc, x, e_enc, W_pre, b_pre, m, grad_out, out):
 
         for step in range(-3, BATCHES + 1):
             last, mid, first, new = step, step + 1, step + 2, step + 3
+            if exists(last):
+                scalar_spikes(last)
             if exists(last - 1):
                 product(last - 1)
+            if exists(new):
+                turn(new)
+            if exists(new + 2):
+                load(new + 2)
             for batch, stage, argument in (
                 (last, spike, LOW), (last, add_linear, None), (first, extreme, LOW), (first, extreme, HIGH),
-                (first, variance, None), (mid, count, 2), (last, spike, HIGH), (first, std_squared, None),
-                (first, std_root, None), (mid, count, 3), (first, compare, LOW), (first, masked_grad, None),
-                (mid, count, 4), (last, add_high, None), (mid, count, 5), (first, invert_std, None),
-                (first, compare, HIGH), (mid, invert_counts, None), (first, slope, None), (last, quantise, None),
-                (mid, divide, None), (first, slope_mean, None), (first, count, 1), (first, offset, None),
+                (first, variance, None), (mid, count, 2), (last, spike, HIGH), (first, inverse_std, None),
+                (mid, count, 3), (first, compare, LOW), (first, masked_grad, None), (mid, count, 4),
+                (last, add_high, None), (mid, count, 5), (first, compare, HIGH), (mid, invert_counts, None),
+                (first, slope, None), (last, quantise, None), (mid, divide, None), (first, slope_mean, None),
+                (first, count, 1), (first, offset, None),
             ):
                 if exists(batch):
                     if argument is None:
@@ -385,9 +396,7 @@ def tile_gnnlayer_pa_v_kernel(tc, x, e_enc, W_pre, b_pre, m, grad_out, out):
             if exists(mid):
                 linear_part(mid)
             if exists(new):
-                turn(new)
-            if exists(new + 2):
-                load(new + 2)
+                means(new)
             if step == -3:
                 prepare_grad()
             if step in (-2, -1):

@@ -37,8 +37,7 @@ CELLS = PLANES * BATCH_TARGETS
 KIND_MEAN, KIND_MIN, KIND_MAX, KIND_STD = 0, 1, 2, 3
 KINDS = 4
 LOW, HIGH = 0, 1
-SCALAR_CELLS = 5 * BATCH_TARGETS
-FIRST, SECOND = 0, 1
+GPSIMD_CELLS = 2 * BATCH_TARGETS
 
 FLOPS = 2 * ROWS * FEATURES * CHANNELS
 BYTES = 4 * ROWS * FEATURES + 2 * TARGETS * KINDS * FEATURES + 2 * CHANNELS * FEATURES + 4 * ROWS * CHANNELS
@@ -150,7 +149,7 @@ def tile_gnnlayer_pa_v_kernel(tc, x, e_enc, W_pre, b_pre, m, grad_out, out):
         def turn(batch):
             tiles = live[batch]
             m_t = planes.tile([P, PLANES, BATCH_ROWS], F32, name="m_t")
-            sums = psum_sums.tile([P, 2, PLANES, BATCH_TARGETS], F32, name="sums")
+            sums = psum_sums.tile(cell_shape, F32, name="sums")
             m_sq = []
             for a in range(BATCH_TILES):
                 squares = work.tile([P, FEATURES], F32, name="m_sq")
@@ -164,25 +163,21 @@ def tile_gnnlayer_pa_v_kernel(tc, x, e_enc, W_pre, b_pre, m, grad_out, out):
                         col0 = (h * PACK + t) * P
                         nc.tensor.transpose(turned[:, t, :], m_nat[:, col0 : col0 + P], ident_f32[:])
                     nc.scalar.copy(out=m_t[:, h * PACK : (h + 1) * PACK, a * P : (a + 1) * P], in_=turned[:])
-            for moment, rows in ((FIRST, tiles["m_nat"]), (SECOND, m_sq)):
-                for a in range(BATCH_TILES):
-                    for plane in range(PLANES):
-                        nc.tensor.matmul(
-                            out=sums[:, moment, plane, a * TILE_TARGETS : (a + 1) * TILE_TARGETS],
-                            lhsT=rows[a][:, plane * P : (plane + 1) * P],
-                            rhs=target_of_row[:],
-                            start=True,
-                            stop=True,
-                        )
+            for a in range(BATCH_TILES):
+                for plane in range(PLANES):
+                    nc.tensor.matmul(
+                        out=sums[:, plane, a * TILE_TARGETS : (a + 1) * TILE_TARGETS],
+                        lhsT=m_sq[a][:, plane * P : (plane + 1) * P],
+                        rhs=target_of_row[:],
+                        start=True,
+                        stop=True,
+                    )
             live[batch] = {"m_t": m_t, "sums": sums}
 
-        def means(batch):
+        def square_mean(batch):
             tiles = live[batch]
-            sums = tiles["sums"]
-            tiles["moments"] = three.tile([P, 2, PLANES, BATCH_TARGETS], F32, name="moments")
-            nc.scalar.mul(out=tiles["moments"][:], in_=sums[:], mul=1.0 / NODES)
-            tiles["mean_sq"] = work.tile(cell_shape, F32, name="mean_sq")
-            nc.scalar.activation(out=tiles["mean_sq"][:], in_=sums[:, FIRST], func=FUNC.Square, scale=1.0 / NODES)
+            tiles["square_mean"] = three.tile(cell_shape, F32, name="square_mean")
+            nc.scalar.mul(out=tiles["square_mean"][:], in_=tiles["sums"][:], mul=1.0 / NODES)
 
         def m_cells(batch):
             return live[batch]["m_t"][:].rearrange("p c (g j) -> p (c g) j", j=NODES)
@@ -195,14 +190,26 @@ def tile_gnnlayer_pa_v_kernel(tc, x, e_enc, W_pre, b_pre, m, grad_out, out):
                 out=tiles["extreme"][:, end, :], in_=m_cells(batch), axis=INNERMOST, op=ALU.min if end == LOW else ALU.max
             )
 
-        def compare(batch, end):
+        def total(batch):
             tiles = live[batch]
-            if end == LOW:
-                tiles["at_extreme"] = three.tile([P, 2, CELLS, NODES], BF16, name="at_extreme")
+            tiles["total"] = work.tile(cell_shape, F32, name="total")
+            nc.vector.tensor_reduce(
+                out=tiles["total"][:].rearrange("p c g -> p (c g)"), in_=m_cells(batch), axis=INNERMOST, op=ALU.add
+            )
+
+        def mean_squared(batch):
+            tiles = live[batch]
+            tiles["mean_sq"] = work.tile(cell_shape, F32, name="mean_sq")
+            nc.scalar.activation(out=tiles["mean_sq"][:], in_=tiles["total"][:], func=FUNC.Square, scale=1.0 / NODES)
+
+        def compare(batch):
+            tiles = live[batch]
+            both_shape = [P, 2, CELLS, NODES]
+            tiles["at_extreme"] = three.tile(both_shape, BF16, name="at_extreme")
             nc.vector.tensor_tensor(
-                out=tiles["at_extreme"][:, end],
-                in0=m_cells(batch),
-                in1=over_sources(tiles["extreme"][:, end, :]),
+                out=tiles["at_extreme"][:],
+                in0=m_cells(batch).unsqueeze(1).to_broadcast(both_shape),
+                in1=tiles["extreme"][:].unsqueeze(3).to_broadcast(both_shape),
                 op=ALU.is_equal,
             )
 
@@ -210,7 +217,7 @@ def tile_gnnlayer_pa_v_kernel(tc, x, e_enc, W_pre, b_pre, m, grad_out, out):
             tiles = live[batch]
             tiles["var"] = work.tile(cell_shape, F32, name="var")
             nc.vector.tensor_tensor(
-                out=tiles["var"][:], in0=tiles["moments"][:, SECOND], in1=tiles["mean_sq"][:], op=ALU.subtract
+                out=tiles["var"][:], in0=tiles["square_mean"][:], in1=tiles["mean_sq"][:], op=ALU.subtract
             )
 
         def inverse_std(batch):
@@ -234,8 +241,9 @@ def tile_gnnlayer_pa_v_kernel(tc, x, e_enc, W_pre, b_pre, m, grad_out, out):
         def slope_mean(batch):
             tiles = live[batch]
             tiles["offset"] = work.tile(cell_shape, F32, name="offset")
-            nc.vector.tensor_tensor(
-                out=tiles["offset"][:], in0=tiles["moments"][:, FIRST], in1=tiles["slope"][:], op=ALU.mult
+            nc.vector.scalar_tensor_tensor(
+                out=tiles["offset"][:], in0=tiles["total"][:], scalar=1.0 / NODES, in1=tiles["slope"][:],
+                op0=ALU.mult, op1=ALU.mult,
             )
 
         def offset(batch):
@@ -245,22 +253,24 @@ def tile_gnnlayer_pa_v_kernel(tc, x, e_enc, W_pre, b_pre, m, grad_out, out):
                 op=ALU.subtract,
             )
 
-        def count(batch, halving):
+        def count_halves(batch):
             tiles = live[batch]
-            width = NODES >> halving
-            if halving == 1:
-                tiles["level"] = tiles["at_extreme"][:].rearrange("p s x j -> p (s x) j")
-            level = tiles["level"]
-            counts = scratch.tile([P, 2 * CELLS, width], F32 if width == 1 else BF16, name="count%d" % width)
-            nc.vector.tensor_tensor(out=counts[:], in0=level[:, :, 0:width], in1=level[:, :, width : 2 * width], op=ALU.add)
-            tiles["level"] = counts[:]
+            both = tiles["at_extreme"][:].rearrange("p s x j -> p (s x) j")
+            tiles["halves"] = scratch.tile([P, 2 * CELLS, NODES // 2], BF16, name="halves")
+            nc.vector.tensor_tensor(
+                out=tiles["halves"][:], in0=both[:, :, 0 : NODES // 2], in1=both[:, :, NODES // 2 : NODES], op=ALU.add
+            )
 
-        def invert_counts(batch):
+        def count(batch):
             tiles = live[batch]
             tiles["amplitude"] = work.tile([P, 2, PLANES, BATCH_TARGETS], F32, name="amplitude")
-            nc.vector.reciprocal(
-                out=tiles["amplitude"][:].rearrange("p s c g -> p (s c g)"), in_=tiles["level"].rearrange("p x o -> p (x o)")
+            nc.vector.tensor_reduce(
+                out=tiles["amplitude"][:].rearrange("p s c g -> p (s c g)"), in_=tiles["halves"][:], axis=INNERMOST, op=ALU.add
             )
+
+        def invert_counts(batch):
+            amplitude = live[batch]["amplitude"]
+            nc.vector.reciprocal(out=amplitude[:], in_=amplitude[:])
 
         def divide(batch):
             tiles = live[batch]
@@ -271,51 +281,61 @@ def tile_gnnlayer_pa_v_kernel(tc, x, e_enc, W_pre, b_pre, m, grad_out, out):
                 op=ALU.mult,
             )
 
-        def linear_part(batch):
+        def linear_part(batch, h):
             tiles = live[batch]
-            linear = work.tile([P, PLANES, BATCH_ROWS], F32, name="linear")
-            for plane in range(PLANES):
+            if h == 0:
+                tiles["linear"] = work.tile([P, PLANES, BATCH_ROWS], F32, name="linear")
+            for plane in range(h * PACK, (h + 1) * PACK):
                 for g in range(BATCH_TARGETS):
                     sources = slice(g * NODES, (g + 1) * NODES)
                     nc.scalar.activation(
-                        out=linear[:, plane, sources],
+                        out=tiles["linear"][:, plane, sources],
                         in_=tiles["m_t"][:, plane, sources],
                         func=FUNC.Identity,
                         scale=tiles["slope"][:, plane, g : g + 1],
                         bias=tiles["offset"][:, plane, g : g + 1],
                     )
-            tiles["linear"] = linear
+
+        def amplitude_of(batch, end, cells):
+            return live[batch]["amplitude"][:, end].rearrange("p c g -> p (c g)")[:, cells]
 
         def scalar_spikes(batch):
             tiles = live[batch]
             tiles["spikes"] = scratch.tile([P, 2, CELLS, NODES], F32, name="spikes")
-            for cell in range(SCALAR_CELLS):
+            for cell in range(GPSIMD_CELLS, CELLS):
                 nc.scalar.activation(
                     out=tiles["spikes"][:, HIGH, cell, :],
                     in_=tiles["at_extreme"][:, HIGH, cell, :],
                     func=FUNC.Copy,
-                    scale=tiles["amplitude"][:, HIGH].rearrange("p c g -> p (c g)")[:, cell : cell + 1],
+                    scale=amplitude_of(batch, HIGH, slice(cell, cell + 1)),
                 )
 
-        def spike(batch, end):
+        def long_spikes(engine, batch, end, cells):
             tiles = live[batch]
-            cells = slice(SCALAR_CELLS if end == HIGH else 0, CELLS)
-            nc.vector.tensor_tensor(
+            engine.tensor_tensor(
                 out=tiles["spikes"][:, end, cells, :],
                 in0=tiles["at_extreme"][:, end, cells, :],
-                in1=tiles["amplitude"][:, end].rearrange("p c g -> p (c g)")[:, cells].unsqueeze(2).to_broadcast(
-                    [P, CELLS - cells.start, NODES]
-                ),
+                in1=amplitude_of(batch, end, cells).unsqueeze(2).to_broadcast([P, cells.stop - cells.start, NODES]),
                 op=ALU.mult,
             )
+
+        def vector_spikes(batch):
+            long_spikes(nc.vector, batch, LOW, slice(CELLS // 2, CELLS))
 
         def by_plane(spikes, end):
             return spikes[:, end].rearrange("p (c g) j -> p c (g j)", c=PLANES)
 
-        def add_linear(batch):
+        def add_linear(batch, h):
             tiles = live[batch]
-            low = by_plane(tiles["spikes"], LOW)
-            nc.gpsimd.tensor_tensor(out=low, in0=low, in1=tiles["linear"][:], op=ALU.add)
+            of_pass = slice(h * PACK, (h + 1) * PACK)
+            low = by_plane(tiles["spikes"], LOW)[:, of_pass, :]
+            nc.gpsimd.tensor_tensor(out=low, in0=low, in1=tiles["linear"][:, of_pass, :], op=ALU.add)
+
+        def gpsimd_share(batch):
+            add_linear(batch, 1)
+            long_spikes(nc.gpsimd, batch, LOW, slice(0, CELLS // 2))
+            add_linear(batch, 0)
+            long_spikes(nc.gpsimd, batch, HIGH, slice(0, GPSIMD_CELLS))
 
         def add_high(batch):
             tiles = live[batch]
@@ -379,12 +399,13 @@ def tile_gnnlayer_pa_v_kernel(tc, x, e_enc, W_pre, b_pre, m, grad_out, out):
             if exists(new + 2):
                 load(new + 2)
             for batch, stage, argument in (
-                (last, spike, LOW), (last, add_linear, None), (first, extreme, LOW), (first, extreme, HIGH),
-                (first, variance, None), (mid, count, 2), (last, spike, HIGH), (first, inverse_std, None),
-                (mid, count, 3), (first, compare, LOW), (first, masked_grad, None), (mid, count, 4),
-                (last, add_high, None), (mid, count, 5), (first, compare, HIGH), (mid, invert_counts, None),
-                (first, slope, None), (last, quantise, None), (mid, divide, None), (first, slope_mean, None),
-                (first, count, 1), (first, offset, None),
+                (last, vector_spikes, None), (last, gpsimd_share, None),
+                (first, extreme, LOW), (first, extreme, HIGH), (first, total, None), (mid, count, None),
+                (first, mean_squared, None), (mid, linear_part, 0),
+                (mid, invert_counts, None), (first, compare, None), (first, variance, None),
+                (first, inverse_std, None), (mid, linear_part, 1),
+                (last, add_high, None), (first, masked_grad, None), (last, quantise, None), (first, slope, None),
+                (first, count_halves, None), (first, slope_mean, None), (mid, divide, None), (first, offset, None),
             ):
                 if exists(batch):
                     if argument is None:
@@ -393,10 +414,8 @@ def tile_gnnlayer_pa_v_kernel(tc, x, e_enc, W_pre, b_pre, m, grad_out, out):
                         stage(batch, argument)
             if step == 0:
                 quantise_weight()
-            if exists(mid):
-                linear_part(mid)
             if exists(new):
-                means(new)
+                square_mean(new)
             if step == -3:
                 prepare_grad()
             if step in (-2, -1):

@@ -37,7 +37,7 @@ CELLS = PLANES * BATCH_TARGETS
 KIND_MEAN, KIND_MIN, KIND_MAX, KIND_STD = 0, 1, 2, 3
 KINDS = 4
 LOW, HIGH = 0, 1
-GPSIMD_CELLS = 2 * BATCH_TARGETS
+HALVES = 2
 
 FLOPS = 2 * ROWS * FEATURES * CHANNELS
 BYTES = 4 * ROWS * FEATURES + 2 * TARGETS * KINDS * FEATURES + 2 * CHANNELS * FEATURES + 4 * ROWS * CHANNELS
@@ -63,8 +63,9 @@ def tile_gnnlayer_pa_v_kernel(tc, x, e_enc, W_pre, b_pre, m, grad_out, out):
         three = stack.enter_context(tc.tile_pool(name="three", bufs=3))
         work = stack.enter_context(tc.tile_pool(name="work", bufs=2))
         scratch = stack.enter_context(tc.tile_pool(name="scratch", bufs=1))
-        psum_turn = stack.enter_context(tc.psum_pool(name="psum_turn", bufs=4))
-        psum_sums = stack.enter_context(tc.psum_pool(name="psum_sums", bufs=2))
+        psum_turn = stack.enter_context(tc.psum_pool(name="psum_turn", bufs=3))
+        psum_count = stack.enter_context(tc.psum_pool(name="psum_count", bufs=1))
+        psum_stats = stack.enter_context(tc.psum_pool(name="psum_stats", bufs=2))
         psum_out = stack.enter_context(tc.psum_pool(name="psum_out", bufs=2))
         stack.enter_context(tc.manual_schedule())
 
@@ -72,13 +73,14 @@ def tile_gnnlayer_pa_v_kernel(tc, x, e_enc, W_pre, b_pre, m, grad_out, out):
         make_identity(nc, ident_f32[:])
         ident_bf16 = keep.tile([P, P], BF16)
         make_identity(nc, ident_bf16[:])
-        target_of_row = keep.tile([P, TILE_TARGETS], F32)
+        mean_of_pair = keep.tile([P, CELLS], F32)
         nc.vector.tensor_reduce(
-            out=target_of_row[:],
-            in_=ident_f32[:].rearrange("p (q j) -> p q j", j=NODES),
+            out=mean_of_pair[:],
+            in_=ident_f32[:].rearrange("p (c q) -> p c q", q=HALVES),
             axis=INNERMOST,
             op=ALU.add,
         )
+        nc.scalar.mul(out=mean_of_pair[:], in_=mean_of_pair[:], mul=1.0 / NODES)
 
         grad_half = KINDS * FEATURES // 2
         grad_nat = keep.tile([P, grad_half], BF16)
@@ -149,12 +151,6 @@ def tile_gnnlayer_pa_v_kernel(tc, x, e_enc, W_pre, b_pre, m, grad_out, out):
         def turn(batch):
             tiles = live[batch]
             m_t = planes.tile([P, PLANES, BATCH_ROWS], F32, name="m_t")
-            sums = psum_sums.tile(cell_shape, F32, name="sums")
-            m_sq = []
-            for a in range(BATCH_TILES):
-                squares = work.tile([P, FEATURES], F32, name="m_sq")
-                nc.scalar.activation(out=squares[:], in_=tiles["m_nat"][a][:], func=FUNC.Square)
-                m_sq.append(squares)
             for a in range(BATCH_TILES):
                 m_nat = tiles["m_nat"][a]
                 for h in range(PASSES):
@@ -163,21 +159,41 @@ def tile_gnnlayer_pa_v_kernel(tc, x, e_enc, W_pre, b_pre, m, grad_out, out):
                         col0 = (h * PACK + t) * P
                         nc.tensor.transpose(turned[:, t, :], m_nat[:, col0 : col0 + P], ident_f32[:])
                     nc.scalar.copy(out=m_t[:, h * PACK : (h + 1) * PACK, a * P : (a + 1) * P], in_=turned[:])
-            for a in range(BATCH_TILES):
-                for plane in range(PLANES):
-                    nc.tensor.matmul(
-                        out=sums[:, plane, a * TILE_TARGETS : (a + 1) * TILE_TARGETS],
-                        lhsT=m_sq[a][:, plane * P : (plane + 1) * P],
-                        rhs=target_of_row[:],
-                        start=True,
-                        stop=True,
-                    )
-            live[batch] = {"m_t": m_t, "sums": sums}
+            live[batch] = {"m_t": m_t}
 
-        def square_mean(batch):
+        def square(batch):
             tiles = live[batch]
-            tiles["square_mean"] = three.tile(cell_shape, F32, name="square_mean")
-            nc.scalar.mul(out=tiles["square_mean"][:], in_=tiles["sums"][:], mul=1.0 / NODES)
+            tiles["m_sq"] = scratch.tile([P, PLANES, BATCH_ROWS], F32, name="m_sq")
+            for h in range(PASSES):
+                of_pass = slice(h * PACK, (h + 1) * PACK)
+                nc.scalar.activation(out=tiles["m_sq"][:, of_pass], in_=tiles["m_t"][:, of_pass], func=FUNC.Square)
+
+        def add_up(out, columns):
+            count_k = columns.shape[2]
+            for k in range(count_k):
+                nc.tensor.matmul(
+                    out=out, lhsT=columns[:, :, k], rhs=ident_f32[:], is_transpose=True, start=(k == 0), stop=(k == count_k - 1)
+                )
+
+        def half_cells(values):
+            return values[:].rearrange("p c (q k) -> p (c q) k", k=NODES // HALVES)
+
+        def stats_sum(batch):
+            tiles = live[batch]
+            tiles["stats_nat"] = psum_stats.tile([P, 2 * P + 2 * CELLS], F32, name="stats")
+            for k, name in enumerate(("m_t", "m_sq")):
+                add_up(tiles["stats_nat"][:, k * P : (k + 1) * P], half_cells(tiles[name]))
+
+        def stats_back(batch):
+            tiles = live[batch]
+            nat = work.tile([P, 2 * P], F32, name="nat")
+            nc.scalar.copy(out=nat[:], in_=tiles["stats_nat"][:, 0 : 2 * P])
+            for k, name in enumerate(("mean", "square_mean")):
+                of_name = slice(2 * P + k * CELLS, 2 * P + (k + 1) * CELLS)
+                tiles[name] = tiles["stats_nat"][:, of_name].rearrange("p (c g) -> p c g", c=PLANES)
+                nc.tensor.matmul(
+                    out=tiles["stats_nat"][:, of_name], lhsT=nat[:, k * P : (k + 1) * P], rhs=mean_of_pair[:], start=True, stop=True
+                )
 
         def m_cells(batch):
             return live[batch]["m_t"][:].rearrange("p c (g j) -> p (c g) j", j=NODES)
@@ -190,22 +206,15 @@ def tile_gnnlayer_pa_v_kernel(tc, x, e_enc, W_pre, b_pre, m, grad_out, out):
                 out=tiles["extreme"][:, end, :], in_=m_cells(batch), axis=INNERMOST, op=ALU.min if end == LOW else ALU.max
             )
 
-        def total(batch):
-            tiles = live[batch]
-            tiles["total"] = work.tile(cell_shape, F32, name="total")
-            nc.vector.tensor_reduce(
-                out=tiles["total"][:].rearrange("p c g -> p (c g)"), in_=m_cells(batch), axis=INNERMOST, op=ALU.add
-            )
-
         def mean_squared(batch):
             tiles = live[batch]
             tiles["mean_sq"] = work.tile(cell_shape, F32, name="mean_sq")
-            nc.scalar.activation(out=tiles["mean_sq"][:], in_=tiles["total"][:], func=FUNC.Square, scale=1.0 / NODES)
+            nc.scalar.activation(out=tiles["mean_sq"][:], in_=tiles["mean"], func=FUNC.Square)
 
         def compare(batch):
             tiles = live[batch]
             both_shape = [P, 2, CELLS, NODES]
-            tiles["at_extreme"] = three.tile(both_shape, BF16, name="at_extreme")
+            tiles["at_extreme"] = three.tile(both_shape, F32, name="at_extreme")
             nc.vector.tensor_tensor(
                 out=tiles["at_extreme"][:],
                 in0=m_cells(batch).unsqueeze(1).to_broadcast(both_shape),
@@ -217,7 +226,7 @@ def tile_gnnlayer_pa_v_kernel(tc, x, e_enc, W_pre, b_pre, m, grad_out, out):
             tiles = live[batch]
             tiles["var"] = work.tile(cell_shape, F32, name="var")
             nc.vector.tensor_tensor(
-                out=tiles["var"][:], in0=tiles["square_mean"][:], in1=tiles["mean_sq"][:], op=ALU.subtract
+                out=tiles["var"][:], in0=tiles["square_mean"], in1=tiles["mean_sq"][:], op=ALU.subtract
             )
 
         def inverse_std(batch):
@@ -241,10 +250,7 @@ def tile_gnnlayer_pa_v_kernel(tc, x, e_enc, W_pre, b_pre, m, grad_out, out):
         def slope_mean(batch):
             tiles = live[batch]
             tiles["offset"] = work.tile(cell_shape, F32, name="offset")
-            nc.vector.scalar_tensor_tensor(
-                out=tiles["offset"][:], in0=tiles["total"][:], scalar=1.0 / NODES, in1=tiles["slope"][:],
-                op0=ALU.mult, op1=ALU.mult,
-            )
+            nc.vector.tensor_tensor(out=tiles["offset"][:], in0=tiles["mean"], in1=tiles["slope"][:], op=ALU.mult)
 
         def offset(batch):
             tiles = live[batch]
@@ -253,24 +259,23 @@ def tile_gnnlayer_pa_v_kernel(tc, x, e_enc, W_pre, b_pre, m, grad_out, out):
                 op=ALU.subtract,
             )
 
-        def count_halves(batch):
-            tiles = live[batch]
-            both = tiles["at_extreme"][:].rearrange("p s x j -> p (s x) j")
-            tiles["halves"] = scratch.tile([P, 2 * CELLS, NODES // 2], BF16, name="halves")
-            nc.vector.tensor_tensor(
-                out=tiles["halves"][:], in0=both[:, :, 0 : NODES // 2], in1=both[:, :, NODES // 2 : NODES], op=ALU.add
-            )
-
         def count(batch):
             tiles = live[batch]
-            tiles["amplitude"] = work.tile([P, 2, PLANES, BATCH_TARGETS], F32, name="amplitude")
-            nc.vector.tensor_reduce(
-                out=tiles["amplitude"][:].rearrange("p s c g -> p (s c g)"), in_=tiles["halves"][:], axis=INNERMOST, op=ALU.add
-            )
+            tiles["counts"] = psum_count.tile([P, 2, 2 * CELLS], F32, name="counts")
+            add_up(tiles["counts"][:, 0, :], tiles["at_extreme"][:].rearrange("p s x j -> p (s x) j"))
+
+        def count_back(batch):
+            tiles = live[batch]
+            counts_nat = work.tile([P, P], F32, name="counts_nat")
+            nc.scalar.copy(out=counts_nat[:], in_=tiles["counts"][:, 0, :])
+            nc.tensor.transpose(tiles["counts"][:, 1, :], counts_nat[:], ident_f32[:])
 
         def invert_counts(batch):
-            amplitude = live[batch]["amplitude"]
-            nc.vector.reciprocal(out=amplitude[:], in_=amplitude[:])
+            tiles = live[batch]
+            tiles["amplitude"] = work.tile([P, 2, PLANES, BATCH_TARGETS], F32, name="amplitude")
+            nc.vector.reciprocal(
+                out=tiles["amplitude"][:].rearrange("p s c g -> p (s c g)"), in_=tiles["counts"][:, 1, :]
+            )
 
         def divide(batch):
             tiles = live[batch]
@@ -296,54 +301,31 @@ def tile_gnnlayer_pa_v_kernel(tc, x, e_enc, W_pre, b_pre, m, grad_out, out):
                         bias=tiles["offset"][:, plane, g : g + 1],
                     )
 
-        def amplitude_of(batch, end, cells):
-            return live[batch]["amplitude"][:, end].rearrange("p c g -> p (c g)")[:, cells]
-
-        def scalar_spikes(batch):
+        def spikes(batch, end):
             tiles = live[batch]
-            tiles["spikes"] = scratch.tile([P, 2, CELLS, NODES], F32, name="spikes")
-            for cell in range(GPSIMD_CELLS, CELLS):
-                nc.scalar.activation(
-                    out=tiles["spikes"][:, HIGH, cell, :],
-                    in_=tiles["at_extreme"][:, HIGH, cell, :],
-                    func=FUNC.Copy,
-                    scale=amplitude_of(batch, HIGH, slice(cell, cell + 1)),
-                )
-
-        def long_spikes(engine, batch, end, cells):
-            tiles = live[batch]
-            engine.tensor_tensor(
-                out=tiles["spikes"][:, end, cells, :],
-                in0=tiles["at_extreme"][:, end, cells, :],
-                in1=amplitude_of(batch, end, cells).unsqueeze(2).to_broadcast([P, cells.stop - cells.start, NODES]),
+            masks_of_end = tiles["at_extreme"][:, end]
+            nc.vector.tensor_tensor(
+                out=masks_of_end,
+                in0=masks_of_end,
+                in1=over_sources(tiles["amplitude"][:, end].rearrange("p c g -> p (c g)")),
                 op=ALU.mult,
             )
 
-        def vector_spikes(batch):
-            long_spikes(nc.vector, batch, LOW, slice(CELLS // 2, CELLS))
-
-        def by_plane(spikes, end):
-            return spikes[:, end].rearrange("p (c g) j -> p c (g j)", c=PLANES)
+        def by_plane(batch, end):
+            return live[batch]["at_extreme"][:, end].rearrange("p (c g) j -> p c (g j)", c=PLANES)
 
         def add_linear(batch, h):
-            tiles = live[batch]
             of_pass = slice(h * PACK, (h + 1) * PACK)
-            low = by_plane(tiles["spikes"], LOW)[:, of_pass, :]
-            nc.gpsimd.tensor_tensor(out=low, in0=low, in1=tiles["linear"][:, of_pass, :], op=ALU.add)
-
-        def gpsimd_share(batch):
-            add_linear(batch, 1)
-            long_spikes(nc.gpsimd, batch, LOW, slice(0, CELLS // 2))
-            add_linear(batch, 0)
-            long_spikes(nc.gpsimd, batch, HIGH, slice(0, GPSIMD_CELLS))
+            low = by_plane(batch, LOW)[:, of_pass, :]
+            nc.gpsimd.tensor_tensor(out=low, in0=low, in1=live[batch]["linear"][:, of_pass, :], op=ALU.add)
 
         def add_high(batch):
             tiles = live[batch]
             tiles["dm_grouped"] = work.tile([P, PASSES, BATCH_ROWS, PACK], BF16, name="dm_grouped", align_bytes=64)
             nc.vector.tensor_tensor(
                 out=tiles["dm_grouped"][:],
-                in0=by_plane(tiles["spikes"], LOW).rearrange("p (h t) r -> p h r t", t=PACK),
-                in1=by_plane(tiles["spikes"], HIGH).rearrange("p (h t) r -> p h r t", t=PACK),
+                in0=by_plane(batch, LOW).rearrange("p (h t) r -> p h r t", t=PACK),
+                in1=by_plane(batch, HIGH).rearrange("p (h t) r -> p h r t", t=PACK),
                 op=ALU.add,
             )
 
@@ -390,22 +372,17 @@ def tile_gnnlayer_pa_v_kernel(tc, x, e_enc, W_pre, b_pre, m, grad_out, out):
 
         for step in range(-3, BATCHES + 1):
             last, mid, first, new = step, step + 1, step + 2, step + 3
-            if exists(last):
-                scalar_spikes(last)
-            if exists(last - 1):
-                product(last - 1)
-            if exists(new):
-                turn(new)
-            if exists(new + 2):
-                load(new + 2)
             for batch, stage, argument in (
-                (last, vector_spikes, None), (last, gpsimd_share, None),
-                (first, extreme, LOW), (first, extreme, HIGH), (first, total, None), (mid, count, None),
-                (first, mean_squared, None), (mid, linear_part, 0),
-                (mid, invert_counts, None), (first, compare, None), (first, variance, None),
-                (first, inverse_std, None), (mid, linear_part, 1),
-                (last, add_high, None), (first, masked_grad, None), (last, quantise, None), (first, slope, None),
-                (first, count_halves, None), (first, slope_mean, None), (mid, divide, None), (first, offset, None),
+                (last, add_linear, 0), (last, add_linear, 1),
+                (mid, count_back, None), (first, mean_squared, None),
+                (new, turn, None), (new, square, None), (new + 2, load, None),
+                (last - 1, product, None), (new, stats_sum, None),
+                (first, extreme, LOW), (first, extreme, HIGH), (mid, invert_counts, None), (first, variance, None),
+                (first, compare, None), (first, inverse_std, None), (mid, divide, None), (first, masked_grad, None),
+                (mid, linear_part, 0), (new, stats_back, None), (mid, linear_part, 1),
+                (last, add_high, None), (first, slope, None), (last, quantise, None), (mid, spikes, LOW),
+                (first, slope_mean, None), (mid, spikes, HIGH), (first, offset, None),
+                (first, count, None),
             ):
                 if exists(batch):
                     if argument is None:
@@ -414,8 +391,6 @@ def tile_gnnlayer_pa_v_kernel(tc, x, e_enc, W_pre, b_pre, m, grad_out, out):
                         stage(batch, argument)
             if step == 0:
                 quantise_weight()
-            if exists(new):
-                square_mean(new)
             if step == -3:
                 prepare_grad()
             if step in (-2, -1):

@@ -184,10 +184,14 @@ def tile_gnnlayer_pa_v_kernel(tc, x, e_enc, W_pre, b_pre, m, grad_out, out):
             for k, name in enumerate(("m_t", "m_sq")):
                 add_up(tiles["stats_nat"][:, k * P : (k + 1) * P], half_cells(tiles[name]))
 
+        def stats_copy(batch):
+            tiles = live[batch]
+            tiles["nat"] = work.tile([P, 2 * P], F32, name="nat")
+            nc.scalar.copy(out=tiles["nat"][:], in_=tiles["stats_nat"][:, 0 : 2 * P])
+
         def stats_back(batch):
             tiles = live[batch]
-            nat = work.tile([P, 2 * P], F32, name="nat")
-            nc.scalar.copy(out=nat[:], in_=tiles["stats_nat"][:, 0 : 2 * P])
+            nat = tiles["nat"]
             for k, name in enumerate(("mean", "square_mean")):
                 of_name = slice(2 * P + k * CELLS, 2 * P + (k + 1) * CELLS)
                 tiles[name] = tiles["stats_nat"][:, of_name].rearrange("p (c g) -> p c g", c=PLANES)
@@ -317,7 +321,8 @@ def tile_gnnlayer_pa_v_kernel(tc, x, e_enc, W_pre, b_pre, m, grad_out, out):
         def add_linear(batch, h):
             of_pass = slice(h * PACK, (h + 1) * PACK)
             low = by_plane(batch, LOW)[:, of_pass, :]
-            nc.gpsimd.tensor_tensor(out=low, in0=low, in1=live[batch]["linear"][:, of_pass, :], op=ALU.add)
+            engine = nc.gpsimd if batch < BATCHES - 1 else nc.vector
+            engine.tensor_tensor(out=low, in0=low, in1=live[batch]["linear"][:, of_pass, :], op=ALU.add)
 
         def add_high(batch):
             tiles = live[batch]
@@ -374,15 +379,13 @@ def tile_gnnlayer_pa_v_kernel(tc, x, e_enc, W_pre, b_pre, m, grad_out, out):
             last, mid, first, new = step, step + 1, step + 2, step + 3
             for batch, stage, argument in (
                 (last, add_linear, 0), (last, add_linear, 1),
-                (mid, count_back, None), (first, mean_squared, None),
-                (new, turn, None), (new, square, None), (new + 2, load, None),
-                (last - 1, product, None), (new, stats_sum, None),
-                (first, extreme, LOW), (first, extreme, HIGH), (mid, invert_counts, None), (first, variance, None),
-                (first, compare, None), (first, inverse_std, None), (mid, divide, None), (first, masked_grad, None),
-                (mid, linear_part, 0), (new, stats_back, None), (mid, linear_part, 1),
-                (last, add_high, None), (first, slope, None), (last, quantise, None), (mid, spikes, LOW),
-                (first, slope_mean, None), (mid, spikes, HIGH), (first, offset, None),
-                (first, count, None),
+                (first, stats_back, None), (new, turn, None), (mid, count_back, None), (new, square, None), (new + 2, load, None),
+                (first, mean_squared, None), (last - 1, product, None), (new, stats_sum, None),
+                (first, extreme, LOW), (mid, offset, None), (first, extreme, HIGH),
+                (first, compare, None), (first, count, None), (mid, invert_counts, None),
+                (last, add_high, None), (mid, divide, None), (first, variance, None), (first, inverse_std, None), (last, quantise, None), (first, masked_grad, None),
+                (mid, spikes, LOW), (first, slope, None), (mid, spikes, HIGH), (first, slope_mean, None),
+                (mid, linear_part, 0), (mid, linear_part, 1), (new, stats_copy, None),
             ):
                 if exists(batch):
                     if argument is None:

@@ -67,7 +67,6 @@ def tile_gnnlayer_pa_v_kernel(tc, x, e_enc, W_pre, b_pre, m, grad_out, out):
         psum_count = stack.enter_context(tc.psum_pool(name="psum_count", bufs=1))
         psum_stats = stack.enter_context(tc.psum_pool(name="psum_stats", bufs=2))
         psum_out = stack.enter_context(tc.psum_pool(name="psum_out", bufs=2))
-        stack.enter_context(tc.manual_schedule())
 
         ident_f32 = keep.tile([P, P], F32)
         make_identity(nc, ident_f32[:])

@@ -27,24 +27,36 @@ PLANES = FEATURES // P
 N_TILE = 512
 ROWS = GRAPHS * NODES * NODES
 TARGETS = GRAPHS * NODES
-TILE_TARGETS = P // NODES
 BATCH_TILES = 2
 BATCH_ROWS = BATCH_TILES * P
-BATCH_TARGETS = BATCH_TILES * TILE_TARGETS
+BATCH_TARGETS = BATCH_ROWS // NODES
 BATCHES = ROWS // BATCH_ROWS
 CELLS = PLANES * BATCH_TARGETS
 
 KIND_MEAN, KIND_MIN, KIND_MAX, KIND_STD = 0, 1, 2, 3
 KINDS = 4
 LOW, HIGH = 0, 1
+
 HALVES = 2
+VECTOR_PLANES = 0
+TENSOR_CELLS = (PLANES - VECTOR_PLANES) * BATCH_TARGETS
+QUARTERS = P // TENSOR_CELLS
+VECTOR_TAIL = 2
+ADD_TAIL = 3
+GPSIMD_LOW = 0
 
 FLOPS = 2 * ROWS * FEATURES * CHANNELS
 BYTES = 4 * ROWS * FEATURES + 2 * TARGETS * KINDS * FEATURES + 2 * CHANNELS * FEATURES + 4 * ROWS * CHANNELS
 
+SQUARE_NAT = slice(0, P)
+SUM_NAT = slice(P, 2 * P)
+SQUARE_MEAN = slice(2 * P, 2 * P + CELLS)
+SUM = slice(2 * P + CELLS, 2 * P + CELLS + TENSOR_CELLS)
+EXTREME = slice(0, 2 * P + CELLS + TENSOR_CELLS)
+
 
 def over_sources(cell_values):
-    return cell_values.unsqueeze(2).to_broadcast([P, CELLS, NODES])
+    return cell_values.unsqueeze(2).to_broadcast([P, cell_values.shape[1], NODES])
 
 
 def tile_gnnlayer_pa_v_kernel(tc, x, e_enc, W_pre, b_pre, m, grad_out, out):
@@ -59,10 +71,10 @@ def tile_gnnlayer_pa_v_kernel(tc, x, e_enc, W_pre, b_pre, m, grad_out, out):
         keep = stack.enter_context(tc.tile_pool(name="keep", bufs=1))
         loads = stack.enter_context(tc.tile_pool(name="loads", bufs=2 * BATCH_TILES))
         stream = stack.enter_context(tc.tile_pool(name="stream", bufs=3))
-        planes = stack.enter_context(tc.tile_pool(name="planes", bufs=4))
+        planes = stack.enter_context(tc.tile_pool(name="planes", bufs=5))
         three = stack.enter_context(tc.tile_pool(name="three", bufs=3))
         work = stack.enter_context(tc.tile_pool(name="work", bufs=2))
-        scratch = stack.enter_context(tc.tile_pool(name="scratch", bufs=1))
+        squares = stack.enter_context(tc.tile_pool(name="squares", bufs=2))
         psum_turn = stack.enter_context(tc.psum_pool(name="psum_turn", bufs=3))
         psum_count = stack.enter_context(tc.psum_pool(name="psum_count", bufs=1))
         psum_stats = stack.enter_context(tc.psum_pool(name="psum_stats", bufs=2))
@@ -72,14 +84,17 @@ def tile_gnnlayer_pa_v_kernel(tc, x, e_enc, W_pre, b_pre, m, grad_out, out):
         make_identity(nc, ident_f32[:])
         ident_bf16 = keep.tile([P, P], BF16)
         make_identity(nc, ident_bf16[:])
-        mean_of_pair = keep.tile([P, CELLS], F32)
-        nc.vector.tensor_reduce(
-            out=mean_of_pair[:],
-            in_=ident_f32[:].rearrange("p (c q) -> p c q", q=HALVES),
-            axis=INNERMOST,
-            op=ALU.add,
-        )
-        nc.scalar.mul(out=mean_of_pair[:], in_=mean_of_pair[:], mul=1.0 / NODES)
+
+        def group_sums(group, name):
+            ones = keep.tile([P, P // group], F32, name=name)
+            nc.vector.tensor_reduce(
+                out=ones[:], in_=ident_f32[:].rearrange("p (c q) -> p c q", q=group), axis=INNERMOST, op=ALU.add
+            )
+            return ones
+
+        mean_of_halves = group_sums(HALVES, "mean_of_halves")
+        nc.scalar.mul(out=mean_of_halves[:], in_=mean_of_halves[:], mul=1.0 / NODES)
+        sum_of_quarters = group_sums(QUARTERS, "sum_of_quarters")
 
         grad_half = KINDS * FEATURES // 2
         grad_nat = keep.tile([P, grad_half], BF16)
@@ -100,27 +115,26 @@ def tile_gnnlayer_pa_v_kernel(tc, x, e_enc, W_pre, b_pre, m, grad_out, out):
                     in_=grad_rows[:, side * grad_half : (side + 1) * grad_half],
                 )
 
-        def prepare_grad():
-            for first in range(2):
-                turned = psum_turn.tile([P, PLANES, P], BF16, name="turned", tag="turned_m")
-                for plane in range(PLANES):
-                    col0 = (first * PLANES + plane) * P
-                    nc.tensor.transpose(turned[:, plane, :], grad_nat[:, col0 : col0 + P], ident_bf16[:])
-                for side in range(2):
-                    kind = 2 * side + first
-                    nc.scalar.activation(
-                        out=grad_t[:, kind],
-                        in_=turned[:, :, side * TARGETS : (side + 1) * TARGETS],
-                        func=FUNC.Copy,
-                        scale=1.0 / NODES if kind in (KIND_MEAN, KIND_STD) else 1.0,
-                    )
+        def prepare_grad(first):
+            turned = psum_turn.tile([P, PLANES, P], BF16, name="turned", tag="turned_m")
+            for plane in range(PLANES):
+                col0 = (first * PLANES + plane) * P
+                nc.tensor.transpose(turned[:, plane, :], grad_nat[:, col0 : col0 + P], ident_bf16[:])
+            for side in range(2):
+                kind = 2 * side + first
+                nc.scalar.activation(
+                    out=grad_t[:, kind],
+                    in_=turned[:, :, side * TARGETS : (side + 1) * TARGETS],
+                    func=FUNC.Copy,
+                    scale=1.0 / NODES if kind in (KIND_MEAN, KIND_STD) else 1.0,
+                )
 
         def load_weight(h):
             features = slice(h * K_PASS, (h + 1) * K_PASS)
             nc.sync.dma_start(out=w_nat[:, :, features], in_=w_edge[:, features].rearrange("(a p) f -> p a f", p=P))
 
-        def turn_weight(h):
-            for a in range(CHANNELS // P):
+        def turn_weight(h, tiles_a):
+            for a in tiles_a:
                 turned = psum_turn.tile([P, PACK, P], BF16, name="turned", tag="turned_m")
                 for t in range(PACK):
                     col0 = (h * PACK + t) * P
@@ -130,106 +144,114 @@ def tile_gnnlayer_pa_v_kernel(tc, x, e_enc, W_pre, b_pre, m, grad_out, out):
                     in_=turned[:].rearrange("p t c -> p c t"),
                 )
 
-        def quantise_weight():
-            for h in range(PASSES):
-                nc.vector.quantize_mx(
-                    out=w_codes[:, h, :].bitcast(E4M3_X4),
-                    scales=w_scales[:, h, :],
-                    in_=w_grouped[:, h].rearrange("p c t -> p (c t)"),
-                )
+        def quantise_weight(h):
+            nc.vector.quantize_mx(
+                out=w_codes[:, h, :].bitcast(E4M3_X4),
+                scales=w_scales[:, h, :],
+                in_=w_grouped[:, h].rearrange("p c t -> p (c t)"),
+            )
 
         def load(batch):
-            m_nat = []
+            live[batch] = {}
+            pieces = PASSES if batch == 0 else 1
             for a in range(BATCH_TILES):
                 row0 = (batch * BATCH_TILES + a) * P
                 rows = loads.tile([P, FEATURES], F32, name="m_nat")
-                nc.sync.dma_start(out=rows[:], in_=m_rows[row0 : row0 + P, :])
-                m_nat.append(rows)
-            live[batch] = {"m_nat": m_nat}
+                for piece in range(pieces):
+                    cols = slice(piece * FEATURES // pieces, (piece + 1) * FEATURES // pieces)
+                    nc.sync.dma_start(out=rows[:, cols], in_=m_rows[row0 : row0 + P, cols])
+                live[batch]["m_nat", a] = rows
 
-        def turn(batch):
+        def turn(batch, part):
             tiles = live[batch]
-            m_t = planes.tile([P, PLANES, BATCH_ROWS], F32, name="m_t")
-            for a in range(BATCH_TILES):
-                m_nat = tiles["m_nat"][a]
-                for h in range(PASSES):
-                    turned = psum_turn.tile([P, PACK, P], F32, name="turned_m")
-                    for t in range(PACK):
-                        col0 = (h * PACK + t) * P
-                        nc.tensor.transpose(turned[:, t, :], m_nat[:, col0 : col0 + P], ident_f32[:])
-                    nc.scalar.copy(out=m_t[:, h * PACK : (h + 1) * PACK, a * P : (a + 1) * P], in_=turned[:])
-            live[batch] = {"m_t": m_t}
+            a, h = divmod(part, PASSES)
+            if part == 0:
+                tiles["m_t"] = planes.tile([P, PLANES, BATCH_ROWS], F32, name="m_t")
+            turned = psum_turn.tile([P, PACK, P], F32, name="turned_m")
+            for t in range(PACK):
+                col0 = (h * PACK + t) * P
+                nc.tensor.transpose(turned[:, t, :], tiles["m_nat", a][:, col0 : col0 + P], ident_f32[:])
+            nc.scalar.copy(out=tiles["m_t"][:, h * PACK : (h + 1) * PACK, a * P : (a + 1) * P], in_=turned[:])
 
-        def square(batch):
+        def square(batch, h):
             tiles = live[batch]
-            tiles["m_sq"] = scratch.tile([P, PLANES, BATCH_ROWS], F32, name="m_sq")
-            for h in range(PASSES):
-                of_pass = slice(h * PACK, (h + 1) * PACK)
-                nc.scalar.activation(out=tiles["m_sq"][:, of_pass], in_=tiles["m_t"][:, of_pass], func=FUNC.Square)
+            if h == 0:
+                tiles["m_sq"] = squares.tile([P, PLANES, BATCH_ROWS], F32, name="m_sq")
+            of_pass = slice(h * PACK, (h + 1) * PACK)
+            nc.scalar.activation(out=tiles["m_sq"][:, of_pass], in_=tiles["m_t"][:, of_pass], func=FUNC.Square)
 
         def add_up(out, columns):
-            count_k = columns.shape[2]
-            for k in range(count_k):
+            last_k = columns.shape[2] - 1
+            for k in range(last_k + 1):
                 nc.tensor.matmul(
-                    out=out, lhsT=columns[:, :, k], rhs=ident_f32[:], is_transpose=True, start=(k == 0), stop=(k == count_k - 1)
+                    out=out, lhsT=columns[:, :, k], rhs=ident_f32[:], is_transpose=True, start=(k == 0), stop=(k == last_k)
                 )
 
-        def half_cells(values):
-            return values[:].rearrange("p c (q k) -> p (c q) k", k=NODES // HALVES)
-
-        def stats_sum(batch):
-            tiles = live[batch]
-            tiles["stats_nat"] = psum_stats.tile([P, 2 * P + 2 * CELLS], F32, name="stats")
-            for k, name in enumerate(("m_t", "m_sq")):
-                add_up(tiles["stats_nat"][:, k * P : (k + 1) * P], half_cells(tiles[name]))
-
-        def stats_copy(batch):
-            tiles = live[batch]
-            tiles["nat"] = work.tile([P, 2 * P], F32, name="nat")
-            nc.scalar.copy(out=tiles["nat"][:], in_=tiles["stats_nat"][:, 0 : 2 * P])
-
-        def stats_back(batch):
-            tiles = live[batch]
-            nat = tiles["nat"]
-            for k, name in enumerate(("mean", "square_mean")):
-                of_name = slice(2 * P + k * CELLS, 2 * P + (k + 1) * CELLS)
-                tiles[name] = tiles["stats_nat"][:, of_name].rearrange("p (c g) -> p c g", c=PLANES)
-                nc.tensor.matmul(
-                    out=tiles["stats_nat"][:, of_name], lhsT=nat[:, k * P : (k + 1) * P], rhs=mean_of_pair[:], start=True, stop=True
-                )
-
-        def m_cells(batch):
-            return live[batch]["m_t"][:].rearrange("p c (g j) -> p (c g) j", j=NODES)
+        def parts_of_cells(values, parts):
+            return values.rearrange("p c (q k) -> p (c q) k", k=NODES // parts)
 
         def extreme(batch, end):
             tiles = live[batch]
             if end == LOW:
-                tiles["extreme"] = work.tile([P, 2, CELLS], F32, name="extreme")
+                tiles["extreme"] = three.tile([P, 2, CELLS], F32, name="extreme")
             nc.vector.tensor_reduce(
-                out=tiles["extreme"][:, end, :], in_=m_cells(batch), axis=INNERMOST, op=ALU.min if end == LOW else ALU.max
+                out=tiles["extreme"][:, end, :],
+                in_=tiles["m_t"][:].rearrange("p c (g j) -> p (c g) j", j=NODES),
+                axis=INNERMOST,
+                op=ALU.min if end == LOW else ALU.max,
             )
+
+        def total(batch):
+            tiles = live[batch]
+            tiles["total"] = three.tile(cell_shape, F32, name="total")
+            if VECTOR_PLANES == 0:
+                return
+            nc.vector.tensor_reduce(
+                out=tiles["total"][:, 0:VECTOR_PLANES].rearrange("p c g -> p (c g)"),
+                in_=tiles["m_t"][:, 0:VECTOR_PLANES].rearrange("p c (g j) -> p (c g) j", j=NODES),
+                axis=INNERMOST,
+                op=ALU.add,
+            )
+
+        def show_extremes(batch):
+            tiles = live[batch]
+            tiles["stats"] = psum_stats.tile([P, EXTREME.stop], F32, name="stats")
+
+        def stats_sum(batch):
+            tiles = live[batch]
+            add_up(tiles["stats"][:, SQUARE_NAT], parts_of_cells(tiles["m_sq"][:], HALVES))
+            add_up(tiles["stats"][:, SUM_NAT], parts_of_cells(tiles["m_t"][:, VECTOR_PLANES:PLANES], QUARTERS))
+
+        def stats_copy(batch):
+            tiles = live[batch]
+            tiles["stats_nat"] = work.tile([P, 2 * P], F32, name="stats_nat")
+            nc.scalar.copy(out=tiles["stats_nat"][:], in_=tiles["stats"][:, 0 : 2 * P])
+
+        def stats_back(batch):
+            tiles = live[batch]
+            for columns, nat, groups in ((SQUARE_MEAN, SQUARE_NAT, mean_of_halves), (SUM, SUM_NAT, sum_of_quarters)):
+                nc.tensor.matmul(
+                    out=tiles["stats"][:, columns], lhsT=tiles["stats_nat"][:, nat], rhs=groups[:], start=True, stop=True
+                )
 
         def mean_squared(batch):
             tiles = live[batch]
-            tiles["mean_sq"] = work.tile(cell_shape, F32, name="mean_sq")
-            nc.scalar.activation(out=tiles["mean_sq"][:], in_=tiles["mean"], func=FUNC.Square)
-
-        def compare(batch):
-            tiles = live[batch]
-            both_shape = [P, 2, CELLS, NODES]
-            tiles["at_extreme"] = three.tile(both_shape, F32, name="at_extreme")
-            nc.vector.tensor_tensor(
-                out=tiles["at_extreme"][:],
-                in0=m_cells(batch).unsqueeze(1).to_broadcast(both_shape),
-                in1=tiles["extreme"][:].unsqueeze(3).to_broadcast(both_shape),
-                op=ALU.is_equal,
+            nc.scalar.copy(
+                out=tiles["total"][:, VECTOR_PLANES:PLANES].rearrange("p c g -> p (c g)"), in_=tiles["stats"][:, SUM]
+            )
+            tiles["mean_sq"] = work.tile([P, CELLS], F32, name="mean_sq")
+            nc.scalar.activation(
+                out=tiles["mean_sq"][:], in_=tiles["total"][:].rearrange("p c g -> p (c g)"), func=FUNC.Square, scale=1.0 / NODES
             )
 
         def variance(batch):
             tiles = live[batch]
             tiles["var"] = work.tile(cell_shape, F32, name="var")
             nc.vector.tensor_tensor(
-                out=tiles["var"][:], in0=tiles["square_mean"], in1=tiles["mean_sq"][:], op=ALU.subtract
+                out=tiles["var"][:].rearrange("p c g -> p (c g)"),
+                in0=tiles["stats"][:, SQUARE_MEAN],
+                in1=tiles["mean_sq"][:],
+                op=ALU.subtract,
             )
 
         def inverse_std(batch):
@@ -253,7 +275,10 @@ def tile_gnnlayer_pa_v_kernel(tc, x, e_enc, W_pre, b_pre, m, grad_out, out):
         def slope_mean(batch):
             tiles = live[batch]
             tiles["offset"] = work.tile(cell_shape, F32, name="offset")
-            nc.vector.tensor_tensor(out=tiles["offset"][:], in0=tiles["mean"], in1=tiles["slope"][:], op=ALU.mult)
+            nc.vector.scalar_tensor_tensor(
+                out=tiles["offset"][:], in0=tiles["total"][:], scalar=1.0 / NODES, in1=tiles["slope"][:],
+                op0=ALU.mult, op1=ALU.mult,
+            )
 
         def offset(batch):
             tiles = live[batch]
@@ -262,16 +287,30 @@ def tile_gnnlayer_pa_v_kernel(tc, x, e_enc, W_pre, b_pre, m, grad_out, out):
                 op=ALU.subtract,
             )
 
+        def compare(batch):
+            tiles = live[batch]
+            both_shape = [P, 2, CELLS, NODES]
+            tiles["at_extreme"] = three.tile(both_shape, F32, name="at_extreme")
+            nc.vector.tensor_tensor(
+                out=tiles["at_extreme"][:],
+                in0=tiles["m_t"][:].rearrange("p c (g j) -> p (c g) j", j=NODES).unsqueeze(1).to_broadcast(both_shape),
+                in1=tiles["extreme"][:].unsqueeze(3).to_broadcast(both_shape),
+                op=ALU.is_equal,
+            )
+
         def count(batch):
             tiles = live[batch]
             tiles["counts"] = psum_count.tile([P, 2, 2 * CELLS], F32, name="counts")
             add_up(tiles["counts"][:, 0, :], tiles["at_extreme"][:].rearrange("p s x j -> p (s x) j"))
 
+        def count_copy(batch):
+            tiles = live[batch]
+            tiles["counts_nat"] = work.tile([P, P], F32, name="counts_nat")
+            nc.scalar.copy(out=tiles["counts_nat"][:], in_=tiles["counts"][:, 0, :])
+
         def count_back(batch):
             tiles = live[batch]
-            counts_nat = work.tile([P, P], F32, name="counts_nat")
-            nc.scalar.copy(out=counts_nat[:], in_=tiles["counts"][:, 0, :])
-            nc.tensor.transpose(tiles["counts"][:, 1, :], counts_nat[:], ident_f32[:])
+            nc.tensor.transpose(tiles["counts"][:, 1, :], tiles["counts_nat"][:], ident_f32[:])
 
         def invert_counts(batch):
             tiles = live[batch]
@@ -280,120 +319,182 @@ def tile_gnnlayer_pa_v_kernel(tc, x, e_enc, W_pre, b_pre, m, grad_out, out):
                 out=tiles["amplitude"][:].rearrange("p s c g -> p (s c g)"), in_=tiles["counts"][:, 1, :]
             )
 
-        def divide(batch):
-            tiles = live[batch]
-            nc.vector.tensor_tensor(
-                out=tiles["amplitude"][:],
-                in0=grad_t[:, KIND_MIN : KIND_MAX + 1, :, targets_of(batch)],
-                in1=tiles["amplitude"][:],
-                op=ALU.mult,
-            )
+        def quantise_last_weight(batch):
+            if batch == 0:
+                quantise_weight(0)
+                quantise_weight(1)
 
-        def linear_part(batch, h):
+        def divide(batch, cells):
+            planes_of_cells = slice(cells.start // BATCH_TARGETS, cells.stop // BATCH_TARGETS)
+            amplitude = live[batch]["amplitude"][:].rearrange("p s c g -> p (s c) g")[:, planes_of_cells]
+            grads = grad_t[:, KIND_MIN : KIND_MAX + 1, :, targets_of(batch)].rearrange("p s c g -> p (s c) g")
+            nc.vector.tensor_tensor(out=amplitude, in0=grads[:, planes_of_cells], in1=amplitude, op=ALU.mult)
+
+        def divide_first(batch):
+            divide(batch, slice(gpsimd_cells(batch), 2 * CELLS))
+
+        def divide_last(batch):
+            if gpsimd_cells(batch) > 0:
+                divide(batch, slice(0, gpsimd_cells(batch)))
+
+        def linear_part(batch, plane):
             tiles = live[batch]
-            if h == 0:
+            if plane == 0:
                 tiles["linear"] = work.tile([P, PLANES, BATCH_ROWS], F32, name="linear")
-            for plane in range(h * PACK, (h + 1) * PACK):
-                for g in range(BATCH_TARGETS):
-                    sources = slice(g * NODES, (g + 1) * NODES)
-                    nc.scalar.activation(
-                        out=tiles["linear"][:, plane, sources],
-                        in_=tiles["m_t"][:, plane, sources],
-                        func=FUNC.Identity,
-                        scale=tiles["slope"][:, plane, g : g + 1],
-                        bias=tiles["offset"][:, plane, g : g + 1],
-                    )
+            for g in range(BATCH_TARGETS):
+                sources = slice(g * NODES, (g + 1) * NODES)
+                nc.scalar.activation(
+                    out=tiles["linear"][:, plane, sources],
+                    in_=tiles["m_t"][:, plane, sources],
+                    func=FUNC.Identity,
+                    scale=tiles["slope"][:, plane, g : g + 1],
+                    bias=tiles["offset"][:, plane, g : g + 1],
+                )
 
-        def spikes(batch, end):
+        def spikes(engine, batch, cells):
             tiles = live[batch]
-            masks_of_end = tiles["at_extreme"][:, end]
-            nc.vector.tensor_tensor(
-                out=masks_of_end,
-                in0=masks_of_end,
-                in1=over_sources(tiles["amplitude"][:, end].rearrange("p c g -> p (c g)")),
-                op=ALU.mult,
-            )
+            at_cells = tiles["at_extreme"][:].rearrange("p s x j -> p (s x) j")[:, cells]
+            amplitude = tiles["amplitude"][:].rearrange("p s c g -> p (s c g)")[:, cells]
+            engine.tensor_tensor(out=at_cells, in0=at_cells, in1=over_sources(amplitude), op=ALU.mult)
+
+        def gpsimd_cells(batch):
+            return GPSIMD_LOW if batch < BATCHES - VECTOR_TAIL else 0
+
+        def gpsimd_spikes(batch):
+            if gpsimd_cells(batch) > 0:
+                spikes(nc.gpsimd, batch, slice(0, gpsimd_cells(batch)))
+
+        def vector_spikes(batch):
+            spikes(nc.vector, batch, slice(gpsimd_cells(batch), 2 * CELLS))
 
         def by_plane(batch, end):
             return live[batch]["at_extreme"][:, end].rearrange("p (c g) j -> p c (g j)", c=PLANES)
 
-        def add_linear(batch, h):
+        def add_linear(engine, batch, h):
             of_pass = slice(h * PACK, (h + 1) * PACK)
             low = by_plane(batch, LOW)[:, of_pass, :]
-            engine = nc.gpsimd if batch < BATCHES - 1 else nc.vector
             engine.tensor_tensor(out=low, in0=low, in1=live[batch]["linear"][:, of_pass, :], op=ALU.add)
 
-        def add_high(batch):
-            tiles = live[batch]
-            tiles["dm_grouped"] = work.tile([P, PASSES, BATCH_ROWS, PACK], BF16, name="dm_grouped", align_bytes=64)
+        def gpsimd_linear(batch):
+            if batch < BATCHES - ADD_TAIL:
+                for h in range(PASSES):
+                    add_linear(nc.gpsimd, batch, h)
+
+        def vector_linear(batch):
+            if batch >= BATCHES - ADD_TAIL:
+                for h in range(PASSES):
+                    add_linear(nc.vector, batch, h)
+
+        def add_high(batch, rows):
             nc.vector.tensor_tensor(
-                out=tiles["dm_grouped"][:],
-                in0=by_plane(batch, LOW).rearrange("p (h t) r -> p h r t", t=PACK),
-                in1=by_plane(batch, HIGH).rearrange("p (h t) r -> p h r t", t=PACK),
+                out=live[batch]["dm_grouped"][:, :, rows],
+                in0=by_plane(batch, LOW)[:, :, rows].rearrange("p (h t) r -> p h r t", t=PACK),
+                in1=by_plane(batch, HIGH)[:, :, rows].rearrange("p (h t) r -> p h r t", t=PACK),
                 op=ALU.add,
             )
 
+        def assemble(batch):
+            tiles = live[batch]
+            tiles["dm_grouped"] = work.tile([P, PASSES, BATCH_ROWS, PACK], BF16, name="dm_grouped", align_bytes=64)
+            tiles["dm_codes"] = work.tile([P, PASSES, BATCH_ROWS], U32, name="dm_codes", align_bytes=64)
+            tiles["dm_scales"] = work.tile([P, PASSES, BATCH_ROWS], U8, name="dm_scales", align_bytes=64)
+            if batch < BATCHES - 1:
+                add_high(batch, slice(0, BATCH_ROWS))
+
         def quantise(batch):
-            dm_codes = work.tile([P, PASSES, BATCH_ROWS], U32, name="dm_codes", align_bytes=64)
-            dm_scales = work.tile([P, PASSES, BATCH_ROWS], U8, name="dm_scales", align_bytes=64)
-            nc.vector.quantize_mx(
-                out=dm_codes[:].rearrange("p h r -> p (h r)").bitcast(E5M2_X4),
-                scales=dm_scales[:].rearrange("p h r -> p (h r)"),
-                in_=live[batch]["dm_grouped"][:].rearrange("p h r t -> p (h r t)"),
-            )
-            live[batch] = {"dm_codes": dm_codes, "dm_scales": dm_scales}
-
-        def product(batch):
-            dm_codes, dm_scales = live[batch]["dm_codes"], live[batch]["dm_scales"]
-            for a in range(BATCH_TILES):
-                rows = slice(a * P, (a + 1) * P)
-                row0 = (batch * BATCH_TILES + a) * P
-                result = stream.tile([P, CHANNELS], F32, name="result")
-                for n in range(CHANNELS // N_TILE):
-                    cols = slice(n * N_TILE, (n + 1) * N_TILE)
-                    acc = psum_out.tile([P, N_TILE], F32, name="acc")
+            tiles = live[batch]
+            if batch < BATCHES - 1:
+                nc.vector.quantize_mx(
+                    out=tiles["dm_codes"][:].rearrange("p h r -> p (h r)").bitcast(E5M2_X4),
+                    scales=tiles["dm_scales"][:].rearrange("p h r -> p (h r)"),
+                    in_=tiles["dm_grouped"][:].rearrange("p h r t -> p (h r t)"),
+                )
+            else:
+                for a in range(BATCH_TILES):
+                    rows = slice(a * P, (a + 1) * P)
+                    add_high(batch, rows)
                     for h in range(PASSES):
-                        nc.tensor.matmul_mx(
-                            out=acc[:],
-                            lhsT=dm_codes[:, h, rows].bitcast(E5M2_X4),
-                            lhsT_scale=dm_scales[:, h, rows],
-                            rhs=w_codes[:, h, cols].bitcast(E4M3_X4),
-                            rhs_scale=w_scales[:, h, cols],
-                            start=(h == 0),
-                            stop=(h == PASSES - 1),
+                        nc.vector.quantize_mx(
+                            out=tiles["dm_codes"][:, h, rows].bitcast(E5M2_X4),
+                            scales=tiles["dm_scales"][:, h, rows],
+                            in_=tiles["dm_grouped"][:, h, rows].rearrange("p r t -> p (r t)"),
                         )
-                    nc.scalar.copy(out=result[:, cols], in_=acc[:])
-                nc.scalar.dma_start(out=out_rows[row0 : row0 + P, :], in_=result[:])
 
-        def exists(batch):
-            return 0 <= batch < BATCHES
+        def product(batch, part):
+            tiles = live[batch]
+            a, n = divmod(part, CHANNELS // N_TILE)
+            rows = slice(a * P, (a + 1) * P)
+            cols = slice(n * N_TILE, (n + 1) * N_TILE)
+            if n == 0:
+                tiles["result"] = stream.tile([P, CHANNELS], F32, name="result")
+            acc = psum_out.tile([P, N_TILE], F32, name="acc")
+            for h in range(PASSES):
+                nc.tensor.matmul_mx(
+                    out=acc[:],
+                    lhsT=tiles["dm_codes"][:, h, rows].bitcast(E5M2_X4),
+                    lhsT_scale=tiles["dm_scales"][:, h, rows],
+                    rhs=w_codes[:, h, cols].bitcast(E4M3_X4),
+                    rhs_scale=w_scales[:, h, cols],
+                    start=(h == 0),
+                    stop=(h == PASSES - 1),
+                )
+            nc.scalar.copy(out=tiles["result"][:, cols], in_=acc[:])
+            row0 = (batch * BATCH_TILES + a) * P
+            if batch == BATCHES - 1:
+                nc.sync.dma_start(out=out_rows[row0 : row0 + P, cols], in_=tiles["result"][:, cols])
+            elif cols.stop == CHANNELS:
+                nc.sync.dma_start(out=out_rows[row0 : row0 + P, :], in_=tiles["result"][:])
 
         load(0)
-        load_grad()
         load(1)
+        load_grad()
         for h in range(PASSES):
             load_weight(h)
 
-        for step in range(-3, BATCHES + 1):
-            last, mid, first, new = step, step + 1, step + 2, step + 3
-            for batch, stage, argument in (
-                (last, add_linear, 0), (last, add_linear, 1),
-                (first, stats_back, None), (new, turn, None), (mid, count_back, None), (new, square, None), (new + 2, load, None),
-                (first, mean_squared, None), (last - 1, product, None), (new, stats_sum, None),
-                (first, extreme, LOW), (mid, offset, None), (first, extreme, HIGH),
-                (first, compare, None), (first, count, None), (mid, invert_counts, None),
-                (last, add_high, None), (mid, divide, None), (first, variance, None), (first, inverse_std, None), (last, quantise, None), (first, masked_grad, None),
-                (mid, spikes, LOW), (first, slope, None), (mid, spikes, HIGH), (first, slope_mean, None),
-                (mid, linear_part, 0), (mid, linear_part, 1), (new, stats_copy, None),
-            ):
-                if exists(batch):
+        def run(stages):
+            for batch, stage, argument in stages:
+                if 0 <= batch < BATCHES:
                     if argument is None:
                         stage(batch)
                     else:
                         stage(batch, argument)
-            if step == 0:
-                quantise_weight()
+
+        for step in range(-4, 0):
+            mid, first, new, next_new = step + 1, step + 2, step + 3, step + 4
+            run((
+                (mid, count_back, None), (first, stats_back, None), (first, mean_squared, None),
+                (next_new, turn, 0), (next_new, turn, 1), (next_new, turn, 2), (next_new, turn, 3), (next_new + 2, load, None),
+                (new, extreme, LOW), (mid, slope, None), (new, extreme, HIGH), (mid, slope_mean, None), (new, total, None), (mid, offset, None),
+                (new, show_extremes, None), (new, stats_sum, None),
+                (first, compare, None), (mid, invert_counts, None), (first, variance, None), (first, inverse_std, None),
+                (next_new, square, 0), (next_new, square, 1), (new, stats_copy, None), (first, count, None), (first, count_copy, None),
+            ))
             if step == -3:
-                prepare_grad()
-            if step in (-2, -1):
-                turn_weight(step + PASSES)
+                prepare_grad(0)
+                prepare_grad(1)
+            run([(mid, linear_part, plane) for plane in range(PLANES)])
+            if step == -1:
+                turn_weight(0, range(CHANNELS // P))
+            run(((mid, divide_first, None), (first, masked_grad, None), (mid, vector_spikes, None), (mid, divide_last, None)))
+        for step in range(BATCHES + 1):
+            last, mid, first, new, next_new = step, step + 1, step + 2, step + 3, step + 4
+            run((
+                (mid, count_back, None), (first, stats_back, None), (first, mean_squared, None),
+                (next_new, turn, 0), (next_new, turn, 1), (next_new, turn, 2), (next_new, turn, 3), (next_new + 2, load, None),
+            ))
+            if step == 0:
+                turn_weight(1, range(CHANNELS // P))
+            run((
+                (new, extreme, LOW), (mid, slope, None), (new, extreme, HIGH), (mid, slope_mean, None), (new, total, None), (mid, offset, None),
+                (last, gpsimd_spikes, None), (last, gpsimd_linear, None),
+                (last - 1, product, 0), (next_new, square, 0), (last - 1, product, 1), (next_new, square, 1),
+                (last - 1, product, 2), (mid, linear_part, 0), (new, show_extremes, None), (last - 1, product, 3),
+                (new, stats_sum, None),
+                (mid, linear_part, 1), (mid, linear_part, 2), (mid, linear_part, 3), (mid, linear_part, 4),
+                (first, compare, None), (mid, invert_counts, None), (last, vector_linear, None), (first, variance, None), (first, count, None), (first, inverse_std, None),
+                (mid, linear_part, 5), (mid, linear_part, 6), (mid, linear_part, 7),
+                (new, stats_copy, None),
+                (last, assemble, None), (mid, divide_first, None), (last, quantise, None), (last, quantise_last_weight, None),
+                (first, masked_grad, None), (mid, vector_spikes, None), (mid, divide_last, None),
+            ))
+            run(((first, count_copy, None),))

from contextlib import ExitStack

import concourse.mybir as mybir
from concourse.masks import make_identity

F32 = mybir.dt.float32
BF16 = mybir.dt.bfloat16
U32 = mybir.dt.uint32
U8 = mybir.dt.uint8
E4M3_X4 = mybir.dt.float8_e4m3fn_x4
E5M2_X4 = mybir.dt.float8_e5m2_x4
ALU = mybir.AluOpType
FUNC = mybir.ActivationFunctionType
INNERMOST = mybir.AxisListType.X

GRAPHS = 2
NODES = 32
FEATURES = 1024
CHANNELS = 1024
EPS_STD = 1e-5

P = 128
PACK = 4
K_PASS = P * PACK
PASSES = FEATURES // K_PASS
PLANES = FEATURES // P
N_TILE = 512
ROWS = GRAPHS * NODES * NODES
TARGETS = GRAPHS * NODES
BATCH_TILES = 2
BATCH_ROWS = BATCH_TILES * P
BATCH_TARGETS = BATCH_ROWS // NODES
BATCHES = ROWS // BATCH_ROWS
CELLS = PLANES * BATCH_TARGETS

KIND_MEAN, KIND_MIN, KIND_MAX, KIND_STD = 0, 1, 2, 3
KINDS = 4
LOW, HIGH = 0, 1

HALVES = 2
VECTOR_PLANES = 0
TENSOR_CELLS = (PLANES - VECTOR_PLANES) * BATCH_TARGETS
QUARTERS = P // TENSOR_CELLS
VECTOR_TAIL = 2
ADD_TAIL = 3
GPSIMD_LOW = 0

FLOPS = 2 * ROWS * FEATURES * CHANNELS
BYTES = 4 * ROWS * FEATURES + 2 * TARGETS * KINDS * FEATURES + 2 * CHANNELS * FEATURES + 4 * ROWS * CHANNELS

SQUARE_NAT = slice(0, P)
SUM_NAT = slice(P, 2 * P)
SQUARE_MEAN = slice(2 * P, 2 * P + CELLS)
SUM = slice(2 * P + CELLS, 2 * P + CELLS + TENSOR_CELLS)
EXTREME = slice(0, 2 * P + CELLS + TENSOR_CELLS)


def over_sources(cell_values):
    return cell_values.unsqueeze(2).to_broadcast([P, cell_values.shape[1], NODES])


def tile_gnnlayer_pa_v_kernel(tc, x, e_enc, W_pre, b_pre, m, grad_out, out):
    nc = tc.nc
    m_rows = m.rearrange("b i j f -> (b i j) f")
    out_rows = out.rearrange("b i j c -> (b i j) c")
    grad_rows = grad_out.rearrange("b i k -> (b i) k")
    w_edge = W_pre[2 * FEATURES : 3 * FEATURES, :]
    cell_shape = [P, PLANES, BATCH_TARGETS]

    with ExitStack() as stack:
        keep = stack.enter_context(tc.tile_pool(name="keep", bufs=1))
        loads = stack.enter_context(tc.tile_pool(name="loads", bufs=2 * BATCH_TILES))
        stream = stack.enter_context(tc.tile_pool(name="stream", bufs=3))
        planes = stack.enter_context(tc.tile_pool(name="planes", bufs=5))
        three = stack.enter_context(tc.tile_pool(name="three", bufs=3))
        work = stack.enter_context(tc.tile_pool(name="work", bufs=2))
        squares = stack.enter_context(tc.tile_pool(name="squares", bufs=2))
        psum_turn = stack.enter_context(tc.psum_pool(name="psum_turn", bufs=3))
        psum_count = stack.enter_context(tc.psum_pool(name="psum_count", bufs=1))
        psum_stats = stack.enter_context(tc.psum_pool(name="psum_stats", bufs=2))
        psum_out = stack.enter_context(tc.psum_pool(name="psum_out", bufs=2))

        ident_f32 = keep.tile([P, P], F32)
        make_identity(nc, ident_f32[:])
        ident_bf16 = keep.tile([P, P], BF16)
        make_identity(nc, ident_bf16[:])

        def group_sums(group, name):
            ones = keep.tile([P, P // group], F32, name=name)
            nc.vector.tensor_reduce(
                out=ones[:], in_=ident_f32[:].rearrange("p (c q) -> p c q", q=group), axis=INNERMOST, op=ALU.add
            )
            return ones

        mean_of_halves = group_sums(HALVES, "mean_of_halves")
        nc.scalar.mul(out=mean_of_halves[:], in_=mean_of_halves[:], mul=1.0 / NODES)
        sum_of_quarters = group_sums(QUARTERS, "sum_of_quarters")

        grad_half = KINDS * FEATURES // 2
        grad_nat = keep.tile([P, grad_half], BF16)
        grad_t = keep.tile([P, KINDS, PLANES, TARGETS], F32)
        w_nat = keep.tile([P, CHANNELS // P, FEATURES], BF16)
        w_grouped = keep.tile([P, PASSES, CHANNELS, PACK], BF16, align_bytes=64)
        w_codes = keep.tile([P, PASSES, CHANNELS], U32, align_bytes=64)
        w_scales = keep.tile([P, PASSES, CHANNELS], U8, align_bytes=64)
        live = {}

        def targets_of(batch):
            return slice(batch * BATCH_TARGETS, (batch + 1) * BATCH_TARGETS)

        def load_grad():
            for side in range(2):
                nc.sync.dma_start(
                    out=grad_nat[side * TARGETS : (side + 1) * TARGETS, :],
                    in_=grad_rows[:, side * grad_half : (side + 1) * grad_half],
                )

        def prepare_grad(first):
            turned = psum_turn.tile([P, PLANES, P], BF16, name="turned", tag="turned_m")
            for plane in range(PLANES):
                col0 = (first * PLANES + plane) * P
                nc.tensor.transpose(turned[:, plane, :], grad_nat[:, col0 : col0 + P], ident_bf16[:])
            for side in range(2):
                kind = 2 * side + first
                nc.scalar.activation(
                    out=grad_t[:, kind],
                    in_=turned[:, :, side * TARGETS : (side + 1) * TARGETS],
                    func=FUNC.Copy,
                    scale=1.0 / NODES if kind in (KIND_MEAN, KIND_STD) else 1.0,
                )

        def load_weight(h):
            features = slice(h * K_PASS, (h + 1) * K_PASS)
            nc.sync.dma_start(out=w_nat[:, :, features], in_=w_edge[:, features].rearrange("(a p) f -> p a f", p=P))

        def turn_weight(h, tiles_a):
            for a in tiles_a:
                turned = psum_turn.tile([P, PACK, P], BF16, name="turned", tag="turned_m")
                for t in range(PACK):
                    col0 = (h * PACK + t) * P
                    nc.tensor.transpose(turned[:, t, :], w_nat[:, a, col0 : col0 + P], ident_bf16[:])
                nc.scalar.copy(
                    out=w_grouped[:, h, a * P : (a + 1) * P, :],
                    in_=turned[:].rearrange("p t c -> p c t"),
                )

        def quantise_weight(h):
            nc.vector.quantize_mx(
                out=w_codes[:, h, :].bitcast(E4M3_X4),
                scales=w_scales[:, h, :],
                in_=w_grouped[:, h].rearrange("p c t -> p (c t)"),
            )

        def load(batch):
            live[batch] = {}
            pieces = PASSES if batch == 0 else 1
            for a in range(BATCH_TILES):
                row0 = (batch * BATCH_TILES + a) * P
                rows = loads.tile([P, FEATURES], F32, name="m_nat")
                for piece in range(pieces):
                    cols = slice(piece * FEATURES // pieces, (piece + 1) * FEATURES // pieces)
                    nc.sync.dma_start(out=rows[:, cols], in_=m_rows[row0 : row0 + P, cols])
                live[batch]["m_nat", a] = rows

        def turn(batch, part):
            tiles = live[batch]
            a, h = divmod(part, PASSES)
            if part == 0:
                tiles["m_t"] = planes.tile([P, PLANES, BATCH_ROWS], F32, name="m_t")
            turned = psum_turn.tile([P, PACK, P], F32, name="turned_m")
            for t in range(PACK):
                col0 = (h * PACK + t) * P
                nc.tensor.transpose(turned[:, t, :], tiles["m_nat", a][:, col0 : col0 + P], ident_f32[:])
            nc.scalar.copy(out=tiles["m_t"][:, h * PACK : (h + 1) * PACK, a * P : (a + 1) * P], in_=turned[:])

        def square(batch, h):
            tiles = live[batch]
            if h == 0:
                tiles["m_sq"] = squares.tile([P, PLANES, BATCH_ROWS], F32, name="m_sq")
            of_pass = slice(h * PACK, (h + 1) * PACK)
            nc.scalar.activation(out=tiles["m_sq"][:, of_pass], in_=tiles["m_t"][:, of_pass], func=FUNC.Square)

        def add_up(out, columns):
            last_k = columns.shape[2] - 1
            for k in range(last_k + 1):
                nc.tensor.matmul(
                    out=out, lhsT=columns[:, :, k], rhs=ident_f32[:], is_transpose=True, start=(k == 0), stop=(k == last_k)
                )

        def parts_of_cells(values, parts):
            return values.rearrange("p c (q k) -> p (c q) k", k=NODES // parts)

        def extreme(batch, end):
            tiles = live[batch]
            if end == LOW:
                tiles["extreme"] = three.tile([P, 2, CELLS], F32, name="extreme")
            nc.vector.tensor_reduce(
                out=tiles["extreme"][:, end, :],
                in_=tiles["m_t"][:].rearrange("p c (g j) -> p (c g) j", j=NODES),
                axis=INNERMOST,
                op=ALU.min if end == LOW else ALU.max,
            )

        def total(batch):
            tiles = live[batch]
            tiles["total"] = three.tile(cell_shape, F32, name="total")
            if VECTOR_PLANES == 0:
                return
            nc.vector.tensor_reduce(
                out=tiles["total"][:, 0:VECTOR_PLANES].rearrange("p c g -> p (c g)"),
                in_=tiles["m_t"][:, 0:VECTOR_PLANES].rearrange("p c (g j) -> p (c g) j", j=NODES),
                axis=INNERMOST,
                op=ALU.add,
            )

        def show_extremes(batch):
            tiles = live[batch]
            tiles["stats"] = psum_stats.tile([P, EXTREME.stop], F32, name="stats")

        def stats_sum(batch):
            tiles = live[batch]
            add_up(tiles["stats"][:, SQUARE_NAT], parts_of_cells(tiles["m_sq"][:], HALVES))
            add_up(tiles["stats"][:, SUM_NAT], parts_of_cells(tiles["m_t"][:, VECTOR_PLANES:PLANES], QUARTERS))

        def stats_copy(batch):
            tiles = live[batch]
            tiles["stats_nat"] = work.tile([P, 2 * P], F32, name="stats_nat")
            nc.scalar.copy(out=tiles["stats_nat"][:], in_=tiles["stats"][:, 0 : 2 * P])

        def stats_back(batch):
            tiles = live[batch]
            for columns, nat, groups in ((SQUARE_MEAN, SQUARE_NAT, mean_of_halves), (SUM, SUM_NAT, sum_of_quarters)):
                nc.tensor.matmul(
                    out=tiles["stats"][:, columns], lhsT=tiles["stats_nat"][:, nat], rhs=groups[:], start=True, stop=True
                )

        def mean_squared(batch):
            tiles = live[batch]
            nc.scalar.copy(
                out=tiles["total"][:, VECTOR_PLANES:PLANES].rearrange("p c g -> p (c g)"), in_=tiles["stats"][:, SUM]
            )
            tiles["mean_sq"] = work.tile([P, CELLS], F32, name="mean_sq")
            nc.scalar.activation(
                out=tiles["mean_sq"][:], in_=tiles["total"][:].rearrange("p c g -> p (c g)"), func=FUNC.Square, scale=1.0 / NODES
            )

        def variance(batch):
            tiles = live[batch]
            tiles["var"] = work.tile(cell_shape, F32, name="var")
            nc.vector.tensor_tensor(
                out=tiles["var"][:].rearrange("p c g -> p (c g)"),
                in0=tiles["stats"][:, SQUARE_MEAN],
                in1=tiles["mean_sq"][:],
                op=ALU.subtract,
            )

        def inverse_std(batch):
            tiles = live[batch]
            tiles["std"] = work.tile(cell_shape, F32, name="std")
            nc.scalar.activation(out=tiles["std"][:], in_=tiles["var"][:], func=FUNC.Relu)
            nc.scalar.activation(out=tiles["std"][:], in_=tiles["std"][:], func=FUNC.Abs_reciprocal_sqrt, bias=EPS_STD)

        def masked_grad(batch):
            tiles = live[batch]
            tiles["slope"] = three.tile(cell_shape, F32, name="slope")
            nc.vector.scalar_tensor_tensor(
                out=tiles["slope"][:], in0=tiles["var"][:], scalar=0.0, in1=grad_t[:, KIND_STD, :, targets_of(batch)],
                op0=ALU.is_gt, op1=ALU.mult,
            )

        def slope(batch):
            tiles = live[batch]
            nc.vector.tensor_tensor(out=tiles["slope"][:], in0=tiles["slope"][:], in1=tiles["std"][:], op=ALU.mult)

        def slope_mean(batch):
            tiles = live[batch]
            tiles["offset"] = work.tile(cell_shape, F32, name="offset")
            nc.vector.scalar_tensor_tensor(
                out=tiles["offset"][:], in0=tiles["total"][:], scalar=1.0 / NODES, in1=tiles["slope"][:],
                op0=ALU.mult, op1=ALU.mult,
            )

        def offset(batch):
            tiles = live[batch]
            nc.vector.tensor_tensor(
                out=tiles["offset"][:], in0=grad_t[:, KIND_MEAN, :, targets_of(batch)], in1=tiles["offset"][:],
                op=ALU.subtract,
            )

        def compare(batch):
            tiles = live[batch]
            both_shape = [P, 2, CELLS, NODES]
            tiles["at_extreme"] = three.tile(both_shape, F32, name="at_extreme")
            nc.vector.tensor_tensor(
                out=tiles["at_extreme"][:],
                in0=tiles["m_t"][:].rearrange("p c (g j) -> p (c g) j", j=NODES).unsqueeze(1).to_broadcast(both_shape),
                in1=tiles["extreme"][:].unsqueeze(3).to_broadcast(both_shape),
                op=ALU.is_equal,
            )

        def count(batch):
            tiles = live[batch]
            tiles["counts"] = psum_count.tile([P, 2, 2 * CELLS], F32, name="counts")
            add_up(tiles["counts"][:, 0, :], tiles["at_extreme"][:].rearrange("p s x j -> p (s x) j"))

        def count_copy(batch):
            tiles = live[batch]
            tiles["counts_nat"] = work.tile([P, P], F32, name="counts_nat")
            nc.scalar.copy(out=tiles["counts_nat"][:], in_=tiles["counts"][:, 0, :])

        def count_back(batch):
            tiles = live[batch]
            nc.tensor.transpose(tiles["counts"][:, 1, :], tiles["counts_nat"][:], ident_f32[:])

        def invert_counts(batch):
            tiles = live[batch]
            tiles["amplitude"] = work.tile([P, 2, PLANES, BATCH_TARGETS], F32, name="amplitude")
            nc.vector.reciprocal(
                out=tiles["amplitude"][:].rearrange("p s c g -> p (s c g)"), in_=tiles["counts"][:, 1, :]
            )

        def quantise_last_weight(batch):
            if batch == 0:
                quantise_weight(0)
                quantise_weight(1)

        def divide(batch, cells):
            planes_of_cells = slice(cells.start // BATCH_TARGETS, cells.stop // BATCH_TARGETS)
            amplitude = live[batch]["amplitude"][:].rearrange("p s c g -> p (s c) g")[:, planes_of_cells]
            grads = grad_t[:, KIND_MIN : KIND_MAX + 1, :, targets_of(batch)].rearrange("p s c g -> p (s c) g")
            nc.vector.tensor_tensor(out=amplitude, in0=grads[:, planes_of_cells], in1=amplitude, op=ALU.mult)

        def divide_first(batch):
            divide(batch, slice(gpsimd_cells(batch), 2 * CELLS))

        def divide_last(batch):
            if gpsimd_cells(batch) > 0:
                divide(batch, slice(0, gpsimd_cells(batch)))

        def linear_part(batch, plane):
            tiles = live[batch]
            if plane == 0:
                tiles["linear"] = work.tile([P, PLANES, BATCH_ROWS], F32, name="linear")
            for g in range(BATCH_TARGETS):
                sources = slice(g * NODES, (g + 1) * NODES)
                nc.scalar.activation(
                    out=tiles["linear"][:, plane, sources],
                    in_=tiles["m_t"][:, plane, sources],
                    func=FUNC.Identity,
                    scale=tiles["slope"][:, plane, g : g + 1],
                    bias=tiles["offset"][:, plane, g : g + 1],
                )

        def spikes(engine, batch, cells):
            tiles = live[batch]
            at_cells = tiles["at_extreme"][:].rearrange("p s x j -> p (s x) j")[:, cells]
            amplitude = tiles["amplitude"][:].rearrange("p s c g -> p (s c g)")[:, cells]
            engine.tensor_tensor(out=at_cells, in0=at_cells, in1=over_sources(amplitude), op=ALU.mult)

        def gpsimd_cells(batch):
            return GPSIMD_LOW if batch < BATCHES - VECTOR_TAIL else 0

        def gpsimd_spikes(batch):
            if gpsimd_cells(batch) > 0:
                spikes(nc.gpsimd, batch, slice(0, gpsimd_cells(batch)))

        def vector_spikes(batch):
            spikes(nc.vector, batch, slice(gpsimd_cells(batch), 2 * CELLS))

        def by_plane(batch, end):
            return live[batch]["at_extreme"][:, end].rearrange("p (c g) j -> p c (g j)", c=PLANES)

        def add_linear(engine, batch, h):
            of_pass = slice(h * PACK, (h + 1) * PACK)
            low = by_plane(batch, LOW)[:, of_pass, :]
            engine.tensor_tensor(out=low, in0=low, in1=live[batch]["linear"][:, of_pass, :], op=ALU.add)

        def gpsimd_linear(batch):
            if batch < BATCHES - ADD_TAIL:
                for h in range(PASSES):
                    add_linear(nc.gpsimd, batch, h)

        def vector_linear(batch):
            if batch >= BATCHES - ADD_TAIL:
                for h in range(PASSES):
                    add_linear(nc.vector, batch, h)

        def add_high(batch, rows):
            nc.vector.tensor_tensor(
                out=live[batch]["dm_grouped"][:, :, rows],
                in0=by_plane(batch, LOW)[:, :, rows].rearrange("p (h t) r -> p h r t", t=PACK),
                in1=by_plane(batch, HIGH)[:, :, rows].rearrange("p (h t) r -> p h r t", t=PACK),
                op=ALU.add,
            )

        def assemble(batch):
            tiles = live[batch]
            tiles["dm_grouped"] = work.tile([P, PASSES, BATCH_ROWS, PACK], BF16, name="dm_grouped", align_bytes=64)
            tiles["dm_codes"] = work.tile([P, PASSES, BATCH_ROWS], U32, name="dm_codes", align_bytes=64)
            tiles["dm_scales"] = work.tile([P, PASSES, BATCH_ROWS], U8, name="dm_scales", align_bytes=64)
            if batch < BATCHES - 1:
                add_high(batch, slice(0, BATCH_ROWS))

        def quantise(batch):
            tiles = live[batch]
            if batch < BATCHES - 1:
                nc.vector.quantize_mx(
                    out=tiles["dm_codes"][:].rearrange("p h r -> p (h r)").bitcast(E5M2_X4),
                    scales=tiles["dm_scales"][:].rearrange("p h r -> p (h r)"),
                    in_=tiles["dm_grouped"][:].rearrange("p h r t -> p (h r t)"),
                )
            else:
                for a in range(BATCH_TILES):
                    rows = slice(a * P, (a + 1) * P)
                    add_high(batch, rows)
                    for h in range(PASSES):
                        nc.vector.quantize_mx(
                            out=tiles["dm_codes"][:, h, rows].bitcast(E5M2_X4),
                            scales=tiles["dm_scales"][:, h, rows],
                            in_=tiles["dm_grouped"][:, h, rows].rearrange("p r t -> p (r t)"),
                        )

        def product(batch, part):
            tiles = live[batch]
            a, n = divmod(part, CHANNELS // N_TILE)
            rows = slice(a * P, (a + 1) * P)
            cols = slice(n * N_TILE, (n + 1) * N_TILE)
            if n == 0:
                tiles["result"] = stream.tile([P, CHANNELS], F32, name="result")
            acc = psum_out.tile([P, N_TILE], F32, name="acc")
            for h in range(PASSES):
                nc.tensor.matmul_mx(
                    out=acc[:],
                    lhsT=tiles["dm_codes"][:, h, rows].bitcast(E5M2_X4),
                    lhsT_scale=tiles["dm_scales"][:, h, rows],
                    rhs=w_codes[:, h, cols].bitcast(E4M3_X4),
                    rhs_scale=w_scales[:, h, cols],
                    start=(h == 0),
                    stop=(h == PASSES - 1),
                )
            nc.scalar.copy(out=tiles["result"][:, cols], in_=acc[:])
            row0 = (batch * BATCH_TILES + a) * P
            if batch == BATCHES - 1:
                nc.sync.dma_start(out=out_rows[row0 : row0 + P, cols], in_=tiles["result"][:, cols])
            elif cols.stop == CHANNELS:
                nc.sync.dma_start(out=out_rows[row0 : row0 + P, :], in_=tiles["result"][:])

        load(0)
        load(1)
        load_grad()
        for h in range(PASSES):
            load_weight(h)

        def run(stages):
            for batch, stage, argument in stages:
                if 0 <= batch < BATCHES:
                    if argument is None:
                        stage(batch)
                    else:
                        stage(batch, argument)

        for step in range(-4, 0):
            mid, first, new, next_new = step + 1, step + 2, step + 3, step + 4
            run((
                (mid, count_back, None), (first, stats_back, None), (first, mean_squared, None),
                (next_new, turn, 0), (next_new, turn, 1), (next_new, turn, 2), (next_new, turn, 3), (next_new + 2, load, None),
                (new, extreme, LOW), (mid, slope, None), (new, extreme, HIGH), (mid, slope_mean, None), (new, total, None), (mid, offset, None),
                (new, show_extremes, None), (new, stats_sum, None),
                (first, compare, None), (mid, invert_counts, None), (first, variance, None), (first, inverse_std, None),
                (next_new, square, 0), (next_new, square, 1), (new, stats_copy, None), (first, count, None), (first, count_copy, None),
            ))
            if step == -3:
                prepare_grad(0)
                prepare_grad(1)
            run([(mid, linear_part, plane) for plane in range(PLANES)])
            if step == -1:
                turn_weight(0, range(CHANNELS // P))
            run(((mid, divide_first, None), (first, masked_grad, None), (mid, vector_spikes, None), (mid, divide_last, None)))
        for step in range(BATCHES + 1):
            last, mid, first, new, next_new = step, step + 1, step + 2, step + 3, step + 4
            run((
                (mid, count_back, None), (first, stats_back, None), (first, mean_squared, None),
                (next_new, turn, 0), (next_new, turn, 1), (next_new, turn, 2), (next_new, turn, 3), (next_new + 2, load, None),
            ))
            if step == 0:
                turn_weight(1, range(CHANNELS // P))
            run((
                (new, extreme, LOW), (mid, slope, None), (new, extreme, HIGH), (mid, slope_mean, None), (new, total, None), (mid, offset, None),
                (last, gpsimd_spikes, None), (last, gpsimd_linear, None),
                (last - 1, product, 0), (next_new, square, 0), (last - 1, product, 1), (next_new, square, 1),
                (last - 1, product, 2), (mid, linear_part, 0), (new, show_extremes, None), (last - 1, product, 3),
                (new, stats_sum, None),
                (mid, linear_part, 1), (mid, linear_part, 2), (mid, linear_part, 3), (mid, linear_part, 4),
                (first, compare, None), (mid, invert_counts, None), (last, vector_linear, None), (first, variance, None), (first, count, None), (first, inverse_std, None),
                (mid, linear_part, 5), (mid, linear_part, 6), (mid, linear_part, 7),
                (new, stats_copy, None),
                (last, assemble, None), (mid, divide_first, None), (last, quantise, None), (last, quantise_last_weight, None),
                (first, masked_grad, None), (mid, vector_spikes, None), (mid, divide_last, None),
            ))
            run(((first, count_copy, None),))
